import numpy as np
import ml_dtypes


def mxq(x, axis, fmt="e4m3"):
    dtype, down = {"e4m3": (ml_dtypes.float8_e4m3fn, 7), "e5m2": (ml_dtypes.float8_e5m2, 14)}[fmt]
    v = np.moveaxis(np.asarray(x, np.float32).astype(ml_dtypes.bfloat16).astype(np.float64), axis, -1)
    blocks = v.reshape(v.shape[:-1] + (-1, 32))
    amax = np.abs(blocks).max(-1, keepdims=True)
    byte = np.maximum(np.where(amax > 0, np.frexp(amax)[1] - 1 + 127, 0) - down, 1)
    scale = np.exp2(byte - 127.0)
    codes = (blocks / scale).astype(np.float32).astype(dtype).astype(np.float64)
    return np.moveaxis((codes * scale).reshape(v.shape), -1, axis)


WIDE = False


def mx_kscale(k):
    if not WIDE:
        return np.ones(k)
    levels = np.array([10, -10, 5, -5, 0])
    a = np.random.permutation(np.resize(levels, k // 512 * 4)).reshape(k // 512, 4)
    idx = np.arange(k)
    return np.exp2(a[idx // 512, idx % 128 // 32])


BF16 = ml_dtypes.bfloat16


def bf(x):
    return np.asarray(x, np.float32).astype(BF16)


def f64(x):
    return np.asarray(x).astype(np.float64)


B, N, C_IN, C_OUT, H = 1, 1024, 512, 1024, 8
DH = C_OUT // H
LN_EPS = 1e-5


def setup_inputs():
    s = mx_kscale(C_IN)
    bound = 1.0 / np.sqrt(C_IN)
    return {
        "x": bf(np.random.standard_normal((B, N, C_IN)) * s),
        "q": bf(np.random.standard_normal((B, H, N, DH)) * 1.4),
        "k": bf(np.random.standard_normal((B, H, N, DH)) * 1.4),
        "W_v": bf(np.random.standard_normal((H, C_IN, DH)) * 2.0 * bound / s[None, :, None]),
        "conv_w": bf(np.random.uniform(-bound, bound, (C_OUT, C_IN)) / s[None, :]),
        "conv_b": bf(np.random.standard_normal(C_OUT) * 0.3),
        "ln_w": bf(1.0 + 0.1 * np.random.standard_normal(C_OUT)),
        "ln_b": bf(0.1 * np.random.standard_normal(C_OUT)),
    }


def reference(x, q, k, W_v, conv_w, conv_b, ln_w, ln_b):
    xq = mxq(f64(x), 2, "e4m3")
    v = xq[:, None] @ mxq(f64(W_v), 1, "e4m3")[None]
    s = f64(q) @ f64(k).transpose(0, 1, 3, 2) * (1.0 / np.sqrt(DH))
    e = np.exp(s - s.max(-1, keepdims=True))
    o = np.maximum((mxq(e, 3, "e4m3") @ mxq(v, 2, "e4m3")) / e.sum(-1, keepdims=True), 0.0)
    o = o.transpose(0, 2, 1, 3).reshape(B, N, C_OUT)
    proj = (xq @ mxq(f64(conv_w), 1, "e4m3").T) + f64(conv_b)
    y = o + proj
    mean = y.mean(-1, keepdims=True)
    var = y.var(-1, keepdims=True)
    return (y - mean) / np.sqrt(var + LN_EPS) * f64(ln_w) + f64(ln_b)

@@ -1,0 +1,438 @@
+from contextlib import ExitStack
+import math
+
+import concourse.mybir as mybir
+from concourse.masks import make_identity
+
+F32 = mybir.dt.float32
+BF16 = mybir.dt.bfloat16
+U32 = mybir.dt.uint32
+U8 = mybir.dt.uint8
+FP8X4 = mybir.dt.float8_e4m3fn_x4
+ALU = mybir.AluOpType
+ACT = mybir.ActivationFunctionType
+
+P = 128
+NODES = 1024
+C_IN = 512
+C_OUT = 1024
+HEADS = 8
+DH = 128
+PACK = 4
+BANK = 512
+TILES = NODES // P
+PAIRS = TILES // 2
+PASSES = NODES // (P * PACK)
+HALVES = C_OUT // BANK
+HALF_HEADS = BANK // DH
+UNITS = TILES * HEADS
+SCALE = 1.0 / math.sqrt(DH)
+LN_EPS = 1e-5
+
+CLOSING_LAG = 9
+
+FLOPS = 2 * NODES * C_IN * C_OUT * 2 + 2 * HEADS * NODES * NODES * DH * 2
+
+
+def tile_transformergraphconv_pa_kernel(tc, x, q, k, W_v, conv_w, conv_b, ln_w, ln_b, out):
+    nc = tc.nc
+    with ExitStack() as ctx:
+        ctx.enter_context(tc.manual_schedule())
+        keep = ctx.enter_context(tc.tile_pool(name="keep", bufs=1))
+        stage = ctx.enter_context(tc.tile_pool(name="stage", bufs=2))
+        work = ctx.enter_context(tc.tile_pool(name="work", bufs=3))
+        small = ctx.enter_context(tc.tile_pool(name="small", bufs=4))
+        psum_s = ctx.enter_context(tc.psum_pool(name="psum_s", bufs=4))
+        psum_t = ctx.enter_context(tc.psum_pool(name="psum_t", bufs=2))
+        psum_o = ctx.enter_context(tc.psum_pool(name="psum_o", bufs=2))
+
+        ident_f32 = keep.tile([P, P], F32)
+        make_identity(nc, ident_f32[:])
+        ident_bf = keep.tile([P, P], BF16)
+        make_identity(nc, ident_bf[:])
+        minus_half = keep.tile([P, 1], F32)
+        nc.gpsimd.memset(minus_half[:], -0.5)
+
+        x_sb = keep.tile([P, PAIRS, 2, C_IN], BF16)
+        x_rows = x.rearrange("b (a p e) c -> (b a) p (e c)", p=P, e=2)
+        wv_sb = keep.tile([P, HEADS, PACK, DH], BF16)
+        wv_rows = W_v.rearrange("h (u p e) d -> u p h (e d)", u=2, e=2)
+        cw_sb = keep.tile([P, TILES, C_IN], BF16)
+        cw_rows = conv_w.rearrange("(j p) c -> p j c", p=P)
+        k_sb = keep.tile([P, HEADS, TILES, DH], BF16)
+        k_rows = k.rearrange("b h (j p) d -> (b h) p j d", p=P)
+        q_sb = keep.tile([P, HEADS, PAIRS, 2, DH], BF16)
+        q_rows = q.rearrange("b h (a p e) d -> a p (b h) (e d)", p=P, e=2)
+        conv_b_all = keep.tile([P, C_OUT], BF16)
+        ln_w_all = keep.tile([P, C_OUT], BF16)
+        ln_b_all = keep.tile([P, C_OUT], BF16)
+
+        for a in range(PAIRS):
+            nc.sync.dma_start(out=x_sb[:, a, :, :].rearrange("p e c -> p (e c)"), in_=x_rows[a, :, :])
+        for half in range(2):
+            heads = slice(HALF_HEADS * half, HALF_HEADS * half + HALF_HEADS)
+            for u in range(2):
+                nc.sync.dma_start(
+                    out=wv_sb[:, heads, 2 * u : 2 * u + 2, :].rearrange("p h e d -> p h (e d)"),
+                    in_=wv_rows[u, :, heads, :],
+                )
+        for half in range(2):
+            rows = slice(PACK * half, PACK * half + PACK)
+            nc.sync.dma_start(out=cw_sb[:, rows, :], in_=cw_rows[:, rows, :])
+        nc.sync.dma_start(out=conv_b_all[:], in_=conv_b.partition_broadcast(P))
+        for h in range(HEADS):
+            nc.sync.dma_start(out=k_sb[:, h, :, :], in_=k_rows[h, :, :, :])
+        for a in range(PAIRS):
+            nc.sync.dma_start(
+                out=q_sb[:, :, a, :, :].rearrange("p h e d -> p h (e d)"), in_=q_rows[a, :, :, :]
+            )
+        nc.sync.dma_start(out=ln_w_all[:], in_=ln_w.partition_broadcast(P))
+        nc.sync.dma_start(out=ln_b_all[:], in_=ln_b.partition_broadcast(P))
+
+        def quantise_channels_last(rows_sb, codes, scales):
+            words = rows_sb.bitcast(F32)
+            for half in range(2):
+                grouped = stage.tile([P, PACK, P, PACK], BF16, tag="grouped", align_bytes=64)
+                grouped_words = grouped[:].bitcast(F32)
+                for pair in range(2):
+                    flipped = psum_t.tile([P, 2, 2, P], F32, tag="flip")
+                    for i in range(2):
+                        for u in range(2):
+                            nc.tensor.transpose(
+                                flipped[:, i, u, :],
+                                words[:, PACK * half + 2 * pair + i, P * u : P * u + P],
+                                ident_f32[:],
+                            )
+                    nc.scalar.copy(
+                        out=grouped_words[:, 2 * pair : 2 * pair + 2, :, :],
+                        in_=flipped[:].rearrange("p i u r -> p i r u"),
+                    )
+                cols = slice(BANK * half, BANK * half + BANK)
+                nc.vector.quantize_mx(
+                    out=codes[:, cols].bitcast(FP8X4),
+                    scales=scales[:, cols],
+                    in_=grouped[:].rearrange("p j r t -> p (j r t)"),
+                )
+
+        x_codes = keep.tile([P, NODES], U32, align_bytes=64)
+        x_scales = keep.tile([P, NODES], U8, align_bytes=64)
+        quantise_channels_last(x_sb[:].rearrange("p a e c -> p (a e) c"), x_codes[:], x_scales[:])
+
+        wv_codes = keep.tile([P, HEADS * DH], U32, align_bytes=64)
+        wv_scales = keep.tile([P, HEADS * DH], U8, align_bytes=64)
+        for half in range(2):
+            heads = slice(HALF_HEADS * half, HALF_HEADS * half + HALF_HEADS)
+            cols = slice(BANK * half, BANK * half + BANK)
+            wv_grouped = stage.tile([P, HALF_HEADS, DH, PACK], BF16, tag="grouped", align_bytes=64)
+            nc.vector.tensor_copy(out=wv_grouped[:], in_=wv_sb[:, heads, :, :].rearrange("p h t d -> p h d t"))
+            nc.vector.quantize_mx(
+                out=wv_codes[:, cols].bitcast(FP8X4),
+                scales=wv_scales[:, cols],
+                in_=wv_grouped[:].rearrange("p h d t -> p (h d t)"),
+            )
+
+        cw_codes = keep.tile([P, C_OUT], U32, align_bytes=64)
+        cw_scales = keep.tile([P, C_OUT], U8, align_bytes=64)
+        quantise_channels_last(cw_sb[:], cw_codes[:], cw_scales[:])
+
+        kT = keep.tile([P, HEADS, NODES], BF16)
+        v_codes = keep.tile([P, HEADS, PASSES, DH], U32, align_bytes=64)
+        v_scales = keep.tile([P, HEADS, PASSES, DH], U8, align_bytes=64)
+        y_all = keep.tile([P, TILES, C_OUT], F32)
+        for n in range(HEADS):
+            v_grouped = stage.tile([P, PASSES, DH, PACK], BF16, tag="v_grouped", align_bytes=64)
+            for g in range(PASSES):
+                v_bank = psum_s.tile([P, PACK, DH], F32, tag="s")
+                for t in range(PACK):
+                    nodes = slice(P * (PACK * g + t), P * (PACK * g + t) + P)
+                    nc.tensor.matmul_mx(
+                        out=v_bank[:, t, :],
+                        lhsT=x_codes[:, nodes].bitcast(FP8X4),
+                        lhsT_scale=x_scales[:, nodes],
+                        rhs=wv_codes[:, DH * n : DH * n + DH].bitcast(FP8X4),
+                        rhs_scale=wv_scales[:, DH * n : DH * n + DH],
+                        start=True,
+                        stop=True,
+                    )
+                nc.scalar.copy(out=v_grouped[:, g, :, :], in_=v_bank[:].rearrange("p t d -> p d t"))
+
+            nodes = slice(P * n, P * n + P)
+            for half in range(HALVES):
+                cols = slice(BANK * half, BANK * half + BANK)
+                proj_bank = psum_s.tile([P, BANK], F32, tag="s")
+                nc.tensor.matmul_mx(
+                    out=proj_bank[:],
+                    lhsT=x_codes[:, nodes].bitcast(FP8X4),
+                    lhsT_scale=x_scales[:, nodes],
+                    rhs=cw_codes[:, cols].bitcast(FP8X4),
+                    rhs_scale=cw_scales[:, cols],
+                    start=True,
+                    stop=True,
+                )
+                nc.vector.tensor_tensor(out=y_all[:, n, cols], in0=proj_bank[:], in1=conv_b_all[:, cols], op=ALU.add)
+
+            nc.vector.quantize_mx(
+                out=v_codes[:, n, :, :].rearrange("p g d -> p (g d)").bitcast(FP8X4),
+                scales=v_scales[:, n, :, :].rearrange("p g d -> p (g d)"),
+                in_=v_grouped[:].rearrange("p g d t -> p (g d t)"),
+            )
+
+            k_flipped = psum_t.tile([P, TILES, P], BF16, tag="flip")
+            for j in range(TILES):
+                nc.tensor.transpose(k_flipped[:, j, :], k_sb[:, n, j, :], ident_bf[:])
+            nc.scalar.copy(out=kT[:, n, :], in_=k_flipped[:].rearrange("d j p -> d (j p)"))
+
+        q_flipped = {}
+        qT = {}
+        s_banks = {}
+        s_rows = {}
+        bank_maxima = {}
+        shift = {}
+        row_sums = {}
+        inverse_sums = {}
+        e_rows = {}
+        e_flipped = {}
+        e_grouped = {}
+        e_packed = {}
+        o_banks = {}
+
+        def transpose_q(tile_no):
+            flipped = psum_t.tile([P, HEADS, P], BF16, tag="flip")
+            for h in range(HEADS):
+                nc.tensor.transpose(flipped[:, h, :], q_sb[:, h, tile_no // 2, tile_no % 2, :], ident_bf[:])
+            q_flipped[tile_no] = flipped
+
+        def copy_q(tile_no):
+            q_cols = work.tile([P, HEADS, P], BF16, tag="qT", bufs=2)
+            nc.scalar.copy(out=q_cols[:], in_=q_flipped[tile_no][:])
+            qT[tile_no] = q_cols
+
+        def scores(unit):
+            tile_no, h = divmod(unit, HEADS)
+            banks = []
+            for g in range(PASSES):
+                s_bank = psum_s.tile([P, BANK], F32, tag="s")
+                nc.tensor.matmul(
+                    out=s_bank[:],
+                    lhsT=qT[tile_no][:, h, :],
+                    rhs=kT[:, h, BANK * g : BANK * g + BANK],
+                    start=True,
+                    stop=True,
+                )
+                banks.append(s_bank)
+            s_banks[unit] = banks
+
+        def scale_and_max(unit):
+            scaled = work.tile([P, NODES], F32, tag="scaled")
+            bank_max = small.tile([P, PASSES], F32, tag="bank_max")
+            for g in range(PASSES):
+                nc.vector.tensor_scalar(
+                    out=scaled[:, BANK * g : BANK * g + BANK],
+                    in0=s_banks[unit][g][:],
+                    scalar1=SCALE,
+                    scalar2=None,
+                    op0=ALU.mult,
+                    op1=ALU.max,
+                    accum_out=bank_max[:, g : g + 1],
+                )
+            s_rows[unit] = scaled
+            bank_maxima[unit] = bank_max
+
+        def row_max(unit):
+            minus_max = small.tile([P, 1], F32, tag="shift")
+            nc.vector.tensor_scalar(
+                out=minus_max[:],
+                in0=bank_maxima[unit][:, 0:1],
+                scalar1=bank_maxima[unit][:, 1:2],
+                scalar2=-1.0,
+                op0=ALU.max,
+                op1=ALU.mult,
+            )
+            shift[unit] = minus_max
+
+        def exponentials(unit):
+            tile_no, h = divmod(unit, HEADS)
+            if h == 0:
+                sums = small.tile([P, HEADS], F32, tag="row_sums", bufs=3)
+                row_sums[tile_no] = sums
+            e_sb = work.tile([P, NODES], BF16, tag="e_sb")
+            nc.scalar.activation(
+                out=e_sb[:],
+                in_=s_rows[unit][:],
+                func=ACT.Exp,
+                bias=shift[unit][:, 0:1],
+                scale=1.0,
+                accum_out=row_sums[tile_no][:, h : h + 1],
+            )
+            e_rows[unit] = e_sb
+
+        def flip(unit):
+            e_words = e_rows[unit][:].bitcast(F32)
+            flipped = psum_t.tile([P, PASSES, 2, P], F32, tag="flip")
+            for g in range(PASSES):
+                for u in range(2):
+                    first = P * (2 * g + u)
+                    nc.tensor.transpose(flipped[:, g, u, :], e_words[:, first : first + P], ident_f32[:])
+            e_flipped[unit] = flipped
+
+        def regroup(unit):
+            grouped = work.tile([P, PASSES, P, PACK], BF16, tag="e_grouped", align_bytes=64)
+            nc.scalar.copy(out=grouped[:].bitcast(F32), in_=e_flipped[unit][:].rearrange("p g u r -> p g r u"))
+            e_grouped[unit] = grouped
+
+        def quantise(unit):
+            e_codes = work.tile([P, PASSES, P], U32, tag="e_codes", align_bytes=64)
+            e_scales = work.tile([P, PASSES, P], U8, tag="e_scales", align_bytes=64)
+            nc.vector.quantize_mx(
+                out=e_codes[:].rearrange("p g r -> p (g r)").bitcast(FP8X4),
+                scales=e_scales[:].rearrange("p g r -> p (g r)"),
+                in_=e_grouped[unit][:].rearrange("p g r t -> p (g r t)"),
+            )
+            e_packed[unit] = (e_codes, e_scales)
+
+        def attend(unit):
+            tile_no, h = divmod(unit, HEADS)
+            half, place = divmod(h, HALF_HEADS)
+            if place == 0:
+                o_bank = psum_o.tile([P, HALF_HEADS, DH], F32, tag="o")
+                o_banks[(tile_no, half)] = o_bank
+            e_codes, e_scales = e_packed[unit]
+            for g in range(PASSES):
+                nc.tensor.matmul_mx(
+                    out=o_banks[(tile_no, half)][:, place, :],
+                    lhsT=e_codes[:, g, :].bitcast(FP8X4),
+                    lhsT_scale=e_scales[:, g, :],
+                    rhs=v_codes[:, h, g, :].bitcast(FP8X4),
+                    rhs_scale=v_scales[:, h, g, :],
+                    start=(g == 0),
+                    stop=(g == PASSES - 1),
+                )
+
+        attended = {}
+        y_sums = {}
+        minus_mean = {}
+        rstd = {}
+        centred = {}
+        out_rows = out.rearrange("b (a p e) c -> (b a) e p c", p=P, e=2)
+
+        def invert_row_sums(tile_no):
+            inverse = small.tile([P, HEADS], F32, tag="inverse")
+            nc.vector.reciprocal(out=inverse[:], in_=row_sums[tile_no][:])
+            inverse_sums[tile_no] = inverse
+
+        def closing_piece(tile_no, step, half):
+            cols = slice(BANK * half, BANK * half + BANK)
+            y = y_all[:, tile_no, :]
+            if step == 0:
+                heads = slice(HALF_HEADS * half, HALF_HEADS * half + HALF_HEADS)
+                relu_o = work.tile([P, HALF_HEADS, DH], F32, tag="attended")
+                nc.vector.scalar_tensor_tensor(
+                    out=relu_o[:],
+                    in0=o_banks[(tile_no, half)][:],
+                    scalar=0.0,
+                    in1=inverse_sums[tile_no][:, heads].unsqueeze(2).to_broadcast([P, HALF_HEADS, DH]),
+                    op0=ALU.max,
+                    op1=ALU.mult,
+                )
+                attended[(tile_no, half)] = relu_o
+            elif step == 1:
+                if half == 0:
+                    sums = small.tile([P, HALVES], F32, tag="y_sums")
+                    y_sums[tile_no] = sums
+                nc.vector.scalar_tensor_tensor(
+                    out=y[:, cols],
+                    in0=attended[(tile_no, half)][:].rearrange("p h d -> p (h d)"),
+                    scalar=0.0,
+                    in1=y[:, cols],
+                    op0=ALU.add,
+                    op1=ALU.add,
+                    accum_out=y_sums[tile_no][:, half : half + 1],
+                )
+                if half == HALVES - 1:
+                    mean(tile_no)
+            elif step == 2:
+                if half == 0:
+                    deviation(tile_no)
+                    scaled = work.tile([P, C_OUT], F32, tag="centred", bufs=2)
+                    centred[tile_no] = scaled
+                nc.vector.scalar_tensor_tensor(
+                    out=centred[tile_no][:, cols],
+                    in0=y[:, cols],
+                    scalar=minus_mean[tile_no][:, 0:1],
+                    in1=ln_w_all[:, cols],
+                    op0=ALU.add,
+                    op1=ALU.mult,
+                )
+            else:
+                result = work.tile([P, BANK], F32, tag="result")
+                nc.vector.scalar_tensor_tensor(
+                    out=result[:],
+                    in0=centred[tile_no][:, cols],
+                    scalar=rstd[tile_no][:, 0:1],
+                    in1=ln_b_all[:, cols],
+                    op0=ALU.mult,
+                    op1=ALU.add,
+                )
+                nc.sync.dma_start(out=out_rows[tile_no // 2, tile_no % 2, :, cols], in_=result[:])
+
+        def mean(tile_no):
+            negative = small.tile([P, 1], F32, tag="minus_mean")
+            nc.vector.tensor_scalar(
+                out=negative[:],
+                in0=y_sums[tile_no][:, 0:1],
+                scalar1=y_sums[tile_no][:, 1:2],
+                scalar2=-1.0 / C_OUT,
+                op0=ALU.add,
+                op1=ALU.mult,
+            )
+            minus_mean[tile_no] = negative
+
+        def deviation(tile_no):
+            squares = work.tile([P, C_OUT], BF16, tag="squares", bufs=2)
+            square_sum = small.tile([P, 1], F32, tag="square_sum")
+            nc.scalar.activation(
+                out=squares[:],
+                in_=y_all[:, tile_no, :],
+                func=ACT.Square,
+                bias=minus_mean[tile_no][:, 0:1],
+                scale=1.0,
+                accum_out=square_sum[:, 0:1],
+            )
+            var_eps = small.tile([P, 1], F32, tag="var_eps")
+            nc.gpsimd.tensor_scalar(
+                out=var_eps[:], in0=square_sum[:], scalar1=1.0 / C_OUT, scalar2=LN_EPS, op0=ALU.mult, op1=ALU.add
+            )
+            inverse_std = small.tile([P, 1], F32, tag="rstd")
+            nc.gpsimd.tensor_tensor(out=inverse_std[:], in0=var_eps[:], in1=minus_half[:], op=ALU.pow)
+            rstd[tile_no] = inverse_std
+
+        transpose_q(0)
+        copy_q(0)
+        for i in range(-1, UNITS + CLOSING_LAG):
+            if 0 <= i - 1 < UNITS:
+                exponentials(i - 1)
+            if 0 <= i - 2 < UNITS:
+                regroup(i - 2)
+            next_tile, h = divmod(i + 4, HEADS)
+            if h == 1 and 1 <= next_tile < TILES:
+                copy_q(next_tile)
+            if 0 <= i + 1 < UNITS:
+                scores(i + 1)
+            if 0 <= i - 1 < UNITS:
+                flip(i - 1)
+            closing_tile, piece = divmod(i - CLOSING_LAG, HEADS)
+            if 0 <= i < UNITS:
+                scale_and_max(i)
+            if 0 <= closing_tile < TILES and piece == 0:
+                invert_row_sums(closing_tile)
+            if 0 <= i - 3 < UNITS:
+                quantise(i - 3)
+                attend(i - 3)
+            if 0 <= i < UNITS:
+                row_max(i)
+            if 0 <= closing_tile < TILES and piece < 2 * HALVES:
+                closing_piece(closing_tile, piece % 2, piece // 2)
+            elif 0 <= closing_tile < TILES:
+                closing_piece(closing_tile, piece // HALVES, piece % HALVES)
+            if h == 0 and 1 <= next_tile < TILES:
+                transpose_q(next_tile)

@@ -29,7 +29,8 @@ UNITS = TILES * HEADS
 SCALE = 1.0 / math.sqrt(DH)
 LN_EPS = 1e-5
 
-CLOSING_LAG = 9
+GROUPS = UNITS // HALF_HEADS
+VECTOR_PLACE = 2
 
 FLOPS = 2 * NODES * C_IN * C_OUT * 2 + 2 * HEADS * NODES * NODES * DH * 2
 
@@ -43,8 +44,8 @@ def tile_transformergraphconv_pa_kernel(tc, x, q, k, W_v, conv_w, conv_b, ln_w, 
         work = ctx.enter_context(tc.tile_pool(name="work", bufs=3))
         small = ctx.enter_context(tc.tile_pool(name="small", bufs=4))
         psum_s = ctx.enter_context(tc.psum_pool(name="psum_s", bufs=4))
-        psum_t = ctx.enter_context(tc.psum_pool(name="psum_t", bufs=2))
-        psum_o = ctx.enter_context(tc.psum_pool(name="psum_o", bufs=2))
+        psum_t = ctx.enter_context(tc.psum_pool(name="psum_t", bufs=3))
+        psum_o = ctx.enter_context(tc.psum_pool(name="psum_o", bufs=1))
 
         ident_f32 = keep.tile([P, P], F32)
         make_identity(nc, ident_f32[:])
@@ -139,6 +140,7 @@ def tile_transformergraphconv_pa_kernel(tc, x, q, k, W_v, conv_w, conv_b, ln_w, 
         v_codes = keep.tile([P, HEADS, PASSES, DH], U32, align_bytes=64)
         v_scales = keep.tile([P, HEADS, PASSES, DH], U8, align_bytes=64)
         y_all = keep.tile([P, TILES, C_OUT], F32)
+        y_sums = keep.tile([P, TILES, 2 * HALVES], F32)
         for n in range(HEADS):
             v_grouped = stage.tile([P, PASSES, DH, PACK], BF16, tag="v_grouped", align_bytes=64)
             for g in range(PASSES):
@@ -169,7 +171,15 @@ def tile_transformergraphconv_pa_kernel(tc, x, q, k, W_v, conv_w, conv_b, ln_w, 
                     start=True,
                     stop=True,
                 )
-                nc.vector.tensor_tensor(out=y_all[:, n, cols], in0=proj_bank[:], in1=conv_b_all[:, cols], op=ALU.add)
+                nc.vector.scalar_tensor_tensor(
+                    out=y_all[:, n, cols],
+                    in0=proj_bank[:],
+                    scalar=0.0,
+                    in1=conv_b_all[:, cols],
+                    op0=ALU.add,
+                    op1=ALU.add,
+                    accum_out=y_sums[:, n, half : half + 1],
+                )
 
             nc.vector.quantize_mx(
                 out=v_codes[:, n, :, :].rearrange("p g d -> p (g d)").bitcast(FP8X4),
@@ -222,21 +232,21 @@ def tile_transformergraphconv_pa_kernel(tc, x, q, k, W_v, conv_w, conv_b, ln_w, 
                 banks.append(s_bank)
             s_banks[unit] = banks
 
-        def scale_and_max(unit):
-            scaled = work.tile([P, NODES], F32, tag="scaled")
-            bank_max = small.tile([P, PASSES], F32, tag="bank_max")
-            for g in range(PASSES):
-                nc.vector.tensor_scalar(
-                    out=scaled[:, BANK * g : BANK * g + BANK],
-                    in0=s_banks[unit][g][:],
-                    scalar1=SCALE,
-                    scalar2=None,
-                    op0=ALU.mult,
-                    op1=ALU.max,
-                    accum_out=bank_max[:, g : g + 1],
-                )
-            s_rows[unit] = scaled
-            bank_maxima[unit] = bank_max
+        def scale_and_max(unit, g):
+            if g == 0:
+                scaled = work.tile([P, NODES], F32, tag="scaled", bufs=4)
+                s_rows[unit] = scaled
+                bank_max = small.tile([P, PASSES], F32, tag="bank_max")
+                bank_maxima[unit] = bank_max
+            nc.vector.tensor_scalar(
+                out=s_rows[unit][:, BANK * g : BANK * g + BANK],
+                in0=s_banks[unit][g][:],
+                scalar1=SCALE,
+                scalar2=None,
+                op0=ALU.mult,
+                op1=ALU.max,
+                accum_out=bank_maxima[unit][:, g : g + 1],
+            )
 
         def row_max(unit):
             minus_max = small.tile([P, 1], F32, tag="shift")
@@ -276,114 +286,92 @@ def tile_transformergraphconv_pa_kernel(tc, x, q, k, W_v, conv_w, conv_b, ln_w, 
             e_flipped[unit] = flipped
 
         def regroup(unit):
-            grouped = work.tile([P, PASSES, P, PACK], BF16, tag="e_grouped", align_bytes=64)
-            nc.scalar.copy(out=grouped[:].bitcast(F32), in_=e_flipped[unit][:].rearrange("p g u r -> p g r u"))
-            e_grouped[unit] = grouped
-
-        def quantise(unit):
-            e_codes = work.tile([P, PASSES, P], U32, tag="e_codes", align_bytes=64)
-            e_scales = work.tile([P, PASSES, P], U8, tag="e_scales", align_bytes=64)
-            nc.vector.quantize_mx(
-                out=e_codes[:].rearrange("p g r -> p (g r)").bitcast(FP8X4),
-                scales=e_scales[:].rearrange("p g r -> p (g r)"),
-                in_=e_grouped[unit][:].rearrange("p g r t -> p (g r t)"),
-            )
-            e_packed[unit] = (e_codes, e_scales)
-
-        def attend(unit):
-            tile_no, h = divmod(unit, HEADS)
-            half, place = divmod(h, HALF_HEADS)
+            group, place = divmod(unit, HALF_HEADS)
             if place == 0:
-                o_bank = psum_o.tile([P, HALF_HEADS, DH], F32, tag="o")
-                o_banks[(tile_no, half)] = o_bank
-            e_codes, e_scales = e_packed[unit]
-            for g in range(PASSES):
-                nc.tensor.matmul_mx(
-                    out=o_banks[(tile_no, half)][:, place, :],
-                    lhsT=e_codes[:, g, :].bitcast(FP8X4),
-                    lhsT_scale=e_scales[:, g, :],
-                    rhs=v_codes[:, h, g, :].bitcast(FP8X4),
-                    rhs_scale=v_scales[:, h, g, :],
-                    start=(g == 0),
-                    stop=(g == PASSES - 1),
-                )
+                grouped = work.tile([P, HALF_HEADS, PASSES, P, PACK], BF16, tag="e_grouped", bufs=2, align_bytes=64)
+                e_grouped[group] = grouped
+            words_out = e_grouped[group][:, place, :, :, :].bitcast(F32)
+            words_in = e_flipped[unit][:].rearrange("p g u r -> p g r u")
+            if place == VECTOR_PLACE:
+                nc.vector.tensor_copy(out=words_out, in_=words_in)
+            else:
+                nc.scalar.copy(out=words_out, in_=words_in)
+
+        def quantise(group):
+            e_codes = work.tile([P, HALF_HEADS, PASSES, P], U32, tag="e_codes", bufs=2, align_bytes=64)
+            e_scales = work.tile([P, HALF_HEADS, PASSES, P], U8, tag="e_scales", bufs=2, align_bytes=64)
+            nc.vector.quantize_mx(
+                out=e_codes[:].rearrange("p n g r -> p (n g r)").bitcast(FP8X4),
+                scales=e_scales[:].rearrange("p n g r -> p (n g r)"),
+                in_=e_grouped[group][:].rearrange("p n g r t -> p (n g r t)"),
+            )
+            e_packed[group] = (e_codes, e_scales)
+
+        def attend(group):
+            o_bank = psum_o.tile([P, HALF_HEADS, DH], F32, tag="o")
+            o_banks[group] = o_bank
+            e_codes, e_scales = e_packed[group]
+            for place in range(HALF_HEADS):
+                h = (HALF_HEADS * group + place) % HEADS
+                for g in range(PASSES):
+                    nc.tensor.matmul_mx(
+                        out=o_bank[:, place, :],
+                        lhsT=e_codes[:, place, g, :].bitcast(FP8X4),
+                        lhsT_scale=e_scales[:, place, g, :],
+                        rhs=v_codes[:, h, g, :].bitcast(FP8X4),
+                        rhs_scale=v_scales[:, h, g, :],
+                        start=(g == 0),
+                        stop=(g == PASSES - 1),
+                    )
 
         attended = {}
-        y_sums = {}
         minus_mean = {}
         rstd = {}
         centred = {}
         out_rows = out.rearrange("b (a p e) c -> (b a) e p c", p=P, e=2)
 
-        def invert_row_sums(tile_no):
-            inverse = small.tile([P, HEADS], F32, tag="inverse")
-            nc.vector.reciprocal(out=inverse[:], in_=row_sums[tile_no][:])
-            inverse_sums[tile_no] = inverse
+        def invert_row_sums(group):
+            tile_no, half = divmod(group, HALVES)
+            heads = slice(HALF_HEADS * half, HALF_HEADS * half + HALF_HEADS)
+            inverse = small.tile([P, HALF_HEADS], F32, tag="inverse")
+            nc.vector.reciprocal(out=inverse[:], in_=row_sums[tile_no][:, heads])
+            inverse_sums[group] = inverse
 
-        def closing_piece(tile_no, step, half):
+        def relu_and_divide(group):
+            tile_no, half = divmod(group, HALVES)
+            relu_o = work.tile([P, HALF_HEADS, DH], F32, tag="attended")
+            nc.vector.scalar_tensor_tensor(
+                out=relu_o[:],
+                in0=o_banks[group][:],
+                scalar=0.0,
+                in1=inverse_sums[group][:].unsqueeze(2).to_broadcast([P, HALF_HEADS, DH]),
+                op0=ALU.max,
+                op1=ALU.mult,
+                accum_out=y_sums[:, tile_no, HALVES + half : HALVES + half + 1],
+            )
+            attended[group] = relu_o
+
+        def add_streams(group):
+            tile_no, half = divmod(group, HALVES)
             cols = slice(BANK * half, BANK * half + BANK)
-            y = y_all[:, tile_no, :]
-            if step == 0:
-                heads = slice(HALF_HEADS * half, HALF_HEADS * half + HALF_HEADS)
-                relu_o = work.tile([P, HALF_HEADS, DH], F32, tag="attended")
-                nc.vector.scalar_tensor_tensor(
-                    out=relu_o[:],
-                    in0=o_banks[(tile_no, half)][:],
-                    scalar=0.0,
-                    in1=inverse_sums[tile_no][:, heads].unsqueeze(2).to_broadcast([P, HALF_HEADS, DH]),
-                    op0=ALU.max,
-                    op1=ALU.mult,
-                )
-                attended[(tile_no, half)] = relu_o
-            elif step == 1:
-                if half == 0:
-                    sums = small.tile([P, HALVES], F32, tag="y_sums")
-                    y_sums[tile_no] = sums
-                nc.vector.scalar_tensor_tensor(
-                    out=y[:, cols],
-                    in0=attended[(tile_no, half)][:].rearrange("p h d -> p (h d)"),
-                    scalar=0.0,
-                    in1=y[:, cols],
-                    op0=ALU.add,
-                    op1=ALU.add,
-                    accum_out=y_sums[tile_no][:, half : half + 1],
-                )
-                if half == HALVES - 1:
-                    mean(tile_no)
-            elif step == 2:
-                if half == 0:
-                    deviation(tile_no)
-                    scaled = work.tile([P, C_OUT], F32, tag="centred", bufs=2)
-                    centred[tile_no] = scaled
-                nc.vector.scalar_tensor_tensor(
-                    out=centred[tile_no][:, cols],
-                    in0=y[:, cols],
-                    scalar=minus_mean[tile_no][:, 0:1],
-                    in1=ln_w_all[:, cols],
-                    op0=ALU.add,
-                    op1=ALU.mult,
-                )
-            else:
-                result = work.tile([P, BANK], F32, tag="result")
-                nc.vector.scalar_tensor_tensor(
-                    out=result[:],
-                    in0=centred[tile_no][:, cols],
-                    scalar=rstd[tile_no][:, 0:1],
-                    in1=ln_b_all[:, cols],
-                    op0=ALU.mult,
-                    op1=ALU.add,
-                )
-                nc.sync.dma_start(out=out_rows[tile_no // 2, tile_no % 2, :, cols], in_=result[:])
+            nc.gpsimd.tensor_tensor(
+                out=y_all[:, tile_no, cols],
+                in0=attended[group][:].rearrange("p h d -> p (h d)"),
+                in1=y_all[:, tile_no, cols],
+                op=ALU.add,
+            )
 
         def mean(tile_no):
+            shares = small.tile([P, 2 * HALVES], F32, tag="shares")
             negative = small.tile([P, 1], F32, tag="minus_mean")
             nc.vector.tensor_scalar(
-                out=negative[:],
-                in0=y_sums[tile_no][:, 0:1],
-                scalar1=y_sums[tile_no][:, 1:2],
-                scalar2=-1.0 / C_OUT,
-                op0=ALU.add,
-                op1=ALU.mult,
+                out=shares[:],
+                in0=y_sums[:, tile_no, :],
+                scalar1=-1.0 / C_OUT,
+                scalar2=None,
+                op0=ALU.mult,
+                op1=ALU.add,
+                accum_out=negative[:, 0:1],
             )
             minus_mean[tile_no] = negative
 
@@ -406,33 +394,92 @@ def tile_transformergraphconv_pa_kernel(tc, x, q, k, W_v, conv_w, conv_b, ln_w, 
             nc.gpsimd.tensor_tensor(out=inverse_std[:], in0=var_eps[:], in1=minus_half[:], op=ALU.pow)
             rstd[tile_no] = inverse_std
 
+        def normalise_first_half(tile_no):
+            cols = slice(0, BANK)
+            result = work.tile([P, BANK], F32, tag="result")
+            nc.gpsimd.tensor_scalar(
+                out=result[:],
+                in0=y_all[:, tile_no, cols],
+                scalar1=minus_mean[tile_no][:, 0:1],
+                scalar2=rstd[tile_no][:, 0:1],
+                op0=ALU.add,
+                op1=ALU.mult,
+            )
+            nc.gpsimd.tensor_tensor(out=result[:], in0=result[:], in1=ln_w_all[:, cols], op=ALU.mult)
+            nc.gpsimd.tensor_tensor(out=result[:], in0=result[:], in1=ln_b_all[:, cols], op=ALU.add)
+            nc.sync.dma_start(out=out_rows[tile_no // 2, tile_no % 2, :, cols], in_=result[:])
+
+        def centre_second_half(tile_no):
+            cols = slice(BANK, C_OUT)
+            scaled = work.tile([P, BANK], F32, tag="centred", bufs=2)
+            nc.vector.scalar_tensor_tensor(
+                out=scaled[:],
+                in0=y_all[:, tile_no, cols],
+                scalar=minus_mean[tile_no][:, 0:1],
+                in1=ln_w_all[:, cols],
+                op0=ALU.add,
+                op1=ALU.mult,
+            )
+            centred[tile_no] = scaled
+
+        def finish_second_half(tile_no):
+            cols = slice(BANK, C_OUT)
+            result = work.tile([P, BANK], F32, tag="result")
+            nc.vector.scalar_tensor_tensor(
+                out=result[:],
+                in0=centred[tile_no][:],
+                scalar=rstd[tile_no][:, 0:1],
+                in1=ln_b_all[:, cols],
+                op0=ALU.mult,
+                op1=ALU.add,
+            )
+            nc.sync.dma_start(out=out_rows[tile_no // 2, tile_no % 2, :, cols], in_=result[:])
+
+        GROUP_LAG = HALF_HEADS - 1 + 4
+        TILE_LAG = HEADS - 1 + 4 + 2
         transpose_q(0)
         copy_q(0)
-        for i in range(-1, UNITS + CLOSING_LAG):
+        scores(0)
+        scores(1)
+        for i in range(UNITS + TILE_LAG - HEADS + 6):
+            group, group_step = divmod(i - GROUP_LAG, HALF_HEADS)
+            tile_no, tile_step = divmod(i - TILE_LAG, HEADS)
+            next_tile, h = divmod(i + 5, HEADS)
+
+            if i < UNITS:
+                scale_and_max(i, 0)
+                scale_and_max(i, 1)
+            if i + 2 < UNITS:
+                scores(i + 2)
             if 0 <= i - 1 < UNITS:
                 exponentials(i - 1)
-            if 0 <= i - 2 < UNITS:
-                regroup(i - 2)
-            next_tile, h = divmod(i + 4, HEADS)
+                flip(i - 1)
+            if 0 <= i - 3 < UNITS:
+                regroup(i - 3)
             if h == 1 and 1 <= next_tile < TILES:
                 copy_q(next_tile)
-            if 0 <= i + 1 < UNITS:
-                scores(i + 1)
-            if 0 <= i - 1 < UNITS:
-                flip(i - 1)
-            closing_tile, piece = divmod(i - CLOSING_LAG, HEADS)
-            if 0 <= i < UNITS:
-                scale_and_max(i)
-            if 0 <= closing_tile < TILES and piece == 0:
-                invert_row_sums(closing_tile)
-            if 0 <= i - 3 < UNITS:
-                quantise(i - 3)
-                attend(i - 3)
-            if 0 <= i < UNITS:
+
+            if 0 <= group < GROUPS:
+                if group_step == 0:
+                    invert_row_sums(group)
+                    quantise(group)
+                    attend(group)
+                elif group_step == 1:
+                    relu_and_divide(group)
+                elif group_step == 2:
+                    add_streams(group)
+            if 0 <= tile_no < TILES:
+                if tile_step == 0:
+                    mean(tile_no)
+                elif tile_step == 1:
+                    centre_second_half(tile_no)
+                elif tile_step == 2:
+                    deviation(tile_no)
+                elif tile_step == 3:
+                    normalise_first_half(tile_no)
+                elif tile_step == 5:
+                    finish_second_half(tile_no)
+            if i < UNITS:
                 row_max(i)
-            if 0 <= closing_tile < TILES and piece < 2 * HALVES:
-                closing_piece(closing_tile, piece % 2, piece // 2)
-            elif 0 <= closing_tile < TILES:
-                closing_piece(closing_tile, piece // HALVES, piece % HALVES)
             if h == 0 and 1 <= next_tile < TILES:
                 transpose_q(next_tile)

@@ -26,11 +26,9 @@ PASSES = NODES // (P * PACK)
 HALVES = C_OUT // BANK
 HALF_HEADS = BANK // DH
 UNITS = TILES * HEADS
+GROUPS = UNITS // HALF_HEADS
 SCALE = 1.0 / math.sqrt(DH)
 LN_EPS = 1e-5
-
-GROUPS = UNITS // HALF_HEADS
-VECTOR_PLACE = 2
 
 FLOPS = 2 * NODES * C_IN * C_OUT * 2 + 2 * HEADS * NODES * NODES * DH * 2
 
@@ -68,81 +66,91 @@ def tile_transformergraphconv_pa_kernel(tc, x, q, k, W_v, conv_w, conv_b, ln_w, 
         ln_w_all = keep.tile([P, C_OUT], BF16)
         ln_b_all = keep.tile([P, C_OUT], BF16)
 
-        for a in range(PAIRS):
-            nc.sync.dma_start(out=x_sb[:, a, :, :].rearrange("p e c -> p (e c)"), in_=x_rows[a, :, :])
-        for half in range(2):
+        def load_k(h):
+            nc.sync.dma_start(out=k_sb[:, h, :, :], in_=k_rows[h, :, :, :])
+
+        def load_q(a):
+            nc.sync.dma_start(
+                out=q_sb[:, :, a, :, :].rearrange("p h e d -> p h (e d)"), in_=q_rows[a, :, :, :]
+            )
+
+        def load_wv(half):
             heads = slice(HALF_HEADS * half, HALF_HEADS * half + HALF_HEADS)
             for u in range(2):
                 nc.sync.dma_start(
                     out=wv_sb[:, heads, 2 * u : 2 * u + 2, :].rearrange("p h e d -> p h (e d)"),
                     in_=wv_rows[u, :, heads, :],
                 )
+
+        for a in range(PAIRS):
+            nc.sync.dma_start(out=x_sb[:, a, :, :].rearrange("p e c -> p (e c)"), in_=x_rows[a, :, :])
+        for half in range(2):
+            load_wv(half)
         for half in range(2):
             rows = slice(PACK * half, PACK * half + PACK)
             nc.sync.dma_start(out=cw_sb[:, rows, :], in_=cw_rows[:, rows, :])
         nc.sync.dma_start(out=conv_b_all[:], in_=conv_b.partition_broadcast(P))
         for h in range(HEADS):
-            nc.sync.dma_start(out=k_sb[:, h, :, :], in_=k_rows[h, :, :, :])
+            load_k(h)
         for a in range(PAIRS):
-            nc.sync.dma_start(
-                out=q_sb[:, :, a, :, :].rearrange("p h e d -> p h (e d)"), in_=q_rows[a, :, :, :]
-            )
+            load_q(a)
         nc.sync.dma_start(out=ln_w_all[:], in_=ln_w.partition_broadcast(P))
         nc.sync.dma_start(out=ln_b_all[:], in_=ln_b.partition_broadcast(P))
 
-        def quantise_channels_last(rows_sb, codes, scales):
-            words = rows_sb.bitcast(F32)
-            for half in range(2):
-                grouped = stage.tile([P, PACK, P, PACK], BF16, tag="grouped", align_bytes=64)
-                grouped_words = grouped[:].bitcast(F32)
-                for pair in range(2):
-                    flipped = psum_t.tile([P, 2, 2, P], F32, tag="flip")
-                    for i in range(2):
-                        for u in range(2):
-                            nc.tensor.transpose(
-                                flipped[:, i, u, :],
-                                words[:, PACK * half + 2 * pair + i, P * u : P * u + P],
-                                ident_f32[:],
-                            )
-                    nc.scalar.copy(
-                        out=grouped_words[:, 2 * pair : 2 * pair + 2, :, :],
-                        in_=flipped[:].rearrange("p i u r -> p i r u"),
-                    )
-                cols = slice(BANK * half, BANK * half + BANK)
-                nc.vector.quantize_mx(
-                    out=codes[:, cols].bitcast(FP8X4),
-                    scales=scales[:, cols],
-                    in_=grouped[:].rearrange("p j r t -> p (j r t)"),
-                )
-
         x_codes = keep.tile([P, NODES], U32, align_bytes=64)
         x_scales = keep.tile([P, NODES], U8, align_bytes=64)
-        quantise_channels_last(x_sb[:].rearrange("p a e c -> p (a e) c"), x_codes[:], x_scales[:])
-
         wv_codes = keep.tile([P, HEADS * DH], U32, align_bytes=64)
         wv_scales = keep.tile([P, HEADS * DH], U8, align_bytes=64)
-        for half in range(2):
+        cw_codes = keep.tile([P, C_OUT], U32, align_bytes=64)
+        cw_scales = keep.tile([P, C_OUT], U8, align_bytes=64)
+        v_codes = keep.tile([P, HEADS, PASSES, DH], U32, align_bytes=64)
+        v_scales = keep.tile([P, HEADS, PASSES, DH], U8, align_bytes=64)
+        kT = keep.tile([P, HEADS, NODES], BF16)
+        y_all = keep.tile([P, TILES, C_OUT], F32)
+
+        def quantise_channels_last(rows_sb, codes, scales, half):
+            words = rows_sb.bitcast(F32)
+            grouped = stage.tile([P, PACK, P, PACK], BF16, tag="grouped", align_bytes=64)
+            grouped_words = grouped[:].bitcast(F32)
+            for pair in range(2):
+                flipped = psum_t.tile([P, 2, 2, P], F32, tag="flip")
+                for n in range(2):
+                    for u in range(2):
+                        nc.tensor.transpose(
+                            flipped[:, n, u, :],
+                            words[:, PACK * half + 2 * pair + n, P * u : P * u + P],
+                            ident_f32[:],
+                        )
+                nc.scalar.copy(
+                    out=grouped_words[:, 2 * pair : 2 * pair + 2, :, :],
+                    in_=flipped[:].rearrange("p n u r -> p n r u"),
+                )
+            cols = slice(BANK * half, BANK * half + BANK)
+            nc.vector.quantize_mx(
+                out=codes[:, cols].bitcast(FP8X4),
+                scales=scales[:, cols],
+                in_=grouped[:].rearrange("p j r t -> p (j r t)"),
+            )
+
+        def quantise_wv(half):
             heads = slice(HALF_HEADS * half, HALF_HEADS * half + HALF_HEADS)
             cols = slice(BANK * half, BANK * half + BANK)
             wv_grouped = stage.tile([P, HALF_HEADS, DH, PACK], BF16, tag="grouped", align_bytes=64)
-            nc.vector.tensor_copy(out=wv_grouped[:], in_=wv_sb[:, heads, :, :].rearrange("p h t d -> p h d t"))
+            if half == 0:
+                nc.vector.tensor_copy(out=wv_grouped[:], in_=wv_sb[:, heads, :, :].rearrange("p h t d -> p h d t"))
+            else:
+                nc.scalar.copy(out=wv_grouped[:], in_=wv_sb[:, heads, :, :].rearrange("p h t d -> p h d t"))
             nc.vector.quantize_mx(
                 out=wv_codes[:, cols].bitcast(FP8X4),
                 scales=wv_scales[:, cols],
                 in_=wv_grouped[:].rearrange("p h d t -> p (h d t)"),
             )
 
-        cw_codes = keep.tile([P, C_OUT], U32, align_bytes=64)
-        cw_scales = keep.tile([P, C_OUT], U8, align_bytes=64)
-        quantise_channels_last(cw_sb[:], cw_codes[:], cw_scales[:])
+        v_grouped = {}
 
-        kT = keep.tile([P, HEADS, NODES], BF16)
-        v_codes = keep.tile([P, HEADS, PASSES, DH], U32, align_bytes=64)
-        v_scales = keep.tile([P, HEADS, PASSES, DH], U8, align_bytes=64)
-        y_all = keep.tile([P, TILES, C_OUT], F32)
-        y_sums = keep.tile([P, TILES, 2 * HALVES], F32)
-        for n in range(HEADS):
-            v_grouped = stage.tile([P, PASSES, DH, PACK], BF16, tag="v_grouped", align_bytes=64)
+        def values(h):
+            grouped = stage.tile([P, PASSES, DH, PACK], BF16, tag="v_grouped", align_bytes=64)
+            v_grouped[h] = grouped
             for g in range(PASSES):
                 v_bank = psum_s.tile([P, PACK, DH], F32, tag="s")
                 for t in range(PACK):
@@ -151,46 +159,45 @@ def tile_transformergraphconv_pa_kernel(tc, x, q, k, W_v, conv_w, conv_b, ln_w, 
                         out=v_bank[:, t, :],
                         lhsT=x_codes[:, nodes].bitcast(FP8X4),
                         lhsT_scale=x_scales[:, nodes],
-                        rhs=wv_codes[:, DH * n : DH * n + DH].bitcast(FP8X4),
-                        rhs_scale=wv_scales[:, DH * n : DH * n + DH],
+                        rhs=wv_codes[:, DH * h : DH * h + DH].bitcast(FP8X4),
+                        rhs_scale=wv_scales[:, DH * h : DH * h + DH],
                         start=True,
                         stop=True,
                     )
-                nc.scalar.copy(out=v_grouped[:, g, :, :], in_=v_bank[:].rearrange("p t d -> p d t"))
+                nc.scalar.copy(out=grouped[:, g, :, :], in_=v_bank[:].rearrange("p t d -> p d t"))
 
-            nodes = slice(P * n, P * n + P)
-            for half in range(HALVES):
-                cols = slice(BANK * half, BANK * half + BANK)
-                proj_bank = psum_s.tile([P, BANK], F32, tag="s")
-                nc.tensor.matmul_mx(
-                    out=proj_bank[:],
-                    lhsT=x_codes[:, nodes].bitcast(FP8X4),
-                    lhsT_scale=x_scales[:, nodes],
-                    rhs=cw_codes[:, cols].bitcast(FP8X4),
-                    rhs_scale=cw_scales[:, cols],
-                    start=True,
-                    stop=True,
-                )
-                nc.vector.scalar_tensor_tensor(
-                    out=y_all[:, n, cols],
-                    in0=proj_bank[:],
-                    scalar=0.0,
-                    in1=conv_b_all[:, cols],
-                    op0=ALU.add,
-                    op1=ALU.add,
-                    accum_out=y_sums[:, n, half : half + 1],
-                )
-
+        def quantise_values(h):
             nc.vector.quantize_mx(
-                out=v_codes[:, n, :, :].rearrange("p g d -> p (g d)").bitcast(FP8X4),
-                scales=v_scales[:, n, :, :].rearrange("p g d -> p (g d)"),
-                in_=v_grouped[:].rearrange("p g d t -> p (g d t)"),
+                out=v_codes[:, h, :, :].rearrange("p g d -> p (g d)").bitcast(FP8X4),
+                scales=v_scales[:, h, :, :].rearrange("p g d -> p (g d)"),
+                in_=v_grouped[h][:].rearrange("p g d t -> p (g d t)"),
             )
 
-            k_flipped = psum_t.tile([P, TILES, P], BF16, tag="flip")
+        def projection(tile_no, half):
+            nodes = slice(P * tile_no, P * tile_no + P)
+            cols = slice(BANK * half, BANK * half + BANK)
+            proj_bank = psum_s.tile([P, BANK], F32, tag="s")
+            nc.tensor.matmul_mx(
+                out=proj_bank[:],
+                lhsT=x_codes[:, nodes].bitcast(FP8X4),
+                lhsT_scale=x_scales[:, nodes],
+                rhs=cw_codes[:, cols].bitcast(FP8X4),
+                rhs_scale=cw_scales[:, cols],
+                start=True,
+                stop=True,
+            )
+            nc.vector.tensor_tensor(out=y_all[:, tile_no, cols], in0=proj_bank[:], in1=conv_b_all[:, cols], op=ALU.add)
+
+        k_flipped = {}
+
+        def transpose_k(h):
+            flipped = psum_t.tile([P, TILES, P], BF16, tag="flip")
             for j in range(TILES):
-                nc.tensor.transpose(k_flipped[:, j, :], k_sb[:, n, j, :], ident_bf[:])
-            nc.scalar.copy(out=kT[:, n, :], in_=k_flipped[:].rearrange("d j p -> d (j p)"))
+                nc.tensor.transpose(flipped[:, j, :], k_sb[:, h, j, :], ident_bf[:])
+            k_flipped[h] = flipped
+
+        def copy_k(h):
+            nc.scalar.copy(out=kT[:, h, :], in_=k_flipped[h][:].rearrange("d j p -> d (j p)"))
 
         q_flipped = {}
         qT = {}
@@ -199,7 +206,6 @@ def tile_transformergraphconv_pa_kernel(tc, x, q, k, W_v, conv_w, conv_b, ln_w, 
         bank_maxima = {}
         shift = {}
         row_sums = {}
-        inverse_sums = {}
         e_rows = {}
         e_flipped = {}
         e_grouped = {}
@@ -232,21 +238,21 @@ def tile_transformergraphconv_pa_kernel(tc, x, q, k, W_v, conv_w, conv_b, ln_w, 
                 banks.append(s_bank)
             s_banks[unit] = banks
 
-        def scale_and_max(unit, g):
-            if g == 0:
-                scaled = work.tile([P, NODES], F32, tag="scaled", bufs=4)
-                s_rows[unit] = scaled
-                bank_max = small.tile([P, PASSES], F32, tag="bank_max")
-                bank_maxima[unit] = bank_max
-            nc.vector.tensor_scalar(
-                out=s_rows[unit][:, BANK * g : BANK * g + BANK],
-                in0=s_banks[unit][g][:],
-                scalar1=SCALE,
-                scalar2=None,
-                op0=ALU.mult,
-                op1=ALU.max,
-                accum_out=bank_maxima[unit][:, g : g + 1],
-            )
+        def scale_and_max(unit):
+            scaled = work.tile([P, NODES], F32, tag="scaled", bufs=4)
+            bank_max = small.tile([P, PASSES], F32, tag="bank_max")
+            for g in range(PASSES):
+                nc.vector.tensor_scalar(
+                    out=scaled[:, BANK * g : BANK * g + BANK],
+                    in0=s_banks[unit][g][:],
+                    scalar1=SCALE,
+                    scalar2=None,
+                    op0=ALU.mult,
+                    op1=ALU.max,
+                    accum_out=bank_max[:, g : g + 1],
+                )
+            s_rows[unit] = scaled
+            bank_maxima[unit] = bank_max
 
         def row_max(unit):
             minus_max = small.tile([P, 1], F32, tag="shift")
@@ -286,26 +292,22 @@ def tile_transformergraphconv_pa_kernel(tc, x, q, k, W_v, conv_w, conv_b, ln_w, 
             e_flipped[unit] = flipped
 
         def regroup(unit):
+            grouped = work.tile([P, PASSES, P, PACK], BF16, tag="e_grouped", align_bytes=64)
+            nc.scalar.copy(out=grouped[:].bitcast(F32), in_=e_flipped[unit][:].rearrange("p g u r -> p g r u"))
+            e_grouped[unit] = grouped
+
+        def quantise(unit):
             group, place = divmod(unit, HALF_HEADS)
             if place == 0:
-                grouped = work.tile([P, HALF_HEADS, PASSES, P, PACK], BF16, tag="e_grouped", bufs=2, align_bytes=64)
-                e_grouped[group] = grouped
-            words_out = e_grouped[group][:, place, :, :, :].bitcast(F32)
-            words_in = e_flipped[unit][:].rearrange("p g u r -> p g r u")
-            if place == VECTOR_PLACE:
-                nc.vector.tensor_copy(out=words_out, in_=words_in)
-            else:
-                nc.scalar.copy(out=words_out, in_=words_in)
-
-        def quantise(group):
-            e_codes = work.tile([P, HALF_HEADS, PASSES, P], U32, tag="e_codes", bufs=2, align_bytes=64)
-            e_scales = work.tile([P, HALF_HEADS, PASSES, P], U8, tag="e_scales", bufs=2, align_bytes=64)
+                e_codes = work.tile([P, HALF_HEADS, PASSES, P], U32, tag="e_codes", bufs=2, align_bytes=64)
+                e_scales = work.tile([P, HALF_HEADS, PASSES, P], U8, tag="e_scales", bufs=2, align_bytes=64)
+                e_packed[group] = (e_codes, e_scales)
+            e_codes, e_scales = e_packed[group]
             nc.vector.quantize_mx(
-                out=e_codes[:].rearrange("p n g r -> p (n g r)").bitcast(FP8X4),
-                scales=e_scales[:].rearrange("p n g r -> p (n g r)"),
-                in_=e_grouped[group][:].rearrange("p n g r t -> p (n g r t)"),
+                out=e_codes[:, place, :, :].rearrange("p g r -> p (g r)").bitcast(FP8X4),
+                scales=e_scales[:, place, :, :].rearrange("p g r -> p (g r)"),
+                in_=e_grouped[unit][:].rearrange("p g r t -> p (g r t)"),
             )
-            e_packed[group] = (e_codes, e_scales)
 
         def attend(group):
             o_bank = psum_o.tile([P, HALF_HEADS, DH], F32, tag="o")
@@ -324,7 +326,9 @@ def tile_transformergraphconv_pa_kernel(tc, x, q, k, W_v, conv_w, conv_b, ln_w, 
                         stop=(g == PASSES - 1),
                     )
 
+        inverse_sums = {}
         attended = {}
+        y_sums = {}
         minus_mean = {}
         rstd = {}
         centred = {}
@@ -338,7 +342,6 @@ def tile_transformergraphconv_pa_kernel(tc, x, q, k, W_v, conv_w, conv_b, ln_w, 
             inverse_sums[group] = inverse
 
         def relu_and_divide(group):
-            tile_no, half = divmod(group, HALVES)
             relu_o = work.tile([P, HALF_HEADS, DH], F32, tag="attended")
             nc.vector.scalar_tensor_tensor(
                 out=relu_o[:],
@@ -347,31 +350,34 @@ def tile_transformergraphconv_pa_kernel(tc, x, q, k, W_v, conv_w, conv_b, ln_w, 
                 in1=inverse_sums[group][:].unsqueeze(2).to_broadcast([P, HALF_HEADS, DH]),
                 op0=ALU.max,
                 op1=ALU.mult,
-                accum_out=y_sums[:, tile_no, HALVES + half : HALVES + half + 1],
             )
             attended[group] = relu_o
 
         def add_streams(group):
             tile_no, half = divmod(group, HALVES)
             cols = slice(BANK * half, BANK * half + BANK)
-            nc.gpsimd.tensor_tensor(
+            if half == 0:
+                sums = small.tile([P, HALVES], F32, tag="y_sums")
+                y_sums[tile_no] = sums
+            nc.vector.scalar_tensor_tensor(
                 out=y_all[:, tile_no, cols],
                 in0=attended[group][:].rearrange("p h d -> p (h d)"),
+                scalar=0.0,
                 in1=y_all[:, tile_no, cols],
-                op=ALU.add,
+                op0=ALU.add,
+                op1=ALU.add,
+                accum_out=y_sums[tile_no][:, half : half + 1],
             )
 
         def mean(tile_no):
-            shares = small.tile([P, 2 * HALVES], F32, tag="shares")
             negative = small.tile([P, 1], F32, tag="minus_mean")
             nc.vector.tensor_scalar(
-                out=shares[:],
-                in0=y_sums[:, tile_no, :],
-                scalar1=-1.0 / C_OUT,
-                scalar2=None,
-                op0=ALU.mult,
-                op1=ALU.add,
-                accum_out=negative[:, 0:1],
+                out=negative[:],
+                in0=y_sums[tile_no][:, 0:1],
+                scalar1=y_sums[tile_no][:, 1:2],
+                scalar2=-1.0 / C_OUT,
+                op0=ALU.add,
+                op1=ALU.mult,
             )
             minus_mean[tile_no] = negative
 
@@ -394,40 +400,26 @@ def tile_transformergraphconv_pa_kernel(tc, x, q, k, W_v, conv_w, conv_b, ln_w, 
             nc.gpsimd.tensor_tensor(out=inverse_std[:], in0=var_eps[:], in1=minus_half[:], op=ALU.pow)
             rstd[tile_no] = inverse_std
 
-        def normalise_first_half(tile_no):
-            cols = slice(0, BANK)
-            result = work.tile([P, BANK], F32, tag="result")
-            nc.gpsimd.tensor_scalar(
-                out=result[:],
-                in0=y_all[:, tile_no, cols],
-                scalar1=minus_mean[tile_no][:, 0:1],
-                scalar2=rstd[tile_no][:, 0:1],
-                op0=ALU.add,
-                op1=ALU.mult,
-            )
-            nc.gpsimd.tensor_tensor(out=result[:], in0=result[:], in1=ln_w_all[:, cols], op=ALU.mult)
-            nc.gpsimd.tensor_tensor(out=result[:], in0=result[:], in1=ln_b_all[:, cols], op=ALU.add)
-            nc.sync.dma_start(out=out_rows[tile_no // 2, tile_no % 2, :, cols], in_=result[:])
-
-        def centre_second_half(tile_no):
-            cols = slice(BANK, C_OUT)
-            scaled = work.tile([P, BANK], F32, tag="centred", bufs=2)
+        def centre(tile_no, half):
+            cols = slice(BANK * half, BANK * half + BANK)
+            if half == 0:
+                scaled = work.tile([P, C_OUT], F32, tag="centred", bufs=2)
+                centred[tile_no] = scaled
             nc.vector.scalar_tensor_tensor(
-                out=scaled[:],
+                out=centred[tile_no][:, cols],
                 in0=y_all[:, tile_no, cols],
                 scalar=minus_mean[tile_no][:, 0:1],
                 in1=ln_w_all[:, cols],
                 op0=ALU.add,
                 op1=ALU.mult,
             )
-            centred[tile_no] = scaled
 
-        def finish_second_half(tile_no):
-            cols = slice(BANK, C_OUT)
+        def finish(tile_no, half):
+            cols = slice(BANK * half, BANK * half + BANK)
             result = work.tile([P, BANK], F32, tag="result")
             nc.vector.scalar_tensor_tensor(
                 out=result[:],
-                in0=centred[tile_no][:],
+                in0=centred[tile_no][:, cols],
                 scalar=rstd[tile_no][:, 0:1],
                 in1=ln_b_all[:, cols],
                 op0=ALU.mult,
@@ -435,20 +427,34 @@ def tile_transformergraphconv_pa_kernel(tc, x, q, k, W_v, conv_w, conv_b, ln_w, 
             )
             nc.sync.dma_start(out=out_rows[tile_no // 2, tile_no % 2, :, cols], in_=result[:])
 
-        GROUP_LAG = HALF_HEADS - 1 + 4
-        TILE_LAG = HEADS - 1 + 4 + 2
+        for half in range(2):
+            quantise_channels_last(x_sb[:].rearrange("p a e c -> p (a e) c"), x_codes[:], x_scales[:], half)
+        for half in range(2):
+            quantise_wv(half)
+        for half in range(2):
+            quantise_channels_last(cw_sb[:], cw_codes[:], cw_scales[:], half)
+        for n in range(HEADS):
+            values(n)
+            for half in range(HALVES):
+                projection(n, half)
+            quantise_values(n)
+            transpose_k(n)
+            copy_k(n)
         transpose_q(0)
         copy_q(0)
+
+        GROUP_LAG = HALF_HEADS - 1 + 4
+        TILE_LAG = HEADS - 1 + 4 + 4
         scores(0)
         scores(1)
         for i in range(UNITS + TILE_LAG - HEADS + 6):
             group, group_step = divmod(i - GROUP_LAG, HALF_HEADS)
+            closing_group, closing_step = divmod(i - GROUP_LAG - 2, HALF_HEADS)
             tile_no, tile_step = divmod(i - TILE_LAG, HEADS)
             next_tile, h = divmod(i + 5, HEADS)
 
             if i < UNITS:
-                scale_and_max(i, 0)
-                scale_and_max(i, 1)
+                scale_and_max(i)
             if i + 2 < UNITS:
                 scores(i + 2)
             if 0 <= i - 1 < UNITS:
@@ -459,27 +465,27 @@ def tile_transformergraphconv_pa_kernel(tc, x, q, k, W_v, conv_w, conv_b, ln_w, 
             if h == 1 and 1 <= next_tile < TILES:
                 copy_q(next_tile)
 
-            if 0 <= group < GROUPS:
-                if group_step == 0:
-                    invert_row_sums(group)
-                    quantise(group)
-                    attend(group)
-                elif group_step == 1:
-                    relu_and_divide(group)
-                elif group_step == 2:
-                    add_streams(group)
-            if 0 <= tile_no < TILES:
-                if tile_step == 0:
-                    mean(tile_no)
-                elif tile_step == 1:
-                    centre_second_half(tile_no)
-                elif tile_step == 2:
-                    deviation(tile_no)
-                elif tile_step == 3:
-                    normalise_first_half(tile_no)
-                elif tile_step == 5:
-                    finish_second_half(tile_no)
+            if 0 <= group < GROUPS and group_step == 0:
+                invert_row_sums(group)
+            if 0 <= i - 4 < UNITS:
+                quantise(i - 4)
             if i < UNITS:
                 row_max(i)
+            if 0 <= group < GROUPS and group_step == 0:
+                attend(group)
+
+            if 0 <= closing_group < GROUPS and closing_step == 0:
+                relu_and_divide(closing_group)
+            if 0 <= closing_group < GROUPS and closing_step == 1:
+                add_streams(closing_group)
+                if closing_group % HALVES == HALVES - 1:
+                    mean(closing_group // HALVES)
+            if 0 <= tile_no < TILES:
+                if tile_step == 0:
+                    deviation(tile_no)
+                if tile_step in (0, 1):
+                    centre(tile_no, tile_step)
+                if tile_step in (4, 5):
+                    finish(tile_no, tile_step - 4)
             if h == 0 and 1 <= next_tile < TILES:
                 transpose_q(next_tile)

@@ -107,6 +107,7 @@ def tile_transformergraphconv_pa_kernel(tc, x, q, k, W_v, conv_w, conv_b, ln_w, 
         v_scales = keep.tile([P, HEADS, PASSES, DH], U8, align_bytes=64)
         kT = keep.tile([P, HEADS, NODES], BF16)
         y_all = keep.tile([P, TILES, C_OUT], F32)
+        y_sums = keep.tile([P, TILES, 2 * HALVES], F32)
 
         def quantise_channels_last(rows_sb, codes, scales, half):
             words = rows_sb.bitcast(F32)
@@ -186,7 +187,15 @@ def tile_transformergraphconv_pa_kernel(tc, x, q, k, W_v, conv_w, conv_b, ln_w, 
                 start=True,
                 stop=True,
             )
-            nc.vector.tensor_tensor(out=y_all[:, tile_no, cols], in0=proj_bank[:], in1=conv_b_all[:, cols], op=ALU.add)
+            nc.vector.scalar_tensor_tensor(
+                out=y_all[:, tile_no, cols],
+                in0=proj_bank[:],
+                scalar=0.0,
+                in1=conv_b_all[:, cols],
+                op0=ALU.add,
+                op1=ALU.add,
+                accum_out=y_sums[:, tile_no, half : half + 1],
+            )
 
         k_flipped = {}
 
@@ -292,28 +301,35 @@ def tile_transformergraphconv_pa_kernel(tc, x, q, k, W_v, conv_w, conv_b, ln_w, 
             e_flipped[unit] = flipped
 
         def regroup(unit):
-            grouped = work.tile([P, PASSES, P, PACK], BF16, tag="e_grouped", align_bytes=64)
-            nc.scalar.copy(out=grouped[:].bitcast(F32), in_=e_flipped[unit][:].rearrange("p g u r -> p g r u"))
-            e_grouped[unit] = grouped
-
-        def quantise(unit):
             group, place = divmod(unit, HALF_HEADS)
             if place == 0:
+                grouped = work.tile([P, HALF_HEADS, PASSES, P, PACK], BF16, tag="e_grouped", bufs=2, align_bytes=64)
+                e_grouped[group] = grouped
+            nc.scalar.copy(
+                out=e_grouped[group][:].bitcast(F32)[:, place, :, :, :],
+                in_=e_flipped[unit][:].rearrange("p g u r -> p g r u"),
+            )
+
+        def quantise(group, first, count):
+            if first == 0:
                 e_codes = work.tile([P, HALF_HEADS, PASSES, P], U32, tag="e_codes", bufs=2, align_bytes=64)
                 e_scales = work.tile([P, HALF_HEADS, PASSES, P], U8, tag="e_scales", bufs=2, align_bytes=64)
                 e_packed[group] = (e_codes, e_scales)
             e_codes, e_scales = e_packed[group]
+            places = slice(first, first + count)
             nc.vector.quantize_mx(
-                out=e_codes[:, place, :, :].rearrange("p g r -> p (g r)").bitcast(FP8X4),
-                scales=e_scales[:, place, :, :].rearrange("p g r -> p (g r)"),
-                in_=e_grouped[unit][:].rearrange("p g r t -> p (g r t)"),
+                out=e_codes[:, places, :, :].rearrange("p n g r -> p (n g r)").bitcast(FP8X4),
+                scales=e_scales[:, places, :, :].rearrange("p n g r -> p (n g r)"),
+                in_=e_grouped[group][:, places, :, :, :].rearrange("p n g r t -> p (n g r t)"),
             )
 
-        def attend(group):
-            o_bank = psum_o.tile([P, HALF_HEADS, DH], F32, tag="o")
-            o_banks[group] = o_bank
+        def attend(group, first, count):
+            if first == 0:
+                o_bank = psum_o.tile([P, HALF_HEADS, DH], F32, tag="o")
+                o_banks[group] = o_bank
+            o_bank = o_banks[group]
             e_codes, e_scales = e_packed[group]
-            for place in range(HALF_HEADS):
+            for place in range(first, first + count):
                 h = (HALF_HEADS * group + place) % HEADS
                 for g in range(PASSES):
                     nc.tensor.matmul_mx(
@@ -328,11 +344,13 @@ def tile_transformergraphconv_pa_kernel(tc, x, q, k, W_v, conv_w, conv_b, ln_w, 
 
         inverse_sums = {}
         attended = {}
-        y_sums = {}
         minus_mean = {}
+        square_sums = {}
         rstd = {}
-        centred = {}
         out_rows = out.rearrange("b (a p e) c -> (b a) e p c", p=P, e=2)
+
+        def half_cols(half):
+            return slice(BANK * half, BANK * half + BANK)
 
         def invert_row_sums(group):
             tile_no, half = divmod(group, HALVES)
@@ -342,6 +360,7 @@ def tile_transformergraphconv_pa_kernel(tc, x, q, k, W_v, conv_w, conv_b, ln_w, 
             inverse_sums[group] = inverse
 
         def relu_and_divide(group):
+            tile_no, half = divmod(group, HALVES)
             relu_o = work.tile([P, HALF_HEADS, DH], F32, tag="attended")
             nc.vector.scalar_tensor_tensor(
                 out=relu_o[:],
@@ -350,82 +369,111 @@ def tile_transformergraphconv_pa_kernel(tc, x, q, k, W_v, conv_w, conv_b, ln_w, 
                 in1=inverse_sums[group][:].unsqueeze(2).to_broadcast([P, HALF_HEADS, DH]),
                 op0=ALU.max,
                 op1=ALU.mult,
+                accum_out=y_sums[:, tile_no, HALVES + half : HALVES + half + 1],
             )
             attended[group] = relu_o
 
-        def add_streams(group):
+        def add_streams(engine, group):
             tile_no, half = divmod(group, HALVES)
-            cols = slice(BANK * half, BANK * half + BANK)
-            if half == 0:
-                sums = small.tile([P, HALVES], F32, tag="y_sums")
-                y_sums[tile_no] = sums
-            nc.vector.scalar_tensor_tensor(
-                out=y_all[:, tile_no, cols],
+            engine.tensor_tensor(
+                out=y_all[:, tile_no, half_cols(half)],
                 in0=attended[group][:].rearrange("p h d -> p (h d)"),
-                scalar=0.0,
-                in1=y_all[:, tile_no, cols],
-                op0=ALU.add,
-                op1=ALU.add,
-                accum_out=y_sums[tile_no][:, half : half + 1],
+                in1=y_all[:, tile_no, half_cols(half)],
+                op=ALU.add,
             )
 
         def mean(tile_no):
+            scaled_sums = small.tile([P, 2 * HALVES], F32, tag="scaled_sums")
             negative = small.tile([P, 1], F32, tag="minus_mean")
             nc.vector.tensor_scalar(
-                out=negative[:],
-                in0=y_sums[tile_no][:, 0:1],
-                scalar1=y_sums[tile_no][:, 1:2],
-                scalar2=-1.0 / C_OUT,
-                op0=ALU.add,
-                op1=ALU.mult,
+                out=scaled_sums[:],
+                in0=y_sums[:, tile_no, :],
+                scalar1=-1.0 / C_OUT,
+                scalar2=None,
+                op0=ALU.mult,
+                op1=ALU.add,
+                accum_out=negative[:, 0:1],
             )
             minus_mean[tile_no] = negative
 
-        def deviation(tile_no):
-            squares = work.tile([P, C_OUT], BF16, tag="squares", bufs=2)
+        def squares(tile_no):
+            squared = work.tile([P, C_OUT], BF16, tag="squared", bufs=2)
             square_sum = small.tile([P, 1], F32, tag="square_sum")
             nc.scalar.activation(
-                out=squares[:],
+                out=squared[:],
                 in_=y_all[:, tile_no, :],
                 func=ACT.Square,
                 bias=minus_mean[tile_no][:, 0:1],
                 scale=1.0,
                 accum_out=square_sum[:, 0:1],
             )
+            square_sums[tile_no] = square_sum
+
+        def deviation(tile_no):
             var_eps = small.tile([P, 1], F32, tag="var_eps")
             nc.gpsimd.tensor_scalar(
-                out=var_eps[:], in0=square_sum[:], scalar1=1.0 / C_OUT, scalar2=LN_EPS, op0=ALU.mult, op1=ALU.add
+                out=var_eps[:],
+                in0=square_sums[tile_no][:],
+                scalar1=1.0 / C_OUT,
+                scalar2=LN_EPS,
+                op0=ALU.mult,
+                op1=ALU.add,
             )
             inverse_std = small.tile([P, 1], F32, tag="rstd")
             nc.gpsimd.tensor_tensor(out=inverse_std[:], in0=var_eps[:], in1=minus_half[:], op=ALU.pow)
             rstd[tile_no] = inverse_std
 
+        def normalise(tile_no):
+            nc.gpsimd.tensor_scalar(
+                out=y_all[:, tile_no, :],
+                in0=y_all[:, tile_no, :],
+                scalar1=minus_mean[tile_no][:, 0:1],
+                scalar2=rstd[tile_no][:, 0:1],
+                op0=ALU.add,
+                op1=ALU.mult,
+            )
+
+        def affine(tile_no, half, vector, op):
+            cols = half_cols(half)
+            nc.gpsimd.tensor_tensor(
+                out=y_all[:, tile_no, cols], in0=y_all[:, tile_no, cols], in1=vector[:, cols], op=op
+            )
+
+        def store(tile_no, half):
+            cols = half_cols(half)
+            nc.sync.dma_start(out=out_rows[tile_no // 2, tile_no % 2, :, cols], in_=y_all[:, tile_no, cols])
+
         def centre(tile_no, half):
-            cols = slice(BANK * half, BANK * half + BANK)
-            if half == 0:
-                scaled = work.tile([P, C_OUT], F32, tag="centred", bufs=2)
-                centred[tile_no] = scaled
+            cols = half_cols(half)
+            centred = work.tile([P, BANK], F32, tag="attended")
             nc.vector.scalar_tensor_tensor(
-                out=centred[tile_no][:, cols],
+                out=centred[:],
                 in0=y_all[:, tile_no, cols],
                 scalar=minus_mean[tile_no][:, 0:1],
                 in1=ln_w_all[:, cols],
                 op0=ALU.add,
                 op1=ALU.mult,
             )
+            return centred
 
-        def finish(tile_no, half):
-            cols = slice(BANK * half, BANK * half + BANK)
-            result = work.tile([P, BANK], F32, tag="result")
+        def finish(tile_no, half, centred):
+            cols = half_cols(half)
             nc.vector.scalar_tensor_tensor(
-                out=result[:],
-                in0=centred[tile_no][:, cols],
+                out=y_all[:, tile_no, cols],
+                in0=centred[:],
                 scalar=rstd[tile_no][:, 0:1],
                 in1=ln_b_all[:, cols],
                 op0=ALU.mult,
                 op1=ALU.add,
             )
-            nc.sync.dma_start(out=out_rows[tile_no // 2, tile_no % 2, :, cols], in_=result[:])
+
+        def close_last(tile_no):
+            squares(tile_no)
+            centred = [centre(tile_no, half) for half in range(HALVES)]
+            deviation(tile_no)
+            for half in range(HALVES):
+                finish(tile_no, half, centred[half])
+                store(tile_no, half)
 
         for half in range(2):
             quantise_channels_last(x_sb[:].rearrange("p a e c -> p (a e) c"), x_codes[:], x_scales[:], half)
@@ -443,15 +491,16 @@ def tile_transformergraphconv_pa_kernel(tc, x, q, k, W_v, conv_w, conv_b, ln_w, 
         transpose_q(0)
         copy_q(0)
 
-        GROUP_LAG = HALF_HEADS - 1 + 4
-        TILE_LAG = HEADS - 1 + 4 + 4
+        LAG = 4
+        CLOSING_LAG = HALF_HEADS - 1 + LAG + 2
         scores(0)
         scores(1)
-        for i in range(UNITS + TILE_LAG - HEADS + 6):
-            group, group_step = divmod(i - GROUP_LAG, HALF_HEADS)
-            closing_group, closing_step = divmod(i - GROUP_LAG - 2, HALF_HEADS)
-            tile_no, tile_step = divmod(i - TILE_LAG, HEADS)
+        for i in range(UNITS + LAG + 2):
             next_tile, h = divmod(i + 5, HEADS)
+            group, place = divmod(i - LAG, HALF_HEADS)
+            closing_group, closing_step = divmod(i - CLOSING_LAG, HALF_HEADS)
+            closing_tile, closing_half = divmod(closing_group, HALVES)
+            closing = 0 <= closing_group < GROUPS - 1
 
             if i < UNITS:
                 scale_and_max(i)
@@ -465,27 +514,41 @@ def tile_transformergraphconv_pa_kernel(tc, x, q, k, W_v, conv_w, conv_b, ln_w, 
             if h == 1 and 1 <= next_tile < TILES:
                 copy_q(next_tile)
 
-            if 0 <= group < GROUPS and group_step == 0:
+            if 0 <= group < GROUPS and place == HALF_HEADS - 1:
                 invert_row_sums(group)
-            if 0 <= i - 4 < UNITS:
-                quantise(i - 4)
+            if 0 <= group < GROUPS - 1 and place == HALF_HEADS - 1:
+                quantise(group, 0, HALF_HEADS)
+            if group == GROUPS - 1:
+                quantise(group, place, 1)
             if i < UNITS:
                 row_max(i)
-            if 0 <= group < GROUPS and group_step == 0:
-                attend(group)
+            if 0 <= group < GROUPS - 1 and place == HALF_HEADS - 1:
+                attend(group, 0, HALF_HEADS)
+            if group == GROUPS - 1:
+                attend(group, place, 1)
 
-            if 0 <= closing_group < GROUPS and closing_step == 0:
+            if closing and closing_step == 0:
                 relu_and_divide(closing_group)
-            if 0 <= closing_group < GROUPS and closing_step == 1:
-                add_streams(closing_group)
-                if closing_group % HALVES == HALVES - 1:
-                    mean(closing_group // HALVES)
-            if 0 <= tile_no < TILES:
-                if tile_step == 0:
-                    deviation(tile_no)
-                if tile_step in (0, 1):
-                    centre(tile_no, tile_step)
-                if tile_step in (4, 5):
-                    finish(tile_no, tile_step - 4)
+                add_streams(nc.gpsimd, closing_group)
+                if closing_half == 0 and closing_tile >= 1:
+                    affine(closing_tile - 1, 1, ln_b_all, ALU.add)
+                    store(closing_tile - 1, 1)
+            if closing and closing_half == HALVES - 1:
+                if closing_step == 1:
+                    mean(closing_tile)
+                if closing_step == 2:
+                    squares(closing_tile)
+                    deviation(closing_tile)
+                    normalise(closing_tile)
+                if closing_step == 3:
+                    affine(closing_tile, 0, ln_w_all, ALU.mult)
+                    affine(closing_tile, 0, ln_b_all, ALU.add)
+                    store(closing_tile, 0)
+                    affine(closing_tile, 1, ln_w_all, ALU.mult)
             if h == 0 and 1 <= next_tile < TILES:
                 transpose_q(next_tile)
+
+        relu_and_divide(GROUPS - 1)
+        add_streams(nc.vector, GROUPS - 1)
+        mean(TILES - 1)
+        close_last(TILES - 1)

@@ -82,17 +82,26 @@ def tile_transformergraphconv_pa_kernel(tc, x, q, k, W_v, conv_w, conv_b, ln_w, 
                     in_=wv_rows[u, :, heads, :],
                 )
 
-        for a in range(PAIRS):
+        def load_x(a):
             nc.sync.dma_start(out=x_sb[:, a, :, :].rearrange("p e c -> p (e c)"), in_=x_rows[a, :, :])
-        for half in range(2):
-            load_wv(half)
-        for half in range(2):
+
+        def load_cw(half):
             rows = slice(PACK * half, PACK * half + PACK)
             nc.sync.dma_start(out=cw_sb[:, rows, :], in_=cw_rows[:, rows, :])
-        nc.sync.dma_start(out=conv_b_all[:], in_=conv_b.partition_broadcast(P))
-        for h in range(HEADS):
+
+        load_q(0)
+        for h in range(3):
             load_k(h)
         for a in range(PAIRS):
+            load_x(a)
+        load_wv(0)
+        for h in range(3, HEADS):
+            load_k(h)
+        load_wv(1)
+        for half in range(2):
+            load_cw(half)
+        nc.sync.dma_start(out=conv_b_all[:], in_=conv_b.partition_broadcast(P))
+        for a in range(1, PAIRS):
             load_q(a)
         nc.sync.dma_start(out=ln_w_all[:], in_=ln_w.partition_broadcast(P))
         nc.sync.dma_start(out=ln_b_all[:], in_=ln_b.partition_broadcast(P))
@@ -109,63 +118,81 @@ def tile_transformergraphconv_pa_kernel(tc, x, q, k, W_v, conv_w, conv_b, ln_w, 
         y_all = keep.tile([P, TILES, C_OUT], F32)
         y_sums = keep.tile([P, TILES, 2 * HALVES], F32)
 
-        def quantise_channels_last(rows_sb, codes, scales, half):
+        def leave_psum(engine, out, in_):
+            if engine == "vector":
+                nc.vector.tensor_copy(out=out, in_=in_)
+            else:
+                nc.scalar.copy(out=out, in_=in_)
+
+        grouped_rows = {}
+
+        def group_channels_last(name, rows_sb, half, pair):
             words = rows_sb.bitcast(F32)
-            grouped = stage.tile([P, PACK, P, PACK], BF16, tag="grouped", align_bytes=64)
-            grouped_words = grouped[:].bitcast(F32)
-            for pair in range(2):
-                flipped = psum_t.tile([P, 2, 2, P], F32, tag="flip")
-                for n in range(2):
-                    for u in range(2):
-                        nc.tensor.transpose(
-                            flipped[:, n, u, :],
-                            words[:, PACK * half + 2 * pair + n, P * u : P * u + P],
-                            ident_f32[:],
-                        )
-                nc.scalar.copy(
-                    out=grouped_words[:, 2 * pair : 2 * pair + 2, :, :],
-                    in_=flipped[:].rearrange("p n u r -> p n r u"),
-                )
+            if pair == 0:
+                grouped = stage.tile([P, PACK, P, PACK], BF16, tag="grouped", align_bytes=64)
+                grouped_rows[name, half] = grouped
+            grouped_words = grouped_rows[name, half][:].bitcast(F32)
+            flipped = psum_t.tile([P, 2, 2, P], F32, tag="flip")
+            for n in range(2):
+                for u in range(2):
+                    nc.tensor.transpose(
+                        flipped[:, n, u, :],
+                        words[:, PACK * half + 2 * pair + n, P * u : P * u + P],
+                        ident_f32[:],
+                    )
+            return grouped_words[:, 2 * pair : 2 * pair + 2, :, :], flipped[:].rearrange("p n u r -> p n r u")
+
+        def quantise_channels_last(name, codes, scales, half):
             cols = slice(BANK * half, BANK * half + BANK)
             nc.vector.quantize_mx(
                 out=codes[:, cols].bitcast(FP8X4),
                 scales=scales[:, cols],
-                in_=grouped[:].rearrange("p j r t -> p (j r t)"),
+                in_=grouped_rows[name, half][:].rearrange("p j r t -> p (j r t)"),
+            )
+
+        wv_grouped = {}
+
+        def group_wv(half):
+            heads = slice(HALF_HEADS * half, HALF_HEADS * half + HALF_HEADS)
+            grouped = stage.tile([P, HALF_HEADS, DH, PACK], BF16, tag="wv_grouped", align_bytes=64)
+            wv_grouped[half] = grouped
+            nc.gpsimd.tensor_scalar(
+                out=grouped[:],
+                in0=wv_sb[:, heads, :, :].rearrange("p h t d -> p h d t"),
+                scalar1=1.0,
+                scalar2=0.0,
+                op0=ALU.mult,
+                op1=ALU.add,
             )
 
         def quantise_wv(half):
-            heads = slice(HALF_HEADS * half, HALF_HEADS * half + HALF_HEADS)
             cols = slice(BANK * half, BANK * half + BANK)
-            wv_grouped = stage.tile([P, HALF_HEADS, DH, PACK], BF16, tag="grouped", align_bytes=64)
-            if half == 0:
-                nc.vector.tensor_copy(out=wv_grouped[:], in_=wv_sb[:, heads, :, :].rearrange("p h t d -> p h d t"))
-            else:
-                nc.scalar.copy(out=wv_grouped[:], in_=wv_sb[:, heads, :, :].rearrange("p h t d -> p h d t"))
             nc.vector.quantize_mx(
                 out=wv_codes[:, cols].bitcast(FP8X4),
                 scales=wv_scales[:, cols],
-                in_=wv_grouped[:].rearrange("p h d t -> p (h d t)"),
+                in_=wv_grouped[half][:].rearrange("p h d t -> p (h d t)"),
             )
 
+        proj_banks = {}
         v_grouped = {}
 
-        def values(h):
-            grouped = stage.tile([P, PASSES, DH, PACK], BF16, tag="v_grouped", align_bytes=64)
-            v_grouped[h] = grouped
-            for g in range(PASSES):
-                v_bank = psum_s.tile([P, PACK, DH], F32, tag="s")
-                for t in range(PACK):
-                    nodes = slice(P * (PACK * g + t), P * (PACK * g + t) + P)
-                    nc.tensor.matmul_mx(
-                        out=v_bank[:, t, :],
-                        lhsT=x_codes[:, nodes].bitcast(FP8X4),
-                        lhsT_scale=x_scales[:, nodes],
-                        rhs=wv_codes[:, DH * h : DH * h + DH].bitcast(FP8X4),
-                        rhs_scale=wv_scales[:, DH * h : DH * h + DH],
-                        start=True,
-                        stop=True,
-                    )
-                nc.scalar.copy(out=grouped[:, g, :, :], in_=v_bank[:].rearrange("p t d -> p d t"))
+        def values(h, g):
+            if g == 0:
+                grouped = stage.tile([P, PASSES, DH, PACK], BF16, tag="v_grouped", align_bytes=64)
+                v_grouped[h] = grouped
+            v_bank = psum_t.tile([P, PACK, DH], F32, tag="flip")
+            for t in range(PACK):
+                nodes = slice(P * (PACK * g + t), P * (PACK * g + t) + P)
+                nc.tensor.matmul_mx(
+                    out=v_bank[:, t, :],
+                    lhsT=x_codes[:, nodes].bitcast(FP8X4),
+                    lhsT_scale=x_scales[:, nodes],
+                    rhs=wv_codes[:, DH * h : DH * h + DH].bitcast(FP8X4),
+                    rhs_scale=wv_scales[:, DH * h : DH * h + DH],
+                    start=True,
+                    stop=True,
+                )
+            return v_grouped[h][:, g, :, :], v_bank[:].rearrange("p t d -> p d t")
 
         def quantise_values(h):
             nc.vector.quantize_mx(
@@ -177,7 +204,8 @@ def tile_transformergraphconv_pa_kernel(tc, x, q, k, W_v, conv_w, conv_b, ln_w, 
         def projection(tile_no, half):
             nodes = slice(P * tile_no, P * tile_no + P)
             cols = slice(BANK * half, BANK * half + BANK)
-            proj_bank = psum_s.tile([P, BANK], F32, tag="s")
+            proj_bank = psum_t.tile([P, BANK], F32, tag="flip")
+            proj_banks[tile_no, half] = proj_bank
             nc.tensor.matmul_mx(
                 out=proj_bank[:],
                 lhsT=x_codes[:, nodes].bitcast(FP8X4),
@@ -187,9 +215,12 @@ def tile_transformergraphconv_pa_kernel(tc, x, q, k, W_v, conv_w, conv_b, ln_w, 
                 start=True,
                 stop=True,
             )
+
+        def add_bias(tile_no, half):
+            cols = slice(BANK * half, BANK * half + BANK)
             nc.vector.scalar_tensor_tensor(
                 out=y_all[:, tile_no, cols],
-                in0=proj_bank[:],
+                in0=proj_banks[tile_no, half][:],
                 scalar=0.0,
                 in1=conv_b_all[:, cols],
                 op0=ALU.add,
@@ -197,22 +228,16 @@ def tile_transformergraphconv_pa_kernel(tc, x, q, k, W_v, conv_w, conv_b, ln_w, 
                 accum_out=y_sums[:, tile_no, half : half + 1],
             )
 
-        k_flipped = {}
-
         def transpose_k(h):
             flipped = psum_t.tile([P, TILES, P], BF16, tag="flip")
             for j in range(TILES):
                 nc.tensor.transpose(flipped[:, j, :], k_sb[:, h, j, :], ident_bf[:])
-            k_flipped[h] = flipped
-
-        def copy_k(h):
-            nc.scalar.copy(out=kT[:, h, :], in_=k_flipped[h][:].rearrange("d j p -> d (j p)"))
+            return kT[:, h, :], flipped[:].rearrange("d j p -> d (j p)")
 
         q_flipped = {}
         qT = {}
         s_banks = {}
         s_rows = {}
-        bank_maxima = {}
         shift = {}
         row_sums = {}
         e_rows = {}
@@ -227,66 +252,51 @@ def tile_transformergraphconv_pa_kernel(tc, x, q, k, W_v, conv_w, conv_b, ln_w, 
                 nc.tensor.transpose(flipped[:, h, :], q_sb[:, h, tile_no // 2, tile_no % 2, :], ident_bf[:])
             q_flipped[tile_no] = flipped
 
-        def copy_q(tile_no):
+        def copy_q(engine, tile_no):
             q_cols = work.tile([P, HEADS, P], BF16, tag="qT", bufs=2)
-            nc.scalar.copy(out=q_cols[:], in_=q_flipped[tile_no][:])
+            leave_psum(engine, out=q_cols[:], in_=q_flipped[tile_no][:])
             qT[tile_no] = q_cols
 
-        def scores(unit):
+        def scores(unit, g):
             tile_no, h = divmod(unit, HEADS)
-            banks = []
-            for g in range(PASSES):
-                s_bank = psum_s.tile([P, BANK], F32, tag="s")
-                nc.tensor.matmul(
-                    out=s_bank[:],
-                    lhsT=qT[tile_no][:, h, :],
-                    rhs=kT[:, h, BANK * g : BANK * g + BANK],
-                    start=True,
-                    stop=True,
-                )
-                banks.append(s_bank)
-            s_banks[unit] = banks
-
-        def scale_and_max(unit):
-            scaled = work.tile([P, NODES], F32, tag="scaled", bufs=4)
-            bank_max = small.tile([P, PASSES], F32, tag="bank_max")
-            for g in range(PASSES):
-                nc.vector.tensor_scalar(
-                    out=scaled[:, BANK * g : BANK * g + BANK],
-                    in0=s_banks[unit][g][:],
-                    scalar1=SCALE,
-                    scalar2=None,
-                    op0=ALU.mult,
-                    op1=ALU.max,
-                    accum_out=bank_max[:, g : g + 1],
-                )
-            s_rows[unit] = scaled
-            bank_maxima[unit] = bank_max
-
-        def row_max(unit):
-            minus_max = small.tile([P, 1], F32, tag="shift")
-            nc.vector.tensor_scalar(
-                out=minus_max[:],
-                in0=bank_maxima[unit][:, 0:1],
-                scalar1=bank_maxima[unit][:, 1:2],
-                scalar2=-1.0,
-                op0=ALU.max,
-                op1=ALU.mult,
+            s_bank = psum_s.tile([P, BANK], F32, tag="s")
+            s_banks[unit, g] = s_bank
+            nc.tensor.matmul(
+                out=s_bank[:],
+                lhsT=qT[tile_no][:, h, :],
+                rhs=kT[:, h, BANK * g : BANK * g + BANK],
+                start=True,
+                stop=True,
             )
-            shift[unit] = minus_max
+
+        def scale_and_min(unit, g):
+            if g == 0:
+                scaled = work.tile([P, NODES], F32, tag="scaled", bufs=4)
+                s_rows[unit] = scaled
+            minimum = small.tile([P, 1], F32, tag="minimum", bufs=8)
+            nc.vector.tensor_scalar(
+                out=s_rows[unit][:, BANK * g : BANK * g + BANK],
+                in0=s_banks[unit, g][:],
+                scalar1=-SCALE,
+                scalar2=None if g == 0 else shift[unit][:, 0:1],
+                op0=ALU.mult,
+                op1=ALU.min,
+                accum_out=minimum[:, 0:1],
+            )
+            shift[unit] = minimum
 
         def exponentials(unit):
             tile_no, h = divmod(unit, HEADS)
             if h == 0:
                 sums = small.tile([P, HEADS], F32, tag="row_sums", bufs=3)
                 row_sums[tile_no] = sums
-            e_sb = work.tile([P, NODES], BF16, tag="e_sb")
+            e_sb = work.tile([P, NODES], BF16, tag="e_sb", bufs=4)
             nc.scalar.activation(
                 out=e_sb[:],
                 in_=s_rows[unit][:],
                 func=ACT.Exp,
                 bias=shift[unit][:, 0:1],
-                scale=1.0,
+                scale=-1.0,
                 accum_out=row_sums[tile_no][:, h : h + 1],
             )
             e_rows[unit] = e_sb
@@ -300,12 +310,13 @@ def tile_transformergraphconv_pa_kernel(tc, x, q, k, W_v, conv_w, conv_b, ln_w, 
                     nc.tensor.transpose(flipped[:, g, u, :], e_words[:, first : first + P], ident_f32[:])
             e_flipped[unit] = flipped
 
-        def regroup(unit):
+        def regroup(engine, unit):
             group, place = divmod(unit, HALF_HEADS)
             if place == 0:
                 grouped = work.tile([P, HALF_HEADS, PASSES, P, PACK], BF16, tag="e_grouped", bufs=2, align_bytes=64)
                 e_grouped[group] = grouped
-            nc.scalar.copy(
+            leave_psum(
+                engine,
                 out=e_grouped[group][:].bitcast(F32)[:, place, :, :, :],
                 in_=e_flipped[unit][:].rearrange("p g u r -> p g r u"),
             )
@@ -475,44 +486,88 @@ def tile_transformergraphconv_pa_kernel(tc, x, q, k, W_v, conv_w, conv_b, ln_w, 
                 finish(tile_no, half, centred[half])
                 store(tile_no, half)
 
-        for half in range(2):
-            quantise_channels_last(x_sb[:].rearrange("p a e c -> p (a e) c"), x_codes[:], x_scales[:], half)
-        for half in range(2):
-            quantise_wv(half)
-        for half in range(2):
-            quantise_channels_last(cw_sb[:], cw_codes[:], cw_scales[:], half)
-        for n in range(HEADS):
-            values(n)
-            for half in range(HALVES):
-                projection(n, half)
-            quantise_values(n)
-            transpose_k(n)
-            copy_k(n)
-        transpose_q(0)
-        copy_q(0)
+        x_tiles = x_sb[:].rearrange("p a e c -> p (a e) c")
 
-        LAG = 4
+        def fill_k(h):
+            return lambda: transpose_k(h), None
+
+        def fill_x(half, pair):
+            done = (lambda: quantise_channels_last("x", x_codes, x_scales, half)) if pair else None
+            return lambda: group_channels_last("x", x_tiles, half, pair), done
+
+        def fill_cw(half, pair):
+            done = (lambda: quantise_channels_last("cw", cw_codes, cw_scales, half)) if pair else None
+            return lambda: group_channels_last("cw", cw_sb[:], half, pair), done
+
+        def fill_v(h, g):
+            done = (lambda: quantise_values(h)) if g else None
+            return lambda: values(h, g), done
+
+        prep = [fill_k(3)] + [fill_x(half, pair) for half in range(2) for pair in range(2)] + [fill_k(4), fill_k(5)]
+        for h in range(2):
+            prep += [fill_v(h, 0), fill_v(h, 1), fill_k(h + 6)]
+        prep += [fill_v(h, g) for h in range(2, 4) for g in range(PASSES)]
+        prep += [fill_cw(half, pair) for half in range(2) for pair in range(2)]
+        prep += [fill_v(h, g) for h in range(4, HEADS) for g in range(PASSES)]
+        DRAIN = ("scalar", "vector")
+        filled = []
+
+        def prepare(n):
+            if 0 <= n - 2 < len(prep) and prep[n - 2][1]:
+                prep[n - 2][1]()
+            if 0 <= n < len(prep):
+                filled.append(prep[n][0]())
+            if 0 <= n - 1 < len(prep):
+                target, source = filled[n - 1]
+                leave_psum(DRAIN[(n - 1) % len(DRAIN)], target, source)
+
+        FLIP = 3
+        LAG = FLIP + 2
         CLOSING_LAG = HALF_HEADS - 1 + LAG + 2
-        scores(0)
-        scores(1)
+        transpose_q(0)
+        copy_q("scalar", 0)
+        for h in range(3):
+            target, source = transpose_k(h)
+            leave_psum("vector" if h % 2 == 0 else "scalar", target, source)
+        scores(0, 0)
+        scores(0, 1)
+        scores(1, 0)
+        prepare(0)
         for i in range(UNITS + LAG + 2):
             next_tile, h = divmod(i + 5, HEADS)
             group, place = divmod(i - LAG, HALF_HEADS)
             closing_group, closing_step = divmod(i - CLOSING_LAG, HALF_HEADS)
             closing_tile, closing_half = divmod(closing_group, HALVES)
             closing = 0 <= closing_group < GROUPS - 1
+            proj_tile, proj_step = divmod(i - 7, HEADS)
 
+            if 0 <= i - FLIP < UNITS:
+                flip(i - FLIP)
             if i < UNITS:
-                scale_and_max(i)
+                scale_and_min(i, 0)
+            if 0 <= proj_tile < TILES and proj_step in (1, 2):
+                add_bias(proj_tile, proj_step - 1)
+            if i in (2, 3):
+                quantise_wv(i - 2)
+            prepare(3 * i + 1)
             if i + 2 < UNITS:
-                scores(i + 2)
+                scores(i + 2, 0)
             if 0 <= i - 1 < UNITS:
-                exponentials(i - 1)
-                flip(i - 1)
-            if 0 <= i - 3 < UNITS:
-                regroup(i - 3)
+                scale_and_min(i - 1, 1)
+            prepare(3 * i + 2)
+            if i + 1 < UNITS:
+                scores(i + 1, 1)
+            if 0 <= i - 2 < UNITS:
+                exponentials(i - 2)
+            if 0 <= i - FLIP - 1 < UNITS:
+                regroup("scalar", i - FLIP - 1)
+            prepare(3 * i + 3)
+            if i in (0, 1):
+                group_wv(i)
             if h == 1 and 1 <= next_tile < TILES:
-                copy_q(next_tile)
+                copy_q("scalar", next_tile)
+            if 0 <= proj_tile < TILES and proj_step in (0, 1):
+                projection(proj_tile, proj_step)
 
             if 0 <= group < GROUPS and place == HALF_HEADS - 1:
                 invert_row_sums(group)
@@ -520,8 +575,6 @@ def tile_transformergraphconv_pa_kernel(tc, x, q, k, W_v, conv_w, conv_b, ln_w, 
                 quantise(group, 0, HALF_HEADS)
             if group == GROUPS - 1:
                 quantise(group, place, 1)
-            if i < UNITS:
-                row_max(i)
             if 0 <= group < GROUPS - 1 and place == HALF_HEADS - 1:
                 attend(group, 0, HALF_HEADS)
             if group == GROUPS - 1:

@@ -41,9 +41,11 @@ def tile_transformergraphconv_pa_kernel(tc, x, q, k, W_v, conv_w, conv_b, ln_w, 
         stage = ctx.enter_context(tc.tile_pool(name="stage", bufs=2))
         work = ctx.enter_context(tc.tile_pool(name="work", bufs=3))
         small = ctx.enter_context(tc.tile_pool(name="small", bufs=4))
-        psum_s = ctx.enter_context(tc.psum_pool(name="psum_s", bufs=4))
-        psum_t = ctx.enter_context(tc.psum_pool(name="psum_t", bufs=3))
-        psum_o = ctx.enter_context(tc.psum_pool(name="psum_o", bufs=1))
+        psum = ctx.enter_context(tc.psum_pool(name="psum", bufs=1))
+
+        def bank(number, shape, dtype):
+            whole = psum.tile(shape, dtype, tag="bank%d" % number)
+            return whole
 
         ident_f32 = keep.tile([P, P], F32)
         make_identity(nc, ident_f32[:])
@@ -52,57 +54,69 @@ def tile_transformergraphconv_pa_kernel(tc, x, q, k, W_v, conv_w, conv_b, ln_w, 
         minus_half = keep.tile([P, 1], F32)
         nc.gpsimd.memset(minus_half[:], -0.5)
 
-        x_sb = keep.tile([P, PAIRS, 2, C_IN], BF16)
-        x_rows = x.rearrange("b (a p e) c -> (b a) p (e c)", p=P, e=2)
-        wv_sb = keep.tile([P, HEADS, PACK, DH], BF16)
+        x_rows = x.rearrange("b (p o) c -> (b p) o c", o=TILES)
+        x_sb = []
         wv_rows = W_v.rearrange("h (u p e) d -> u p h (e d)", u=2, e=2)
-        cw_sb = keep.tile([P, TILES, C_IN], BF16)
+        wv_sb = []
         cw_rows = conv_w.rearrange("(j p) c -> p j c", p=P)
-        k_sb = keep.tile([P, HEADS, TILES, DH], BF16)
-        k_rows = k.rearrange("b h (j p) d -> (b h) p j d", p=P)
-        q_sb = keep.tile([P, HEADS, PAIRS, 2, DH], BF16)
-        q_rows = q.rearrange("b h (a p e) d -> a p (b h) (e d)", p=P, e=2)
+        cw_sb = []
+        k_rows = k.rearrange("b h (s p f) d -> (b h) p s (f d)", s=2, f=4)
+        k_sb = []
+        q_rows = q.rearrange("b h (p o) d -> p (b h) (o d)", o=TILES)
+        q_sb = {}
         conv_b_all = keep.tile([P, C_OUT], BF16)
         ln_w_all = keep.tile([P, C_OUT], BF16)
         ln_b_all = keep.tile([P, C_OUT], BF16)
 
-        def load_k(h):
-            nc.sync.dma_start(out=k_sb[:, h, :, :], in_=k_rows[h, :, :, :])
-
-        def load_q(a):
-            nc.sync.dma_start(
-                out=q_sb[:, :, a, :, :].rearrange("p h e d -> p h (e d)"), in_=q_rows[a, :, :, :]
-            )
+        def load_x(pair):
+            rows = keep.tile([P, 2, C_IN], BF16, tag="x_rows%d" % pair)
+            nc.sync.dma_start(out=rows[:], in_=x_rows[:, 2 * pair : 2 * pair + 2, :])
+            x_sb.append(rows)
 
         def load_wv(half):
             heads = slice(HALF_HEADS * half, HALF_HEADS * half + HALF_HEADS)
+            rows = keep.tile([P, HALF_HEADS, PACK, DH], BF16, tag="wv_rows%d" % half)
             for u in range(2):
                 nc.sync.dma_start(
-                    out=wv_sb[:, heads, 2 * u : 2 * u + 2, :].rearrange("p h e d -> p h (e d)"),
+                    out=rows[:, :, 2 * u : 2 * u + 2, :].rearrange("p h e d -> p h (e d)"),
                     in_=wv_rows[u, :, heads, :],
                 )
-
-        def load_x(a):
-            nc.sync.dma_start(out=x_sb[:, a, :, :].rearrange("p e c -> p (e c)"), in_=x_rows[a, :, :])
+            wv_sb.append(rows)
 
         def load_cw(half):
-            rows = slice(PACK * half, PACK * half + PACK)
-            nc.sync.dma_start(out=cw_sb[:, rows, :], in_=cw_rows[:, rows, :])
+            rows = keep.tile([P, PACK, C_IN], BF16, tag="cw_rows%d" % half)
+            nc.sync.dma_start(out=rows[:], in_=cw_rows[:, PACK * half : PACK * half + PACK, :])
+            cw_sb.append(rows)
 
-        load_q(0)
-        for h in range(3):
+        def load_k(h):
+            rows = keep.tile([P, 2, 4, DH], BF16, tag="k_rows%d" % h)
+            nc.sync.dma_start(out=rows[:].rearrange("p s f d -> p s (f d)"), in_=k_rows[h, :, :, :])
+            k_sb.append(rows)
+
+        def load_q(head_half, tile_half):
+            heads = slice(HALF_HEADS * head_half, HALF_HEADS * head_half + HALF_HEADS)
+            columns = slice(PACK * DH * tile_half, PACK * DH * (tile_half + 1))
+            rows = keep.tile([P, HALF_HEADS, PACK, DH], BF16, tag="q_rows%d%d" % (head_half, tile_half))
+            nc.sync.dma_start(out=rows[:].rearrange("p h o d -> p h (o d)"), in_=q_rows[:, heads, columns])
+            q_sb[head_half, tile_half] = rows
+
+        load_q(0, 0)
+        for h in range(4):
             load_k(h)
-        for a in range(PAIRS):
-            load_x(a)
+        for pair in range(PAIRS):
+            load_x(pair)
+        load_q(1, 0)
+        load_k(4)
         load_wv(0)
-        for h in range(3, HEADS):
-            load_k(h)
+        load_k(5)
         load_wv(1)
+        load_k(6)
+        load_k(7)
         for half in range(2):
             load_cw(half)
         nc.sync.dma_start(out=conv_b_all[:], in_=conv_b.partition_broadcast(P))
-        for a in range(1, PAIRS):
-            load_q(a)
+        for head_half in range(2):
+            load_q(head_half, 1)
         nc.sync.dma_start(out=ln_w_all[:], in_=ln_w.partition_broadcast(P))
         nc.sync.dma_start(out=ln_b_all[:], in_=ln_b.partition_broadcast(P))
 
@@ -126,21 +140,18 @@ def tile_transformergraphconv_pa_kernel(tc, x, q, k, W_v, conv_w, conv_b, ln_w, 
 
         grouped_rows = {}
 
-        def group_channels_last(name, rows_sb, half, pair):
-            words = rows_sb.bitcast(F32)
+        def group_channels_last(number, name, pair_rows, half, pair):
+            words = pair_rows.bitcast(F32)
             if pair == 0:
                 grouped = stage.tile([P, PACK, P, PACK], BF16, tag="grouped", align_bytes=64)
                 grouped_rows[name, half] = grouped
             grouped_words = grouped_rows[name, half][:].bitcast(F32)
-            flipped = psum_t.tile([P, 2, 2, P], F32, tag="flip")
+            flipped = bank(number, [P, 2, 2, P], F32)
             for n in range(2):
                 for u in range(2):
-                    nc.tensor.transpose(
-                        flipped[:, n, u, :],
-                        words[:, PACK * half + 2 * pair + n, P * u : P * u + P],
-                        ident_f32[:],
-                    )
-            return grouped_words[:, 2 * pair : 2 * pair + 2, :, :], flipped[:].rearrange("p n u r -> p n r u")
+                    nc.tensor.transpose(flipped[:, n, u, :], words[:, n, P * u : P * u + P], ident_f32[:])
+            target = grouped_words[:, 2 * pair : 2 * pair + 2, :, :]
+            return lambda engine: leave_psum(engine, target, flipped[:].rearrange("p n u r -> p n r u"))
 
         def quantise_channels_last(name, codes, scales, half):
             cols = slice(BANK * half, BANK * half + BANK)
@@ -153,12 +164,11 @@ def tile_transformergraphconv_pa_kernel(tc, x, q, k, W_v, conv_w, conv_b, ln_w, 
         wv_grouped = {}
 
         def group_wv(half):
-            heads = slice(HALF_HEADS * half, HALF_HEADS * half + HALF_HEADS)
             grouped = stage.tile([P, HALF_HEADS, DH, PACK], BF16, tag="wv_grouped", align_bytes=64)
             wv_grouped[half] = grouped
             nc.gpsimd.tensor_scalar(
                 out=grouped[:],
-                in0=wv_sb[:, heads, :, :].rearrange("p h t d -> p h d t"),
+                in0=wv_sb[half][:].rearrange("p h t d -> p h d t"),
                 scalar1=1.0,
                 scalar2=0.0,
                 op0=ALU.mult,
@@ -173,16 +183,17 @@ def tile_transformergraphconv_pa_kernel(tc, x, q, k, W_v, conv_w, conv_b, ln_w, 
                 in_=wv_grouped[half][:].rearrange("p h d t -> p (h d t)"),
             )
 
-        proj_banks = {}
         v_grouped = {}
 
-        def values(h, g):
+        def values(number, h, g):
             if g == 0:
                 grouped = stage.tile([P, PASSES, DH, PACK], BF16, tag="v_grouped", align_bytes=64)
                 v_grouped[h] = grouped
-            v_bank = psum_t.tile([P, PACK, DH], F32, tag="flip")
+            v_bank = bank(number, [P, PACK, DH], F32)
             for t in range(PACK):
-                nodes = slice(P * (PACK * g + t), P * (PACK * g + t) + P)
+                u, e = divmod(t, 2)
+                first = P * (4 * e + 2 * g + u)
+                nodes = slice(first, first + P)
                 nc.tensor.matmul_mx(
                     out=v_bank[:, t, :],
                     lhsT=x_codes[:, nodes].bitcast(FP8X4),
@@ -192,7 +203,8 @@ def tile_transformergraphconv_pa_kernel(tc, x, q, k, W_v, conv_w, conv_b, ln_w, 
                     start=True,
                     stop=True,
                 )
-            return v_grouped[h][:, g, :, :], v_bank[:].rearrange("p t d -> p d t")
+            target = v_grouped[h][:, g, :, :]
+            return lambda engine: leave_psum(engine, target, v_bank[:].rearrange("p t d -> p d t"))
 
         def quantise_values(h):
             nc.vector.quantize_mx(
@@ -201,11 +213,10 @@ def tile_transformergraphconv_pa_kernel(tc, x, q, k, W_v, conv_w, conv_b, ln_w, 
                 in_=v_grouped[h][:].rearrange("p g d t -> p (g d t)"),
             )
 
-        def projection(tile_no, half):
+        def projection(number, tile_no, half):
             nodes = slice(P * tile_no, P * tile_no + P)
             cols = slice(BANK * half, BANK * half + BANK)
-            proj_bank = psum_t.tile([P, BANK], F32, tag="flip")
-            proj_banks[tile_no, half] = proj_bank
+            proj_bank = bank(number, [P, BANK], F32)
             nc.tensor.matmul_mx(
                 out=proj_bank[:],
                 lhsT=x_codes[:, nodes].bitcast(FP8X4),
@@ -215,12 +226,9 @@ def tile_transformergraphconv_pa_kernel(tc, x, q, k, W_v, conv_w, conv_b, ln_w, 
                 start=True,
                 stop=True,
             )
-
-        def add_bias(tile_no, half):
-            cols = slice(BANK * half, BANK * half + BANK)
-            nc.vector.scalar_tensor_tensor(
+            return lambda engine: nc.vector.scalar_tensor_tensor(
                 out=y_all[:, tile_no, cols],
-                in0=proj_banks[tile_no, half][:],
+                in0=proj_bank[:],
                 scalar=0.0,
                 in1=conv_b_all[:, cols],
                 op0=ALU.add,
@@ -228,13 +236,14 @@ def tile_transformergraphconv_pa_kernel(tc, x, q, k, W_v, conv_w, conv_b, ln_w, 
                 accum_out=y_sums[:, tile_no, half : half + 1],
             )
 
-        def transpose_k(h):
-            flipped = psum_t.tile([P, TILES, P], BF16, tag="flip")
-            for j in range(TILES):
-                nc.tensor.transpose(flipped[:, j, :], k_sb[:, h, j, :], ident_bf[:])
-            return kT[:, h, :], flipped[:].rearrange("d j p -> d (j p)")
+        def transpose_k(number, h):
+            flipped = bank(number, [P, PASSES, 2, 2, P], BF16)
+            for g in range(PASSES):
+                for u in range(2):
+                    for s in range(2):
+                        nc.tensor.transpose(flipped[:, g, u, s, :], k_sb[h][:, s, 2 * g + u, :], ident_bf[:])
+            return lambda engine: leave_psum(engine, kT[:, h, :], flipped[:].rearrange("d g u s p -> d (g u s p)"))
 
-        q_flipped = {}
         qT = {}
         s_banks = {}
         s_rows = {}
@@ -246,20 +255,22 @@ def tile_transformergraphconv_pa_kernel(tc, x, q, k, W_v, conv_w, conv_b, ln_w, 
         e_packed = {}
         o_banks = {}
 
-        def transpose_q(tile_no):
-            flipped = psum_t.tile([P, HEADS, P], BF16, tag="flip")
-            for h in range(HEADS):
-                nc.tensor.transpose(flipped[:, h, :], q_sb[:, h, tile_no // 2, tile_no % 2, :], ident_bf[:])
-            q_flipped[tile_no] = flipped
-
-        def copy_q(engine, tile_no):
-            q_cols = work.tile([P, HEADS, P], BF16, tag="qT", bufs=2)
-            leave_psum(engine, out=q_cols[:], in_=q_flipped[tile_no][:])
-            qT[tile_no] = q_cols
+        def transpose_q(number, tile_no, half):
+            flipped = bank(number, [P, HALF_HEADS, P], BF16)
+            for n in range(HALF_HEADS):
+                nc.tensor.transpose(flipped[:, n, :], q_sb[half, tile_no // PACK][:, n, tile_no % PACK, :], ident_bf[:])
+            if half == 0:
+                q_cols = work.tile([P, HEADS, P], BF16, tag="qT", bufs=2)
+                qT[tile_no] = q_cols
+            heads = slice(HALF_HEADS * half, HALF_HEADS * half + HALF_HEADS)
+            return lambda engine: leave_psum(engine, qT[tile_no][:, heads, :], flipped[:])
 
         def scores(unit, g):
             tile_no, h = divmod(unit, HEADS)
-            s_bank = psum_s.tile([P, BANK], F32, tag="s")
+            place = 2 * unit + 3 * g
+            late = place - (2 * PREP_ROUNDS + 3)
+            number = place % 3 if late < 0 else (3, *[(2 * PREP_ROUNDS + n) % 3 for n in range(3)])[late % 4]
+            s_bank = bank(number, [P, BANK], F32)
             s_banks[unit, g] = s_bank
             nc.tensor.matmul(
                 out=s_bank[:],
@@ -303,7 +314,7 @@ def tile_transformergraphconv_pa_kernel(tc, x, q, k, W_v, conv_w, conv_b, ln_w, 
 
         def flip(unit):
             e_words = e_rows[unit][:].bitcast(F32)
-            flipped = psum_t.tile([P, PASSES, 2, P], F32, tag="flip")
+            flipped = bank(4 + unit % 2, [P, PASSES, 2, P], F32)
             for g in range(PASSES):
                 for u in range(2):
                     first = P * (2 * g + u)
@@ -336,7 +347,7 @@ def tile_transformergraphconv_pa_kernel(tc, x, q, k, W_v, conv_w, conv_b, ln_w, 
 
         def attend(group, first, count):
             if first == 0:
-                o_bank = psum_o.tile([P, HALF_HEADS, DH], F32, tag="o")
+                o_bank = bank(6, [P, HALF_HEADS, DH], F32)
                 o_banks[group] = o_bank
             o_bank = o_banks[group]
             e_codes, e_scales = e_packed[group]
@@ -358,7 +369,7 @@ def tile_transformergraphconv_pa_kernel(tc, x, q, k, W_v, conv_w, conv_b, ln_w, 
         minus_mean = {}
         square_sums = {}
         rstd = {}
-        out_rows = out.rearrange("b (a p e) c -> (b a) e p c", p=P, e=2)
+        out_rows = out.rearrange("b (p o) c -> (b o) p c", o=TILES)
 
         def half_cols(half):
             return slice(BANK * half, BANK * half + BANK)
@@ -452,7 +463,7 @@ def tile_transformergraphconv_pa_kernel(tc, x, q, k, W_v, conv_w, conv_b, ln_w, 
 
         def store(tile_no, half):
             cols = half_cols(half)
-            nc.sync.dma_start(out=out_rows[tile_no // 2, tile_no % 2, :, cols], in_=y_all[:, tile_no, cols])
+            nc.sync.dma_start(out=out_rows[tile_no, :, cols], in_=y_all[:, tile_no, cols])
 
         def centre(tile_no, half):
             cols = half_cols(half)
@@ -486,29 +497,38 @@ def tile_transformergraphconv_pa_kernel(tc, x, q, k, W_v, conv_w, conv_b, ln_w, 
                 finish(tile_no, half, centred[half])
                 store(tile_no, half)
 
-        x_tiles = x_sb[:].rearrange("p a e c -> p (a e) c")
-
         def fill_k(h):
-            return lambda: transpose_k(h), None
+            return lambda number: transpose_k(number, h), None
 
         def fill_x(half, pair):
             done = (lambda: quantise_channels_last("x", x_codes, x_scales, half)) if pair else None
-            return lambda: group_channels_last("x", x_tiles, half, pair), done
+            return lambda number: group_channels_last(number, "x", x_sb[2 * half + pair][:], half, pair), done
 
         def fill_cw(half, pair):
             done = (lambda: quantise_channels_last("cw", cw_codes, cw_scales, half)) if pair else None
-            return lambda: group_channels_last("cw", cw_sb[:], half, pair), done
+            rows = slice(2 * pair, 2 * pair + 2)
+            return lambda number: group_channels_last(number, "cw", cw_sb[half][:, rows, :], half, pair), done
 
         def fill_v(h, g):
             done = (lambda: quantise_values(h)) if g else None
-            return lambda: values(h, g), done
+            return lambda number: values(number, h, g), done
 
-        prep = [fill_k(3)] + [fill_x(half, pair) for half in range(2) for pair in range(2)] + [fill_k(4), fill_k(5)]
-        for h in range(2):
-            prep += [fill_v(h, 0), fill_v(h, 1), fill_k(h + 6)]
-        prep += [fill_v(h, g) for h in range(2, 4) for g in range(PASSES)]
-        prep += [fill_cw(half, pair) for half in range(2) for pair in range(2)]
-        prep += [fill_v(h, g) for h in range(4, HEADS) for g in range(PASSES)]
+        def fill_q(tile_no, half):
+            return lambda number: transpose_q(number, tile_no, half), None
+
+        def fill_projection(tile_no, half):
+            return lambda number: projection(number, tile_no, half), None
+
+        def fill_vs(h):
+            return [fill_v(h, 0), fill_v(h, 1)]
+
+        halves = [(half, pair) for half in range(2) for pair in range(2)]
+        prep = [fill_x(half, pair) for half, pair in halves] + [fill_q(0, 1), fill_k(4), fill_k(5)]
+        prep += fill_vs(0) + [fill_k(6)] + fill_vs(1) + [fill_k(7), fill_q(1, 0)] + fill_vs(2) + fill_vs(3)
+        prep += [fill_cw(half, pair) for half, pair in halves]
+        prep += fill_vs(4) + [fill_projection(0, 0)] + fill_vs(5) + [fill_q(1, 1)] + fill_vs(6) + fill_vs(7)
+        prep += [fill_projection(0, 1)]
+        PREP_BANKS = (7, 3)
         DRAIN = ("scalar", "vector")
         filled = []
 
@@ -516,46 +536,45 @@ def tile_transformergraphconv_pa_kernel(tc, x, q, k, W_v, conv_w, conv_b, ln_w, 
             if 0 <= n - 2 < len(prep) and prep[n - 2][1]:
                 prep[n - 2][1]()
             if 0 <= n < len(prep):
-                filled.append(prep[n][0]())
+                filled.append(prep[n][0](PREP_BANKS[n % 2]))
             if 0 <= n - 1 < len(prep):
-                target, source = filled[n - 1]
-                leave_psum(DRAIN[(n - 1) % len(DRAIN)], target, source)
+                filled[n - 1](DRAIN[(n - 1) % 2])
 
         FLIP = 3
         LAG = FLIP + 2
-        CLOSING_LAG = HALF_HEADS - 1 + LAG + 2
-        transpose_q(0)
-        copy_q("scalar", 0)
-        for h in range(3):
-            target, source = transpose_k(h)
-            leave_psum("vector" if h % 2 == 0 else "scalar", target, source)
+        PREP_ROUNDS = 11
+        first = [transpose_q(7, 0, 0)] + [transpose_k(3 + h, h) for h in range(4)]
+        for n, copy in enumerate(first):
+            copy(DRAIN[n % 2])
+        late_copies = []
         scores(0, 0)
-        scores(0, 1)
         scores(1, 0)
         prepare(0)
-        for i in range(UNITS + LAG + 2):
-            next_tile, h = divmod(i + 5, HEADS)
-            group, place = divmod(i - LAG, HALF_HEADS)
-            closing_group, closing_step = divmod(i - CLOSING_LAG, HALF_HEADS)
-            closing_tile, closing_half = divmod(closing_group, HALVES)
-            closing = 0 <= closing_group < GROUPS - 1
-            proj_tile, proj_step = divmod(i - 7, HEADS)
+        for i in range(UNITS + LAG):
+            group, step = divmod(i - LAG - HALF_HEADS + 1, HALF_HEADS)
+            group_runs = 0 <= group < GROUPS - 1
+            closing_tile, closing_half = divmod(group, HALVES)
+            place = i - LAG - HALF_HEADS * (GROUPS - 1)
 
             if 0 <= i - FLIP < UNITS:
                 flip(i - FLIP)
             if i < UNITS:
                 scale_and_min(i, 0)
-            if 0 <= proj_tile < TILES and proj_step in (1, 2):
-                add_bias(proj_tile, proj_step - 1)
             if i in (2, 3):
                 quantise_wv(i - 2)
             prepare(3 * i + 1)
-            if i + 2 < UNITS:
+            if i <= PREP_ROUNDS:
+                scores(i, 1)
+            if PREP_ROUNDS <= i < UNITS - 2:
                 scores(i + 2, 0)
+            if group_runs and step == 1:
+                attend(group, 2, 2)
             if 0 <= i - 1 < UNITS:
                 scale_and_min(i - 1, 1)
             prepare(3 * i + 2)
-            if i + 1 < UNITS:
+            if i < PREP_ROUNDS:
+                scores(i + 2, 0)
+            if PREP_ROUNDS <= i < UNITS - 1:
                 scores(i + 1, 1)
             if 0 <= i - 2 < UNITS:
                 exponentials(i - 2)
@@ -564,42 +583,49 @@ def tile_transformergraphconv_pa_kernel(tc, x, q, k, W_v, conv_w, conv_b, ln_w, 
             prepare(3 * i + 3)
             if i in (0, 1):
                 group_wv(i)
-            if h == 1 and 1 <= next_tile < TILES:
-                copy_q("scalar", next_tile)
-            if 0 <= proj_tile < TILES and proj_step in (0, 1):
-                projection(proj_tile, proj_step)
 
-            if 0 <= group < GROUPS and place == HALF_HEADS - 1:
-                invert_row_sums(group)
-            if 0 <= group < GROUPS - 1 and place == HALF_HEADS - 1:
-                quantise(group, 0, HALF_HEADS)
-            if group == GROUPS - 1:
-                quantise(group, place, 1)
-            if 0 <= group < GROUPS - 1 and place == HALF_HEADS - 1:
-                attend(group, 0, HALF_HEADS)
-            if group == GROUPS - 1:
-                attend(group, place, 1)
+            for copy in late_copies:
+                copy("scalar")
+            late_copies.clear()
+            q_tile, q_step = divmod(i + 4, HEADS)
+            if 2 <= q_tile < TILES and q_step in (0, 4):
+                late_copies.append(transpose_q(PREP_BANKS[0], q_tile, q_step // 4))
+            proj_tile, proj_step = divmod(i - 7, HEADS)
+            if 1 <= proj_tile < TILES and proj_step in (0, 2):
+                late_copies.append(projection(PREP_BANKS[0], proj_tile, proj_step // 2))
 
-            if closing and closing_step == 0:
-                relu_and_divide(closing_group)
-                add_streams(nc.gpsimd, closing_group)
+            if group_runs and step == 2:
+                relu_and_divide(group)
+                add_streams(nc.gpsimd, group)
                 if closing_half == 0 and closing_tile >= 1:
                     affine(closing_tile - 1, 1, ln_b_all, ALU.add)
                     store(closing_tile - 1, 1)
-            if closing and closing_half == HALVES - 1:
-                if closing_step == 1:
-                    mean(closing_tile)
-                if closing_step == 2:
+            if 0 <= group < GROUPS and step == 0:
+                invert_row_sums(group)
+            if group_runs and step == 0:
+                quantise(group, 0, HALF_HEADS)
+                attend(group, 0, 2)
+            if place == 1:
+                quantise(GROUPS - 1, 0, 2)
+                attend(GROUPS - 1, 0, 2)
+            if place in (2, 3):
+                quantise(GROUPS - 1, place, 1)
+                attend(GROUPS - 1, place, 1)
+
+            previous = group - 1
+            closing_tile, closing_half = divmod(previous, HALVES)
+            if 0 <= previous < GROUPS - 1 and closing_half == HALVES - 1:
+                if step == 0:
                     squares(closing_tile)
                     deviation(closing_tile)
                     normalise(closing_tile)
-                if closing_step == 3:
+                if step == 1:
                     affine(closing_tile, 0, ln_w_all, ALU.mult)
                     affine(closing_tile, 0, ln_b_all, ALU.add)
                     store(closing_tile, 0)
                     affine(closing_tile, 1, ln_w_all, ALU.mult)
-            if h == 0 and 1 <= next_tile < TILES:
-                transpose_q(next_tile)
+            if group_runs and group % HALVES == HALVES - 1 and step == 3:
+                mean(group // HALVES)
 
         relu_and_divide(GROUPS - 1)
         add_streams(nc.vector, GROUPS - 1)

@@ -100,23 +100,18 @@ def tile_transformergraphconv_pa_kernel(tc, x, q, k, W_v, conv_w, conv_b, ln_w, 
             nc.sync.dma_start(out=rows[:].rearrange("p h o d -> p h (o d)"), in_=q_rows[:, heads, columns])
             q_sb[head_half, tile_half] = rows
 
-        load_q(0, 0)
-        for h in range(4):
-            load_k(h)
         for pair in range(PAIRS):
             load_x(pair)
-        load_q(1, 0)
-        load_k(4)
-        load_wv(0)
-        load_k(5)
-        load_wv(1)
-        load_k(6)
-        load_k(7)
+        for half in range(2):
+            load_wv(half)
+        for h in range(HEADS):
+            load_k(h)
         for half in range(2):
             load_cw(half)
         nc.sync.dma_start(out=conv_b_all[:], in_=conv_b.partition_broadcast(P))
-        for head_half in range(2):
-            load_q(head_half, 1)
+        for tile_half in range(2):
+            for head_half in range(2):
+                load_q(head_half, tile_half)
         nc.sync.dma_start(out=ln_w_all[:], in_=ln_w.partition_broadcast(P))
         nc.sync.dma_start(out=ln_b_all[:], in_=ln_b.partition_broadcast(P))
 
@@ -166,14 +161,7 @@ def tile_transformergraphconv_pa_kernel(tc, x, q, k, W_v, conv_w, conv_b, ln_w, 
         def group_wv(half):
             grouped = stage.tile([P, HALF_HEADS, DH, PACK], BF16, tag="wv_grouped", align_bytes=64)
             wv_grouped[half] = grouped
-            nc.gpsimd.tensor_scalar(
-                out=grouped[:],
-                in0=wv_sb[half][:].rearrange("p h t d -> p h d t"),
-                scalar1=1.0,
-                scalar2=0.0,
-                op0=ALU.mult,
-                op1=ALU.add,
-            )
+            nc.vector.tensor_copy(out=grouped[:], in_=wv_sb[half][:].rearrange("p h t d -> p h d t"))
 
         def quantise_wv(half):
             cols = slice(BANK * half, BANK * half + BANK)
@@ -267,10 +255,7 @@ def tile_transformergraphconv_pa_kernel(tc, x, q, k, W_v, conv_w, conv_b, ln_w, 
 
         def scores(unit, g):
             tile_no, h = divmod(unit, HEADS)
-            place = 2 * unit + 3 * g
-            late = place - (2 * PREP_ROUNDS + 3)
-            number = place % 3 if late < 0 else (3, *[(2 * PREP_ROUNDS + n) % 3 for n in range(3)])[late % 4]
-            s_bank = bank(number, [P, BANK], F32)
+            s_bank = bank(2 * g + unit % 2, [P, BANK], F32)
             s_banks[unit, g] = s_bank
             nc.tensor.matmul(
                 out=s_bank[:],
@@ -523,33 +508,35 @@ def tile_transformergraphconv_pa_kernel(tc, x, q, k, W_v, conv_w, conv_b, ln_w, 
             return [fill_v(h, 0), fill_v(h, 1)]
 
         halves = [(half, pair) for half in range(2) for pair in range(2)]
-        prep = [fill_x(half, pair) for half, pair in halves] + [fill_q(0, 1), fill_k(4), fill_k(5)]
-        prep += fill_vs(0) + [fill_k(6)] + fill_vs(1) + [fill_k(7), fill_q(1, 0)] + fill_vs(2) + fill_vs(3)
+        prep = [fill_x(half, pair) for half, pair in halves]
+        prep += [fill_k(0), fill_k(1)]
+        for h in range(HEADS):
+            prep += fill_vs(h) + ([fill_k(h + 2)] if h + 2 < HEADS else [])
         prep += [fill_cw(half, pair) for half, pair in halves]
-        prep += fill_vs(4) + [fill_projection(0, 0)] + fill_vs(5) + [fill_q(1, 1)] + fill_vs(6) + fill_vs(7)
-        prep += [fill_projection(0, 1)]
-        PREP_BANKS = (7, 3)
-        DRAIN = ("scalar", "vector")
+        prep += [fill_q(0, 0), fill_q(0, 1)]
+        DRAIN = ("scalar", "vector", "scalar")
         filled = []
 
         def prepare(n):
-            if 0 <= n - 2 < len(prep) and prep[n - 2][1]:
-                prep[n - 2][1]()
+            if 0 <= n - 3 < len(prep) and prep[n - 3][1]:
+                prep[n - 3][1]()
             if 0 <= n < len(prep):
-                filled.append(prep[n][0](PREP_BANKS[n % 2]))
-            if 0 <= n - 1 < len(prep):
-                filled[n - 1](DRAIN[(n - 1) % 2])
+                filled.append(prep[n][0](n % 8))
+            if 0 <= n - 2 < len(prep):
+                filled[n - 2](DRAIN[(n - 2) % 3])
 
         FLIP = 3
         LAG = FLIP + 2
-        PREP_ROUNDS = 11
-        first = [transpose_q(7, 0, 0)] + [transpose_k(3 + h, h) for h in range(4)]
-        for n, copy in enumerate(first):
-            copy(DRAIN[n % 2])
+        for n in range(len(prep) + 3):
+            prepare(n)
+            if n in (2, 3):
+                group_wv(n - 2)
+            if n in (4, 5):
+                quantise_wv(n - 4)
         late_copies = []
         scores(0, 0)
         scores(1, 0)
-        prepare(0)
+        scores(0, 1)
         for i in range(UNITS + LAG):
             group, step = divmod(i - LAG - HALF_HEADS + 1, HALF_HEADS)
             group_runs = 0 <= group < GROUPS - 1
@@ -560,39 +547,28 @@ def tile_transformergraphconv_pa_kernel(tc, x, q, k, W_v, conv_w, conv_b, ln_w, 
                 flip(i - FLIP)
             if i < UNITS:
                 scale_and_min(i, 0)
-            if i in (2, 3):
-                quantise_wv(i - 2)
-            prepare(3 * i + 1)
-            if i <= PREP_ROUNDS:
-                scores(i, 1)
-            if PREP_ROUNDS <= i < UNITS - 2:
+            if i + 2 < UNITS:
                 scores(i + 2, 0)
             if group_runs and step == 1:
                 attend(group, 2, 2)
             if 0 <= i - 1 < UNITS:
                 scale_and_min(i - 1, 1)
-            prepare(3 * i + 2)
-            if i < PREP_ROUNDS:
-                scores(i + 2, 0)
-            if PREP_ROUNDS <= i < UNITS - 1:
+            if i + 1 < UNITS:
                 scores(i + 1, 1)
             if 0 <= i - 2 < UNITS:
                 exponentials(i - 2)
             if 0 <= i - FLIP - 1 < UNITS:
                 regroup("scalar", i - FLIP - 1)
-            prepare(3 * i + 3)
-            if i in (0, 1):
-                group_wv(i)
 
             for copy in late_copies:
                 copy("scalar")
             late_copies.clear()
             q_tile, q_step = divmod(i + 4, HEADS)
-            if 2 <= q_tile < TILES and q_step in (0, 4):
-                late_copies.append(transpose_q(PREP_BANKS[0], q_tile, q_step // 4))
-            proj_tile, proj_step = divmod(i - 7, HEADS)
-            if 1 <= proj_tile < TILES and proj_step in (0, 2):
-                late_copies.append(projection(PREP_BANKS[0], proj_tile, proj_step // 2))
+            if 1 <= q_tile < TILES and q_step in (0, 4):
+                late_copies.append(transpose_q(7, q_tile, q_step // 4))
+            proj_tile, proj_step = divmod(i - 1, HEADS)
+            if 0 <= proj_tile < TILES and proj_step in (0, 4):
+                late_copies.append(projection(7, proj_tile, proj_step // 4))
 
             if group_runs and step == 2:
                 relu_and_divide(group)

@@ -27,6 +27,7 @@ HALVES = C_OUT // BANK
 HALF_HEADS = BANK // DH
 UNITS = TILES * HEADS
 GROUPS = UNITS // HALF_HEADS
+KEEP_WARM = 256
 SCALE = 1.0 / math.sqrt(DH)
 LN_EPS = 1e-5
 
@@ -257,6 +258,15 @@ def tile_transformergraphconv_pa_kernel(tc, x, q, k, W_v, conv_w, conv_b, ln_w, 
             tile_no, h = divmod(unit, HEADS)
             s_bank = bank(2 * g + unit % 2, [P, BANK], F32)
             s_banks[unit, g] = s_bank
+            nc.tensor.matmul_mx(
+                out=s_bank[:, :KEEP_WARM],
+                lhsT=x_codes[:, :P].bitcast(FP8X4),
+                lhsT_scale=x_scales[:, :P],
+                rhs=cw_codes[:, :KEEP_WARM].bitcast(FP8X4),
+                rhs_scale=cw_scales[:, :KEEP_WARM],
+                start=True,
+                stop=True,
+            )
             nc.tensor.matmul(
                 out=s_bank[:],
                 lhsT=qT[tile_no][:, h, :],
@@ -354,6 +364,7 @@ def tile_transformergraphconv_pa_kernel(tc, x, q, k, W_v, conv_w, conv_b, ln_w, 
         minus_mean = {}
         square_sums = {}
         rstd = {}
+        centred = {}
         out_rows = out.rearrange("b (p o) c -> (b o) p c", o=TILES)
 
         def half_cols(half):
@@ -452,35 +463,27 @@ def tile_transformergraphconv_pa_kernel(tc, x, q, k, W_v, conv_w, conv_b, ln_w, 
 
         def centre(tile_no, half):
             cols = half_cols(half)
-            centred = work.tile([P, BANK], F32, tag="attended")
+            scaled = work.tile([P, BANK], F32, tag="attended")
+            centred[tile_no, half] = scaled
             nc.vector.scalar_tensor_tensor(
-                out=centred[:],
+                out=scaled[:],
                 in0=y_all[:, tile_no, cols],
                 scalar=minus_mean[tile_no][:, 0:1],
                 in1=ln_w_all[:, cols],
                 op0=ALU.add,
                 op1=ALU.mult,
             )
-            return centred
 
-        def finish(tile_no, half, centred):
+        def finish(tile_no, half):
             cols = half_cols(half)
             nc.vector.scalar_tensor_tensor(
                 out=y_all[:, tile_no, cols],
-                in0=centred[:],
+                in0=centred[tile_no, half][:],
                 scalar=rstd[tile_no][:, 0:1],
                 in1=ln_b_all[:, cols],
                 op0=ALU.mult,
                 op1=ALU.add,
             )
-
-        def close_last(tile_no):
-            squares(tile_no)
-            centred = [centre(tile_no, half) for half in range(HALVES)]
-            deviation(tile_no)
-            for half in range(HALVES):
-                finish(tile_no, half, centred[half])
-                store(tile_no, half)
 
         def fill_k(h):
             return lambda number: transpose_k(number, h), None
@@ -537,6 +540,20 @@ def tile_transformergraphconv_pa_kernel(tc, x, q, k, W_v, conv_w, conv_b, ln_w, 
         scores(0, 0)
         scores(1, 0)
         scores(0, 1)
+        def close_group(group):
+            tile_no, half = divmod(group, HALVES)
+            relu_and_divide(group)
+            add_streams(nc.vector if tile_no >= TILES - 2 and (tile_no, half) != (TILES - 2, 0) else nc.gpsimd, group)
+            if half == 0 and 1 <= tile_no < TILES - 1:
+                deviation(tile_no - 1)
+                normalise(tile_no - 1)
+                affine(tile_no - 1, 0, ln_w_all, ALU.mult)
+            if half == 1 and 1 <= tile_no < TILES - 1:
+                affine(tile_no - 1, 1, ln_w_all, ALU.mult)
+                for n in range(HALVES):
+                    affine(tile_no - 1, n, ln_b_all, ALU.add)
+                    store(tile_no - 1, n)
+
         for i in range(UNITS + LAG):
             group, step = divmod(i - LAG - HALF_HEADS + 1, HALF_HEADS)
             group_runs = 0 <= group < GROUPS - 1
@@ -547,6 +564,8 @@ def tile_transformergraphconv_pa_kernel(tc, x, q, k, W_v, conv_w, conv_b, ln_w, 
                 flip(i - FLIP)
             if i < UNITS:
                 scale_and_min(i, 0)
+            if group_runs and step == 0:
+                quantise(group, 0, 2)
             if i + 2 < UNITS:
                 scores(i + 2, 0)
             if group_runs and step == 1:
@@ -570,40 +589,45 @@ def tile_transformergraphconv_pa_kernel(tc, x, q, k, W_v, conv_w, conv_b, ln_w, 
             if 0 <= proj_tile < TILES and proj_step in (0, 4):
                 late_copies.append(projection(7, proj_tile, proj_step // 4))
 
-            if group_runs and step == 2:
-                relu_and_divide(group)
-                add_streams(nc.gpsimd, group)
-                if closing_half == 0 and closing_tile >= 1:
-                    affine(closing_tile - 1, 1, ln_b_all, ALU.add)
-                    store(closing_tile - 1, 1)
             if 0 <= group < GROUPS and step == 0:
                 invert_row_sums(group)
             if group_runs and step == 0:
-                quantise(group, 0, HALF_HEADS)
+                quantise(group, 2, 2)
+                if group >= 1:
+                    close_group(group - 1)
                 attend(group, 0, 2)
+            if 1 <= group < GROUPS - 2 and group % HALVES == 0:
+                if step == 1:
+                    mean(group // HALVES - 1)
+                if step == 2:
+                    squares(group // HALVES - 1)
             if place == 1:
+                close_group(GROUPS - 2)
+                squares(TILES - 2)
                 quantise(GROUPS - 1, 0, 2)
                 attend(GROUPS - 1, 0, 2)
-            if place in (2, 3):
+            if place == 2:
                 quantise(GROUPS - 1, place, 1)
                 attend(GROUPS - 1, place, 1)
+                deviation(TILES - 2)
+                for half in range(HALVES):
+                    centre(TILES - 2, half)
+            if place == 3:
+                quantise(GROUPS - 1, place, 1)
+                attend(GROUPS - 1, place, 1)
+                finish(TILES - 2, 0)
+                store(TILES - 2, 0)
+            if place == 0:
+                mean(TILES - 2)
 
-            previous = group - 1
-            closing_tile, closing_half = divmod(previous, HALVES)
-            if 0 <= previous < GROUPS - 1 and closing_half == HALVES - 1:
-                if step == 0:
-                    squares(closing_tile)
-                    deviation(closing_tile)
-                    normalise(closing_tile)
-                if step == 1:
-                    affine(closing_tile, 0, ln_w_all, ALU.mult)
-                    affine(closing_tile, 0, ln_b_all, ALU.add)
-                    store(closing_tile, 0)
-                    affine(closing_tile, 1, ln_w_all, ALU.mult)
-            if group_runs and group % HALVES == HALVES - 1 and step == 3:
-                mean(group // HALVES)
-
-        relu_and_divide(GROUPS - 1)
-        add_streams(nc.vector, GROUPS - 1)
+        close_group(GROUPS - 1)
         mean(TILES - 1)
-        close_last(TILES - 1)
+        finish(TILES - 2, 1)
+        store(TILES - 2, 1)
+        squares(TILES - 1)
+        for half in range(HALVES):
+            centre(TILES - 1, half)
+        deviation(TILES - 1)
+        for half in range(HALVES):
+            finish(TILES - 1, half)
+            store(TILES - 1, half)

@@ -54,6 +54,10 @@ def tile_transformergraphconv_pa_kernel(tc, x, q, k, W_v, conv_w, conv_b, ln_w, 
         make_identity(nc, ident_bf[:])
         minus_half = keep.tile([P, 1], F32)
         nc.gpsimd.memset(minus_half[:], -0.5)
+        ones = keep.tile([P, P], BF16)
+        nc.gpsimd.memset(ones[:], 1.0)
+        minus_one = keep.tile([P, HALF_HEADS], F32)
+        nc.gpsimd.memset(minus_one[:], -1.0)
 
         x_rows = x.rearrange("b (p o) c -> (b p) o c", o=TILES)
         x_sb = []
@@ -65,6 +69,7 @@ def tile_transformergraphconv_pa_kernel(tc, x, q, k, W_v, conv_w, conv_b, ln_w, 
         k_sb = []
         q_rows = q.rearrange("b h (p o) d -> p (b h) (o d)", o=TILES)
         q_sb = {}
+        conv_b_sb = keep.tile([P, C_OUT // P], BF16)
         conv_b_all = keep.tile([P, C_OUT], BF16)
         ln_w_all = keep.tile([P, C_OUT], BF16)
         ln_b_all = keep.tile([P, C_OUT], BF16)
@@ -101,14 +106,23 @@ def tile_transformergraphconv_pa_kernel(tc, x, q, k, W_v, conv_w, conv_b, ln_w, 
             nc.sync.dma_start(out=rows[:].rearrange("p h o d -> p h (o d)"), in_=q_rows[:, heads, columns])
             q_sb[head_half, tile_half] = rows
 
-        for pair in range(PAIRS):
-            load_x(pair)
-        for half in range(2):
-            load_wv(half)
-        for h in range(HEADS):
-            load_k(h)
-        for half in range(2):
-            load_cw(half)
+        load_x(0)
+        load_x(1)
+        load_x(2)
+        load_x(3)
+        load_wv(0)
+        load_k(0)
+        load_k(1)
+        load_wv(1)
+        load_k(2)
+        load_k(3)
+        load_k(4)
+        load_k(5)
+        load_k(6)
+        load_k(7)
+        load_cw(0)
+        load_cw(1)
+        nc.sync.dma_start(out=conv_b_sb[:], in_=conv_b.rearrange("(p j) -> p j", p=P))
         nc.sync.dma_start(out=conv_b_all[:], in_=conv_b.partition_broadcast(P))
         for tile_half in range(2):
             for head_half in range(2):
@@ -125,8 +139,8 @@ def tile_transformergraphconv_pa_kernel(tc, x, q, k, W_v, conv_w, conv_b, ln_w, 
         v_codes = keep.tile([P, HEADS, PASSES, DH], U32, align_bytes=64)
         v_scales = keep.tile([P, HEADS, PASSES, DH], U8, align_bytes=64)
         kT = keep.tile([P, HEADS, NODES], BF16)
-        y_all = keep.tile([P, TILES, C_OUT], F32)
-        y_sums = keep.tile([P, TILES, 2 * HALVES], F32)
+        y_rows = {}
+        y_sums = {}
 
         def leave_psum(engine, out, in_):
             if engine == "vector":
@@ -139,7 +153,7 @@ def tile_transformergraphconv_pa_kernel(tc, x, q, k, W_v, conv_w, conv_b, ln_w, 
         def group_channels_last(number, name, pair_rows, half, pair):
             words = pair_rows.bitcast(F32)
             if pair == 0:
-                grouped = stage.tile([P, PACK, P, PACK], BF16, tag="grouped", align_bytes=64)
+                grouped = stage.tile([P, PACK, P, PACK], BF16, tag="grouped", bufs=4, align_bytes=64)
                 grouped_rows[name, half] = grouped
             grouped_words = grouped_rows[name, half][:].bitcast(F32)
             flipped = bank(number, [P, 2, 2, P], F32)
@@ -176,7 +190,7 @@ def tile_transformergraphconv_pa_kernel(tc, x, q, k, W_v, conv_w, conv_b, ln_w, 
 
         def values(number, h, g):
             if g == 0:
-                grouped = stage.tile([P, PASSES, DH, PACK], BF16, tag="v_grouped", align_bytes=64)
+                grouped = stage.tile([P, PASSES, DH, PACK], BF16, tag="v_grouped", bufs=4, align_bytes=64)
                 v_grouped[h] = grouped
             v_bank = bank(number, [P, PACK, DH], F32)
             for t in range(PACK):
@@ -202,6 +216,8 @@ def tile_transformergraphconv_pa_kernel(tc, x, q, k, W_v, conv_w, conv_b, ln_w, 
                 in_=v_grouped[h][:].rearrange("p g d t -> p (g d t)"),
             )
 
+        proj_banks = {}
+
         def projection(number, tile_no, half):
             nodes = slice(P * tile_no, P * tile_no + P)
             cols = slice(BANK * half, BANK * half + BANK)
@@ -215,15 +231,7 @@ def tile_transformergraphconv_pa_kernel(tc, x, q, k, W_v, conv_w, conv_b, ln_w, 
                 start=True,
                 stop=True,
             )
-            return lambda engine: nc.vector.scalar_tensor_tensor(
-                out=y_all[:, tile_no, cols],
-                in0=proj_bank[:],
-                scalar=0.0,
-                in1=conv_b_all[:, cols],
-                op0=ALU.add,
-                op1=ALU.add,
-                accum_out=y_sums[:, tile_no, half : half + 1],
-            )
+            proj_banks[tile_no, half] = proj_bank
 
         def transpose_k(number, h):
             flipped = bank(number, [P, PASSES, 2, 2, P], BF16)
@@ -258,15 +266,6 @@ def tile_transformergraphconv_pa_kernel(tc, x, q, k, W_v, conv_w, conv_b, ln_w, 
             tile_no, h = divmod(unit, HEADS)
             s_bank = bank(2 * g + unit % 2, [P, BANK], F32)
             s_banks[unit, g] = s_bank
-            nc.tensor.matmul_mx(
-                out=s_bank[:, :KEEP_WARM],
-                lhsT=x_codes[:, :P].bitcast(FP8X4),
-                lhsT_scale=x_scales[:, :P],
-                rhs=cw_codes[:, :KEEP_WARM].bitcast(FP8X4),
-                rhs_scale=cw_scales[:, :KEEP_WARM],
-                start=True,
-                stop=True,
-            )
             nc.tensor.matmul(
                 out=s_bank[:],
                 lhsT=qT[tile_no][:, h, :],
@@ -370,46 +369,87 @@ def tile_transformergraphconv_pa_kernel(tc, x, q, k, W_v, conv_w, conv_b, ln_w, 
         def half_cols(half):
             return slice(BANK * half, BANK * half + BANK)
 
+        half_bias_mean = keep.tile([P, 1], F32)
+        scaled_bias = keep.tile([P, C_OUT // P], F32)
+
+        def bias_mean(number):
+            added = bank(number, [P, C_OUT // P], F32)
+            nc.tensor.matmul(out=added[:], lhsT=ones[:], rhs=conv_b_sb[:], start=True, stop=True)
+            return lambda engine: nc.scalar.activation(
+                out=scaled_bias[:],
+                in_=added[:],
+                func=ACT.Copy,
+                scale=-0.5 / C_OUT,
+                accum_out=half_bias_mean[:, 0:1],
+            )
+
         def invert_row_sums(group):
             tile_no, half = divmod(group, HALVES)
             heads = slice(HALF_HEADS * half, HALF_HEADS * half + HALF_HEADS)
             inverse = small.tile([P, HALF_HEADS], F32, tag="inverse")
-            nc.vector.reciprocal(out=inverse[:], in_=row_sums[tile_no][:, heads])
+            nc.gpsimd.tensor_tensor(out=inverse[:], in0=row_sums[tile_no][:, heads], in1=minus_one[:], op=ALU.pow)
             inverse_sums[group] = inverse
 
-        def relu_and_divide(group):
-            tile_no, half = divmod(group, HALVES)
+        def relu_and_divide(engine, group):
             relu_o = work.tile([P, HALF_HEADS, DH], F32, tag="attended")
-            nc.vector.scalar_tensor_tensor(
-                out=relu_o[:],
-                in0=o_banks[group][:],
-                scalar=0.0,
-                in1=inverse_sums[group][:].unsqueeze(2).to_broadcast([P, HALF_HEADS, DH]),
-                op0=ALU.max,
-                op1=ALU.mult,
-                accum_out=y_sums[:, tile_no, HALVES + half : HALVES + half + 1],
-            )
             attended[group] = relu_o
+            if engine == "vector":
+                nc.vector.scalar_tensor_tensor(
+                    out=relu_o[:],
+                    in0=o_banks[group][:],
+                    scalar=0.0,
+                    in1=inverse_sums[group][:].unsqueeze(2).to_broadcast([P, HALF_HEADS, DH]),
+                    op0=ALU.max,
+                    op1=ALU.mult,
+                )
+            else:
+                for n in range(HALF_HEADS):
+                    nc.scalar.activation(
+                        out=relu_o[:, n, :],
+                        in_=o_banks[group][:, n, :],
+                        func=ACT.Relu,
+                        scale=inverse_sums[group][:, n : n + 1],
+                    )
 
-        def add_streams(engine, group):
+        def add_streams(group, first, second):
             tile_no, half = divmod(group, HALVES)
-            engine.tensor_tensor(
-                out=y_all[:, tile_no, half_cols(half)],
-                in0=attended[group][:].rearrange("p h d -> p (h d)"),
-                in1=y_all[:, tile_no, half_cols(half)],
-                op=ALU.add,
+            if half == 0:
+                sums = small.tile([P, HALVES], F32, tag="y_sums")
+                y_sums[tile_no] = sums
+            nc.vector.scalar_tensor_tensor(
+                out=y_rows[tile_no][:, half_cols(half)],
+                in0=first,
+                scalar=0.0,
+                in1=second,
+                op0=ALU.add,
+                op1=ALU.add,
+                accum_out=y_sums[tile_no][:, half : half + 1],
             )
 
-        def mean(tile_no):
-            scaled_sums = small.tile([P, 2 * HALVES], F32, tag="scaled_sums")
+        def open_rows(group):
+            if group % HALVES == 0:
+                rows = work.tile([P, C_OUT], F32, tag="y", bufs=4)
+                y_rows[group // HALVES] = rows
+
+        def add_projection(group):
+            open_rows(group)
+            heads = attended[group][:].rearrange("p h d -> p (h d)")
+            add_streams(group, proj_banks[divmod(group, HALVES)][:], heads)
+
+        def add_bias(engine, group, source):
+            tile_no, half = divmod(group, HALVES)
+            cols = half_cols(half)
+            engine.tensor_tensor(out=y_rows[tile_no][:, cols], in0=source, in1=conv_b_all[:, cols], op=ALU.add)
+
+        def mean(tile_no, bias):
+            scaled_sums = small.tile([P, HALVES], F32, tag="scaled_sums")
             negative = small.tile([P, 1], F32, tag="minus_mean")
-            nc.vector.tensor_scalar(
+            nc.scalar.activation(
                 out=scaled_sums[:],
-                in0=y_sums[:, tile_no, :],
-                scalar1=-1.0 / C_OUT,
-                scalar2=None,
-                op0=ALU.mult,
-                op1=ALU.add,
+                in_=y_sums[tile_no][:],
+                func=ACT.Identity,
+                bias=bias,
+                scale=-1.0 / C_OUT,
                 accum_out=negative[:, 0:1],
             )
             minus_mean[tile_no] = negative
@@ -419,7 +459,7 @@ def tile_transformergraphconv_pa_kernel(tc, x, q, k, W_v, conv_w, conv_b, ln_w, 
             square_sum = small.tile([P, 1], F32, tag="square_sum")
             nc.scalar.activation(
                 out=squared[:],
-                in_=y_all[:, tile_no, :],
+                in_=y_rows[tile_no][:],
                 func=ACT.Square,
                 bias=minus_mean[tile_no][:, 0:1],
                 scale=1.0,
@@ -443,8 +483,8 @@ def tile_transformergraphconv_pa_kernel(tc, x, q, k, W_v, conv_w, conv_b, ln_w, 
 
         def normalise(tile_no):
             nc.gpsimd.tensor_scalar(
-                out=y_all[:, tile_no, :],
-                in0=y_all[:, tile_no, :],
+                out=y_rows[tile_no][:],
+                in0=y_rows[tile_no][:],
                 scalar1=minus_mean[tile_no][:, 0:1],
                 scalar2=rstd[tile_no][:, 0:1],
                 op0=ALU.add,
@@ -454,12 +494,12 @@ def tile_transformergraphconv_pa_kernel(tc, x, q, k, W_v, conv_w, conv_b, ln_w, 
         def affine(tile_no, half, vector, op):
             cols = half_cols(half)
             nc.gpsimd.tensor_tensor(
-                out=y_all[:, tile_no, cols], in0=y_all[:, tile_no, cols], in1=vector[:, cols], op=op
+                out=y_rows[tile_no][:, cols], in0=y_rows[tile_no][:, cols], in1=vector[:, cols], op=op
             )
 
         def store(tile_no, half):
             cols = half_cols(half)
-            nc.sync.dma_start(out=out_rows[tile_no, :, cols], in_=y_all[:, tile_no, cols])
+            nc.sync.dma_start(out=out_rows[tile_no, :, cols], in_=y_rows[tile_no][:, cols])
 
         def centre(tile_no, half):
             cols = half_cols(half)
@@ -467,7 +507,7 @@ def tile_transformergraphconv_pa_kernel(tc, x, q, k, W_v, conv_w, conv_b, ln_w, 
             centred[tile_no, half] = scaled
             nc.vector.scalar_tensor_tensor(
                 out=scaled[:],
-                in0=y_all[:, tile_no, cols],
+                in0=y_rows[tile_no][:, cols],
                 scalar=minus_mean[tile_no][:, 0:1],
                 in1=ln_w_all[:, cols],
                 op0=ALU.add,
@@ -477,7 +517,7 @@ def tile_transformergraphconv_pa_kernel(tc, x, q, k, W_v, conv_w, conv_b, ln_w, 
         def finish(tile_no, half):
             cols = half_cols(half)
             nc.vector.scalar_tensor_tensor(
-                out=y_all[:, tile_no, cols],
+                out=y_rows[tile_no][:, cols],
                 in0=centred[tile_no, half][:],
                 scalar=rstd[tile_no][:, 0:1],
                 in1=ln_b_all[:, cols],
@@ -504,51 +544,57 @@ def tile_transformergraphconv_pa_kernel(tc, x, q, k, W_v, conv_w, conv_b, ln_w, 
         def fill_q(tile_no, half):
             return lambda number: transpose_q(number, tile_no, half), None
 
-        def fill_projection(tile_no, half):
-            return lambda number: projection(number, tile_no, half), None
-
         def fill_vs(h):
             return [fill_v(h, 0), fill_v(h, 1)]
 
         halves = [(half, pair) for half in range(2) for pair in range(2)]
-        prep = [fill_x(half, pair) for half, pair in halves]
-        prep += [fill_k(0), fill_k(1)]
-        for h in range(HEADS):
-            prep += fill_vs(h) + ([fill_k(h + 2)] if h + 2 < HEADS else [])
-        prep += [fill_cw(half, pair) for half, pair in halves]
-        prep += [fill_q(0, 0), fill_q(0, 1)]
+        prep = [fill_x(0, 0), fill_x(0, 1), fill_x(1, 0), fill_x(1, 1), fill_k(0), fill_k(1), fill_v(0, 0), fill_v(0, 1), fill_v(1, 0), fill_v(1, 1), fill_v(2, 0), fill_v(2, 1), fill_v(3, 0), fill_v(3, 1), fill_k(2), fill_k(3), fill_k(4), fill_k(5), fill_v(4, 0), fill_v(4, 1), fill_v(5, 0), fill_v(5, 1), fill_v(6, 0), fill_v(6, 1), fill_v(7, 0), fill_v(7, 1), fill_k(6), fill_k(7), fill_cw(0, 0), fill_cw(0, 1), fill_cw(1, 0), fill_cw(1, 1), fill_q(0, 0), fill_q(0, 1)]
+
         DRAIN = ("scalar", "vector", "scalar")
+        DELAY = 2
         filled = []
 
         def prepare(n):
-            if 0 <= n - 3 < len(prep) and prep[n - 3][1]:
-                prep[n - 3][1]()
+            if 0 <= n - DELAY - 1 < len(prep) and prep[n - DELAY - 1][1]:
+                prep[n - DELAY - 1][1]()
             if 0 <= n < len(prep):
                 filled.append(prep[n][0](n % 8))
-            if 0 <= n - 2 < len(prep):
-                filled[n - 2](DRAIN[(n - 2) % 3])
+            if 0 <= n - DELAY < len(prep):
+                filled[n - DELAY](DRAIN[(n - DELAY) % len(DRAIN)])
 
         FLIP = 3
         LAG = FLIP + 2
-        for n in range(len(prep) + 3):
+        for n in range(len(prep) + DELAY + 1):
             prepare(n)
-            if n in (2, 3):
-                group_wv(n - 2)
-            if n in (4, 5):
-                quantise_wv(n - 4)
+            if n == 4:
+                group_wv(0)
+            if n == 5:
+                quantise_wv(0)
+            if n == 7:
+                group_wv(1)
+            if n == 8:
+                quantise_wv(1)
+        bias_mean(7)("scalar")
         late_copies = []
+        late_adds = []
         scores(0, 0)
         scores(1, 0)
         scores(0, 1)
         def close_group(group):
+            relu_and_divide("scalar" if group % HALVES == 0 and group < GROUPS - 2 else "vector", group)
+            if group < GROUPS - 2:
+                projection(7, *divmod(group, HALVES))
+
+        def finish_group(group):
             tile_no, half = divmod(group, HALVES)
-            relu_and_divide(group)
-            add_streams(nc.vector if tile_no >= TILES - 2 and (tile_no, half) != (TILES - 2, 0) else nc.gpsimd, group)
-            if half == 0 and 1 <= tile_no < TILES - 1:
+            add_projection(group)
+            invert_row_sums(group + 1)
+            add_bias(nc.gpsimd, group, y_rows[tile_no][:, half_cols(half)])
+            if half == 0 and tile_no >= 1:
                 deviation(tile_no - 1)
                 normalise(tile_no - 1)
                 affine(tile_no - 1, 0, ln_w_all, ALU.mult)
-            if half == 1 and 1 <= tile_no < TILES - 1:
+            if half == 1 and 1 <= tile_no < TILES - 2 or half == 0 and tile_no == TILES - 2:
                 affine(tile_no - 1, 1, ln_w_all, ALU.mult)
                 for n in range(HALVES):
                     affine(tile_no - 1, n, ln_b_all, ALU.add)
@@ -574,6 +620,9 @@ def tile_transformergraphconv_pa_kernel(tc, x, q, k, W_v, conv_w, conv_b, ln_w, 
                 scale_and_min(i - 1, 1)
             if i + 1 < UNITS:
                 scores(i + 1, 1)
+            for early in late_adds:
+                add_bias(nc.vector, early, proj_banks[divmod(early, HALVES)][:])
+            late_adds.clear()
             if 0 <= i - 2 < UNITS:
                 exponentials(i - 2)
             if 0 <= i - FLIP - 1 < UNITS:
@@ -582,31 +631,42 @@ def tile_transformergraphconv_pa_kernel(tc, x, q, k, W_v, conv_w, conv_b, ln_w, 
             for copy in late_copies:
                 copy("scalar")
             late_copies.clear()
-            q_tile, q_step = divmod(i + 4, HEADS)
+            q_tile, q_step = divmod(i + 7, HEADS)
             if 1 <= q_tile < TILES and q_step in (0, 4):
                 late_copies.append(transpose_q(7, q_tile, q_step // 4))
-            proj_tile, proj_step = divmod(i - 1, HEADS)
-            if 0 <= proj_tile < TILES and proj_step in (0, 4):
-                late_copies.append(projection(7, proj_tile, proj_step // 4))
 
-            if 0 <= group < GROUPS and step == 0:
-                invert_row_sums(group)
             if group_runs and step == 0:
                 quantise(group, 2, 2)
                 if group >= 1:
-                    close_group(group - 1)
+                    finish_group(group - 1)
                 attend(group, 0, 2)
-            if 1 <= group < GROUPS - 2 and group % HALVES == 0:
-                if step == 1:
-                    mean(group // HALVES - 1)
+            if group_runs and step == 3 and group < GROUPS - 2:
+                close_group(group)
+            if 1 <= group < GROUPS - 1 and group % HALVES == 0:
                 if step == 2:
+                    mean(group // HALVES - 1, half_bias_mean[:, 0:1])
+                if step == 3:
                     squares(group // HALVES - 1)
+            if group == 0 and step == 1:
+                invert_row_sums(0)
+            if place == 1:
+                invert_row_sums(GROUPS - 1)
+
+            if i in (UNITS - 7, UNITS - 3):
+                early = GROUPS - 2 + (i - UNITS + 7) // 4
+                open_rows(early)
+                projection(7, *divmod(early, HALVES))
+                late_adds.append(early)
             if place == 1:
                 close_group(GROUPS - 2)
-                squares(TILES - 2)
                 quantise(GROUPS - 1, 0, 2)
                 attend(GROUPS - 1, 0, 2)
             if place == 2:
+                add_streams(
+                    GROUPS - 2,
+                    attended[GROUPS - 2][:].rearrange("p h d -> p (h d)"),
+                    y_rows[TILES - 1][:, half_cols(0)],
+                )
                 quantise(GROUPS - 1, place, 1)
                 attend(GROUPS - 1, place, 1)
                 deviation(TILES - 2)
@@ -617,11 +677,12 @@ def tile_transformergraphconv_pa_kernel(tc, x, q, k, W_v, conv_w, conv_b, ln_w, 
                 attend(GROUPS - 1, place, 1)
                 finish(TILES - 2, 0)
                 store(TILES - 2, 0)
-            if place == 0:
-                mean(TILES - 2)
 
         close_group(GROUPS - 1)
-        mean(TILES - 1)
+        add_streams(
+            GROUPS - 1, attended[GROUPS - 1][:].rearrange("p h d -> p (h d)"), y_rows[TILES - 1][:, half_cols(1)]
+        )
+        mean(TILES - 1, 0.0)
         finish(TILES - 2, 1)
         store(TILES - 2, 1)
         squares(TILES - 1)

@@ -56,8 +56,6 @@ def tile_transformergraphconv_pa_kernel(tc, x, q, k, W_v, conv_w, conv_b, ln_w, 
         nc.gpsimd.memset(minus_half[:], -0.5)
         ones = keep.tile([P, P], BF16)
         nc.gpsimd.memset(ones[:], 1.0)
-        minus_one = keep.tile([P, HALF_HEADS], F32)
-        nc.gpsimd.memset(minus_one[:], -1.0)
 
         x_rows = x.rearrange("b (p o) c -> (b p) o c", o=TILES)
         x_sb = []
@@ -387,54 +385,56 @@ def tile_transformergraphconv_pa_kernel(tc, x, q, k, W_v, conv_w, conv_b, ln_w, 
             tile_no, half = divmod(group, HALVES)
             heads = slice(HALF_HEADS * half, HALF_HEADS * half + HALF_HEADS)
             inverse = small.tile([P, HALF_HEADS], F32, tag="inverse")
-            nc.gpsimd.tensor_tensor(out=inverse[:], in0=row_sums[tile_no][:, heads], in1=minus_one[:], op=ALU.pow)
+            nc.vector.reciprocal(out=inverse[:], in_=row_sums[tile_no][:, heads])
             inverse_sums[group] = inverse
 
-        def relu_and_divide(engine, group):
-            relu_o = work.tile([P, HALF_HEADS, DH], F32, tag="attended")
-            attended[group] = relu_o
+        def relu_and_divide(engine, group, first, count):
+            if first == 0:
+                relu_o = work.tile([P, HALF_HEADS, DH], F32, tag="attended")
+                attended[group] = relu_o
             if engine == "vector":
+                heads = slice(first, first + count)
+                inverse = inverse_sums[group][:, heads].unsqueeze(2).to_broadcast([P, count, DH])
                 nc.vector.scalar_tensor_tensor(
-                    out=relu_o[:],
-                    in0=o_banks[group][:],
+                    out=attended[group][:, heads, :],
+                    in0=o_banks[group][:, heads, :],
                     scalar=0.0,
-                    in1=inverse_sums[group][:].unsqueeze(2).to_broadcast([P, HALF_HEADS, DH]),
+                    in1=inverse,
                     op0=ALU.max,
                     op1=ALU.mult,
                 )
             else:
-                for n in range(HALF_HEADS):
+                for n in range(first, first + count):
                     nc.scalar.activation(
-                        out=relu_o[:, n, :],
+                        out=attended[group][:, n, :],
                         in_=o_banks[group][:, n, :],
                         func=ACT.Relu,
                         scale=inverse_sums[group][:, n : n + 1],
                     )
 
-        def add_streams(group, first, second):
+        def open_rows(tile_no):
+            rows = work.tile([P, C_OUT], F32, tag="y", bufs=4)
+            y_rows[tile_no] = rows
+            sums = small.tile([P, HALVES + tile_no // (TILES - 1)], F32, tag="y_sums")
+            y_sums[tile_no] = sums
+
+        def add_streams(group, first, count, other, column):
             tile_no, half = divmod(group, HALVES)
-            if half == 0:
-                sums = small.tile([P, HALVES], F32, tag="y_sums")
-                y_sums[tile_no] = sums
+            start = BANK * half + DH * first
             nc.vector.scalar_tensor_tensor(
-                out=y_rows[tile_no][:, half_cols(half)],
-                in0=first,
+                out=y_rows[tile_no][:, start : start + DH * count],
+                in0=other,
                 scalar=0.0,
-                in1=second,
+                in1=attended[group][:, first : first + count, :].rearrange("p h d -> p (h d)"),
                 op0=ALU.add,
                 op1=ALU.add,
-                accum_out=y_sums[tile_no][:, half : half + 1],
+                accum_out=y_sums[tile_no][:, column : column + 1],
             )
 
-        def open_rows(group):
-            if group % HALVES == 0:
-                rows = work.tile([P, C_OUT], F32, tag="y", bufs=4)
-                y_rows[group // HALVES] = rows
-
-        def add_projection(group):
-            open_rows(group)
-            heads = attended[group][:].rearrange("p h d -> p (h d)")
-            add_streams(group, proj_banks[divmod(group, HALVES)][:], heads)
+        def add_to_early(group, first, count, column):
+            tile_no, half = divmod(group, HALVES)
+            start = BANK * half + DH * first
+            add_streams(group, first, count, y_rows[tile_no][:, start : start + DH * count], column)
 
         def add_bias(engine, group, source):
             tile_no, half = divmod(group, HALVES)
@@ -442,7 +442,7 @@ def tile_transformergraphconv_pa_kernel(tc, x, q, k, W_v, conv_w, conv_b, ln_w, 
             engine.tensor_tensor(out=y_rows[tile_no][:, cols], in0=source, in1=conv_b_all[:, cols], op=ALU.add)
 
         def mean(tile_no, bias):
-            scaled_sums = small.tile([P, HALVES], F32, tag="scaled_sums")
+            scaled_sums = small.tile([P, HALVES + tile_no // (TILES - 1)], F32, tag="scaled_sums")
             negative = small.tile([P, 1], F32, tag="minus_mean")
             nc.scalar.activation(
                 out=scaled_sums[:],
@@ -497,8 +497,7 @@ def tile_transformergraphconv_pa_kernel(tc, x, q, k, W_v, conv_w, conv_b, ln_w, 
                 out=y_rows[tile_no][:, cols], in0=y_rows[tile_no][:, cols], in1=vector[:, cols], op=op
             )
 
-        def store(tile_no, half):
-            cols = half_cols(half)
+        def store(tile_no, cols):
             nc.sync.dma_start(out=out_rows[tile_no, :, cols], in_=y_rows[tile_no][:, cols])
 
         def centre(tile_no, half):
@@ -514,16 +513,19 @@ def tile_transformergraphconv_pa_kernel(tc, x, q, k, W_v, conv_w, conv_b, ln_w, 
                 op1=ALU.mult,
             )
 
-        def finish(tile_no, half):
-            cols = half_cols(half)
+        def finish(tile_no, half, part, parts):
+            width = BANK // parts
+            within = slice(width * part, width * part + width)
+            cols = slice(BANK * half + width * part, BANK * half + width * part + width)
             nc.vector.scalar_tensor_tensor(
                 out=y_rows[tile_no][:, cols],
-                in0=centred[tile_no, half][:],
+                in0=centred[tile_no, half][:, within],
                 scalar=rstd[tile_no][:, 0:1],
                 in1=ln_b_all[:, cols],
                 op0=ALU.mult,
                 op1=ALU.add,
             )
+            store(tile_no, cols)
 
         def fill_k(h):
             return lambda number: transpose_k(number, h), None
@@ -581,14 +583,14 @@ def tile_transformergraphconv_pa_kernel(tc, x, q, k, W_v, conv_w, conv_b, ln_w, 
         scores(1, 0)
         scores(0, 1)
         def close_group(group):
-            relu_and_divide("scalar" if group % HALVES == 0 and group < GROUPS - 2 else "vector", group)
-            if group < GROUPS - 2:
-                projection(7, *divmod(group, HALVES))
+            relu_and_divide("scalar" if group % HALVES == 0 else "vector", group, 0, HALF_HEADS)
+            projection(7, *divmod(group, HALVES))
 
         def finish_group(group):
             tile_no, half = divmod(group, HALVES)
-            add_projection(group)
-            invert_row_sums(group + 1)
+            if half == 0:
+                open_rows(tile_no)
+            add_streams(group, 0, HALF_HEADS, proj_banks[tile_no, half][:], half)
             add_bias(nc.gpsimd, group, y_rows[tile_no][:, half_cols(half)])
             if half == 0 and tile_no >= 1:
                 deviation(tile_no - 1)
@@ -598,7 +600,7 @@ def tile_transformergraphconv_pa_kernel(tc, x, q, k, W_v, conv_w, conv_b, ln_w, 
                 affine(tile_no - 1, 1, ln_w_all, ALU.mult)
                 for n in range(HALVES):
                     affine(tile_no - 1, n, ln_b_all, ALU.add)
-                    store(tile_no - 1, n)
+                    store(tile_no - 1, half_cols(n))
 
         for i in range(UNITS + LAG):
             group, step = divmod(i - LAG - HALF_HEADS + 1, HALF_HEADS)
@@ -606,8 +608,6 @@ def tile_transformergraphconv_pa_kernel(tc, x, q, k, W_v, conv_w, conv_b, ln_w, 
             closing_tile, closing_half = divmod(group, HALVES)
             place = i - LAG - HALF_HEADS * (GROUPS - 1)
 
-            if 0 <= i - FLIP < UNITS:
-                flip(i - FLIP)
             if i < UNITS:
                 scale_and_min(i, 0)
             if group_runs and step == 0:
@@ -620,6 +620,8 @@ def tile_transformergraphconv_pa_kernel(tc, x, q, k, W_v, conv_w, conv_b, ln_w, 
                 scale_and_min(i - 1, 1)
             if i + 1 < UNITS:
                 scores(i + 1, 1)
+            if 0 <= i - FLIP < UNITS:
+                flip(i - FLIP)
             for early in late_adds:
                 add_bias(nc.vector, early, proj_banks[divmod(early, HALVES)][:])
             late_adds.clear()
@@ -631,7 +633,7 @@ def tile_transformergraphconv_pa_kernel(tc, x, q, k, W_v, conv_w, conv_b, ln_w, 
             for copy in late_copies:
                 copy("scalar")
             late_copies.clear()
-            q_tile, q_step = divmod(i + 7, HEADS)
+            q_tile, q_step = divmod(i + 12 - LAG, HEADS)
             if 1 <= q_tile < TILES and q_step in (0, 4):
                 late_copies.append(transpose_q(7, q_tile, q_step // 4))
 
@@ -647,48 +649,43 @@ def tile_transformergraphconv_pa_kernel(tc, x, q, k, W_v, conv_w, conv_b, ln_w, 
                     mean(group // HALVES - 1, half_bias_mean[:, 0:1])
                 if step == 3:
                     squares(group // HALVES - 1)
-            if group == 0 and step == 1:
-                invert_row_sums(0)
-            if place == 1:
+            if group_runs and step == 1:
+                invert_row_sums(group)
+            if place == 2:
                 invert_row_sums(GROUPS - 1)
 
-            if i in (UNITS - 7, UNITS - 3):
-                early = GROUPS - 2 + (i - UNITS + 7) // 4
-                open_rows(early)
+            if group in (GROUPS - 4, GROUPS - 3) and step == 1:
+                early = group + 2
+                if early % HALVES == 0:
+                    open_rows(early // HALVES)
                 projection(7, *divmod(early, HALVES))
                 late_adds.append(early)
             if place == 1:
-                close_group(GROUPS - 2)
+                relu_and_divide("vector", GROUPS - 2, 0, HALF_HEADS)
                 quantise(GROUPS - 1, 0, 2)
                 attend(GROUPS - 1, 0, 2)
             if place == 2:
-                add_streams(
-                    GROUPS - 2,
-                    attended[GROUPS - 2][:].rearrange("p h d -> p (h d)"),
-                    y_rows[TILES - 1][:, half_cols(0)],
-                )
+                add_to_early(GROUPS - 2, 0, HALF_HEADS, 0)
                 quantise(GROUPS - 1, place, 1)
                 attend(GROUPS - 1, place, 1)
                 deviation(TILES - 2)
-                for half in range(HALVES):
-                    centre(TILES - 2, half)
             if place == 3:
+                relu_and_divide("vector", GROUPS - 1, 0, place)
                 quantise(GROUPS - 1, place, 1)
                 attend(GROUPS - 1, place, 1)
-                finish(TILES - 2, 0)
-                store(TILES - 2, 0)
+                add_to_early(GROUPS - 1, 0, place, 1)
+                for half in range(HALVES):
+                    centre(TILES - 2, half)
 
-        close_group(GROUPS - 1)
-        add_streams(
-            GROUPS - 1, attended[GROUPS - 1][:].rearrange("p h d -> p (h d)"), y_rows[TILES - 1][:, half_cols(1)]
-        )
+        relu_and_divide("vector", GROUPS - 1, HALF_HEADS - 1, 1)
+        add_to_early(GROUPS - 1, HALF_HEADS - 1, 1, HALVES)
         mean(TILES - 1, 0.0)
-        finish(TILES - 2, 1)
-        store(TILES - 2, 1)
+        for half in range(HALVES):
+            finish(TILES - 2, half, 0, 1)
         squares(TILES - 1)
         for half in range(HALVES):
             centre(TILES - 1, half)
         deviation(TILES - 1)
         for half in range(HALVES):
-            finish(TILES - 1, half)
-            store(TILES - 1, half)
+            for part in range(2):
+                finish(TILES - 1, half, part, 2)

from contextlib import ExitStack
import math

import concourse.mybir as mybir
from concourse.masks import make_identity

F32 = mybir.dt.float32
BF16 = mybir.dt.bfloat16
U32 = mybir.dt.uint32
U8 = mybir.dt.uint8
FP8X4 = mybir.dt.float8_e4m3fn_x4
ALU = mybir.AluOpType
ACT = mybir.ActivationFunctionType

P = 128
NODES = 1024
C_IN = 512
C_OUT = 1024
HEADS = 8
DH = 128
PACK = 4
BANK = 512
TILES = NODES // P
PAIRS = TILES // 2
PASSES = NODES // (P * PACK)
HALVES = C_OUT // BANK
HALF_HEADS = BANK // DH
UNITS = TILES * HEADS
GROUPS = UNITS // HALF_HEADS
KEEP_WARM = 256
SCALE = 1.0 / math.sqrt(DH)
LN_EPS = 1e-5

FLOPS = 2 * NODES * C_IN * C_OUT * 2 + 2 * HEADS * NODES * NODES * DH * 2


def tile_transformergraphconv_pa_kernel(tc, x, q, k, W_v, conv_w, conv_b, ln_w, ln_b, out):
    nc = tc.nc
    with ExitStack() as ctx:
        ctx.enter_context(tc.manual_schedule())
        keep = ctx.enter_context(tc.tile_pool(name="keep", bufs=1))
        stage = ctx.enter_context(tc.tile_pool(name="stage", bufs=2))
        work = ctx.enter_context(tc.tile_pool(name="work", bufs=3))
        small = ctx.enter_context(tc.tile_pool(name="small", bufs=4))
        psum = ctx.enter_context(tc.psum_pool(name="psum", bufs=1))

        def bank(number, shape, dtype):
            whole = psum.tile(shape, dtype, tag="bank%d" % number)
            return whole

        ident_f32 = keep.tile([P, P], F32)
        make_identity(nc, ident_f32[:])
        ident_bf = keep.tile([P, P], BF16)
        make_identity(nc, ident_bf[:])
        minus_half = keep.tile([P, 1], F32)
        nc.gpsimd.memset(minus_half[:], -0.5)
        ones = keep.tile([P, P], BF16)
        nc.gpsimd.memset(ones[:], 1.0)

        x_rows = x.rearrange("b (p o) c -> (b p) o c", o=TILES)
        x_sb = []
        wv_rows = W_v.rearrange("h (u p e) d -> u p h (e d)", u=2, e=2)
        wv_sb = []
        cw_rows = conv_w.rearrange("(j p) c -> p j c", p=P)
        cw_sb = []
        k_rows = k.rearrange("b h (s p f) d -> (b h) p s (f d)", s=2, f=4)
        k_sb = []
        q_rows = q.rearrange("b h (p o) d -> p (b h) (o d)", o=TILES)
        q_sb = {}
        conv_b_sb = keep.tile([P, C_OUT // P], BF16)
        conv_b_all = keep.tile([P, C_OUT], BF16)
        ln_w_all = keep.tile([P, C_OUT], BF16)
        ln_b_all = keep.tile([P, C_OUT], BF16)

        def load_x(pair):
            rows = keep.tile([P, 2, C_IN], BF16, tag="x_rows%d" % pair)
            nc.sync.dma_start(out=rows[:], in_=x_rows[:, 2 * pair : 2 * pair + 2, :])
            x_sb.append(rows)

        def load_wv(half):
            heads = slice(HALF_HEADS * half, HALF_HEADS * half + HALF_HEADS)
            rows = keep.tile([P, HALF_HEADS, PACK, DH], BF16, tag="wv_rows%d" % half)
            for u in range(2):
                nc.sync.dma_start(
                    out=rows[:, :, 2 * u : 2 * u + 2, :].rearrange("p h e d -> p h (e d)"),
                    in_=wv_rows[u, :, heads, :],
                )
            wv_sb.append(rows)

        def load_cw(half):
            rows = keep.tile([P, PACK, C_IN], BF16, tag="cw_rows%d" % half)
            nc.sync.dma_start(out=rows[:], in_=cw_rows[:, PACK * half : PACK * half + PACK, :])
            cw_sb.append(rows)

        def load_k(h):
            rows = keep.tile([P, 2, 4, DH], BF16, tag="k_rows%d" % h)
            nc.sync.dma_start(out=rows[:].rearrange("p s f d -> p s (f d)"), in_=k_rows[h, :, :, :])
            k_sb.append(rows)

        def load_q(head_half, tile_half):
            heads = slice(HALF_HEADS * head_half, HALF_HEADS * head_half + HALF_HEADS)
            columns = slice(PACK * DH * tile_half, PACK * DH * (tile_half + 1))
            rows = keep.tile([P, HALF_HEADS, PACK, DH], BF16, tag="q_rows%d%d" % (head_half, tile_half))
            nc.sync.dma_start(out=rows[:].rearrange("p h o d -> p h (o d)"), in_=q_rows[:, heads, columns])
            q_sb[head_half, tile_half] = rows

        load_x(0)
        load_x(1)
        load_x(2)
        load_x(3)
        load_wv(0)
        load_k(0)
        load_k(1)
        load_wv(1)
        load_k(2)
        load_k(3)
        load_k(4)
        load_k(5)
        load_k(6)
        load_k(7)
        load_cw(0)
        load_cw(1)
        nc.sync.dma_start(out=conv_b_sb[:], in_=conv_b.rearrange("(p j) -> p j", p=P))
        nc.sync.dma_start(out=conv_b_all[:], in_=conv_b.partition_broadcast(P))
        for tile_half in range(2):
            for head_half in range(2):
                load_q(head_half, tile_half)
        nc.sync.dma_start(out=ln_w_all[:], in_=ln_w.partition_broadcast(P))
        nc.sync.dma_start(out=ln_b_all[:], in_=ln_b.partition_broadcast(P))

        x_codes = keep.tile([P, NODES], U32, align_bytes=64)
        x_scales = keep.tile([P, NODES], U8, align_bytes=64)
        wv_codes = keep.tile([P, HEADS * DH], U32, align_bytes=64)
        wv_scales = keep.tile([P, HEADS * DH], U8, align_bytes=64)
        cw_codes = keep.tile([P, C_OUT], U32, align_bytes=64)
        cw_scales = keep.tile([P, C_OUT], U8, align_bytes=64)
        v_codes = keep.tile([P, HEADS, PASSES, DH], U32, align_bytes=64)
        v_scales = keep.tile([P, HEADS, PASSES, DH], U8, align_bytes=64)
        kT = keep.tile([P, HEADS, NODES], BF16)
        y_rows = {}
        y_sums = {}

        def leave_psum(engine, out, in_):
            if engine == "vector":
                nc.vector.tensor_copy(out=out, in_=in_)
            else:
                nc.scalar.copy(out=out, in_=in_)

        grouped_rows = {}

        def group_channels_last(number, name, pair_rows, half, pair):
            words = pair_rows.bitcast(F32)
            if pair == 0:
                grouped = stage.tile([P, PACK, P, PACK], BF16, tag="grouped", bufs=4, align_bytes=64)
                grouped_rows[name, half] = grouped
            grouped_words = grouped_rows[name, half][:].bitcast(F32)
            flipped = bank(number, [P, 2, 2, P], F32)
            for n in range(2):
                for u in range(2):
                    nc.tensor.transpose(flipped[:, n, u, :], words[:, n, P * u : P * u + P], ident_f32[:])
            target = grouped_words[:, 2 * pair : 2 * pair + 2, :, :]
            return lambda engine: leave_psum(engine, target, flipped[:].rearrange("p n u r -> p n r u"))

        def quantise_channels_last(name, codes, scales, half):
            cols = slice(BANK * half, BANK * half + BANK)
            nc.vector.quantize_mx(
                out=codes[:, cols].bitcast(FP8X4),
                scales=scales[:, cols],
                in_=grouped_rows[name, half][:].rearrange("p j r t -> p (j r t)"),
            )

        wv_grouped = {}

        def group_wv(half):
            grouped = stage.tile([P, HALF_HEADS, DH, PACK], BF16, tag="wv_grouped", align_bytes=64)
            wv_grouped[half] = grouped
            nc.vector.tensor_copy(out=grouped[:], in_=wv_sb[half][:].rearrange("p h t d -> p h d t"))

        def quantise_wv(half):
            cols = slice(BANK * half, BANK * half + BANK)
            nc.vector.quantize_mx(
                out=wv_codes[:, cols].bitcast(FP8X4),
                scales=wv_scales[:, cols],
                in_=wv_grouped[half][:].rearrange("p h d t -> p (h d t)"),
            )

        v_grouped = {}

        def values(number, h, g):
            if g == 0:
                grouped = stage.tile([P, PASSES, DH, PACK], BF16, tag="v_grouped", bufs=4, align_bytes=64)
                v_grouped[h] = grouped
            v_bank = bank(number, [P, PACK, DH], F32)
            for t in range(PACK):
                u, e = divmod(t, 2)
                first = P * (4 * e + 2 * g + u)
                nodes = slice(first, first + P)
                nc.tensor.matmul_mx(
                    out=v_bank[:, t, :],
                    lhsT=x_codes[:, nodes].bitcast(FP8X4),
                    lhsT_scale=x_scales[:, nodes],
                    rhs=wv_codes[:, DH * h : DH * h + DH].bitcast(FP8X4),
                    rhs_scale=wv_scales[:, DH * h : DH * h + DH],
                    start=True,
                    stop=True,
                )
            target = v_grouped[h][:, g, :, :]
            return lambda engine: leave_psum(engine, target, v_bank[:].rearrange("p t d -> p d t"))

        def quantise_values(h):
            nc.vector.quantize_mx(
                out=v_codes[:, h, :, :].rearrange("p g d -> p (g d)").bitcast(FP8X4),
                scales=v_scales[:, h, :, :].rearrange("p g d -> p (g d)"),
                in_=v_grouped[h][:].rearrange("p g d t -> p (g d t)"),
            )

        proj_banks = {}

        def projection(number, tile_no, half):
            nodes = slice(P * tile_no, P * tile_no + P)
            cols = slice(BANK * half, BANK * half + BANK)
            proj_bank = bank(number, [P, BANK], F32)
            nc.tensor.matmul_mx(
                out=proj_bank[:],
                lhsT=x_codes[:, nodes].bitcast(FP8X4),
                lhsT_scale=x_scales[:, nodes],
                rhs=cw_codes[:, cols].bitcast(FP8X4),
                rhs_scale=cw_scales[:, cols],
                start=True,
                stop=True,
            )
            proj_banks[tile_no, half] = proj_bank

        def transpose_k(number, h):
            flipped = bank(number, [P, PASSES, 2, 2, P], BF16)
            for g in range(PASSES):
                for u in range(2):
                    for s in range(2):
                        nc.tensor.transpose(flipped[:, g, u, s, :], k_sb[h][:, s, 2 * g + u, :], ident_bf[:])
            return lambda engine: leave_psum(engine, kT[:, h, :], flipped[:].rearrange("d g u s p -> d (g u s p)"))

        qT = {}
        s_banks = {}
        s_rows = {}
        shift = {}
        row_sums = {}
        e_rows = {}
        e_flipped = {}
        e_grouped = {}
        e_packed = {}
        o_banks = {}

        def transpose_q(number, tile_no, half):
            flipped = bank(number, [P, HALF_HEADS, P], BF16)
            for n in range(HALF_HEADS):
                nc.tensor.transpose(flipped[:, n, :], q_sb[half, tile_no // PACK][:, n, tile_no % PACK, :], ident_bf[:])
            if half == 0:
                q_cols = work.tile([P, HEADS, P], BF16, tag="qT", bufs=2)
                qT[tile_no] = q_cols
            heads = slice(HALF_HEADS * half, HALF_HEADS * half + HALF_HEADS)
            return lambda engine: leave_psum(engine, qT[tile_no][:, heads, :], flipped[:])

        def scores(unit, g):
            tile_no, h = divmod(unit, HEADS)
            s_bank = bank(2 * g + unit % 2, [P, BANK], F32)
            s_banks[unit, g] = s_bank
            nc.tensor.matmul(
                out=s_bank[:],
                lhsT=qT[tile_no][:, h, :],
                rhs=kT[:, h, BANK * g : BANK * g + BANK],
                start=True,
                stop=True,
            )

        def scale_and_min(unit, g):
            if g == 0:
                scaled = work.tile([P, NODES], F32, tag="scaled", bufs=4)
                s_rows[unit] = scaled
            minimum = small.tile([P, 1], F32, tag="minimum", bufs=8)
            nc.vector.tensor_scalar(
                out=s_rows[unit][:, BANK * g : BANK * g + BANK],
                in0=s_banks[unit, g][:],
                scalar1=-SCALE,
                scalar2=None if g == 0 else shift[unit][:, 0:1],
                op0=ALU.mult,
                op1=ALU.min,
                accum_out=minimum[:, 0:1],
            )
            shift[unit] = minimum

        def exponentials(unit):
            tile_no, h = divmod(unit, HEADS)
            if h == 0:
                sums = small.tile([P, HEADS], F32, tag="row_sums", bufs=3)
                row_sums[tile_no] = sums
            e_sb = work.tile([P, NODES], BF16, tag="e_sb", bufs=4)
            nc.scalar.activation(
                out=e_sb[:],
                in_=s_rows[unit][:],
                func=ACT.Exp,
                bias=shift[unit][:, 0:1],
                scale=-1.0,
                accum_out=row_sums[tile_no][:, h : h + 1],
            )
            e_rows[unit] = e_sb

        def flip(unit):
            e_words = e_rows[unit][:].bitcast(F32)
            flipped = bank(4 + unit % 2, [P, PASSES, 2, P], F32)
            for g in range(PASSES):
                for u in range(2):
                    first = P * (2 * g + u)
                    nc.tensor.transpose(flipped[:, g, u, :], e_words[:, first : first + P], ident_f32[:])
            e_flipped[unit] = flipped

        def regroup(engine, unit):
            group, place = divmod(unit, HALF_HEADS)
            if place == 0:
                grouped = work.tile([P, HALF_HEADS, PASSES, P, PACK], BF16, tag="e_grouped", bufs=2, align_bytes=64)
                e_grouped[group] = grouped
            leave_psum(
                engine,
                out=e_grouped[group][:].bitcast(F32)[:, place, :, :, :],
                in_=e_flipped[unit][:].rearrange("p g u r -> p g r u"),
            )

        def quantise(group, first, count):
            if first == 0:
                e_codes = work.tile([P, HALF_HEADS, PASSES, P], U32, tag="e_codes", bufs=2, align_bytes=64)
                e_scales = work.tile([P, HALF_HEADS, PASSES, P], U8, tag="e_scales", bufs=2, align_bytes=64)
                e_packed[group] = (e_codes, e_scales)
            e_codes, e_scales = e_packed[group]
            places = slice(first, first + count)
            nc.vector.quantize_mx(
                out=e_codes[:, places, :, :].rearrange("p n g r -> p (n g r)").bitcast(FP8X4),
                scales=e_scales[:, places, :, :].rearrange("p n g r -> p (n g r)"),
                in_=e_grouped[group][:, places, :, :, :].rearrange("p n g r t -> p (n g r t)"),
            )

        def attend(group, first, count):
            if first == 0:
                o_bank = bank(6, [P, HALF_HEADS, DH], F32)
                o_banks[group] = o_bank
            o_bank = o_banks[group]
            e_codes, e_scales = e_packed[group]
            for place in range(first, first + count):
                h = (HALF_HEADS * group + place) % HEADS
                for g in range(PASSES):
                    nc.tensor.matmul_mx(
                        out=o_bank[:, place, :],
                        lhsT=e_codes[:, place, g, :].bitcast(FP8X4),
                        lhsT_scale=e_scales[:, place, g, :],
                        rhs=v_codes[:, h, g, :].bitcast(FP8X4),
                        rhs_scale=v_scales[:, h, g, :],
                        start=(g == 0),
                        stop=(g == PASSES - 1),
                    )

        inverse_sums = {}
        attended = {}
        minus_mean = {}
        square_sums = {}
        rstd = {}
        centred = {}
        out_rows = out.rearrange("b (p o) c -> (b o) p c", o=TILES)

        def half_cols(half):
            return slice(BANK * half, BANK * half + BANK)

        half_bias_mean = keep.tile([P, 1], F32)
        scaled_bias = keep.tile([P, C_OUT // P], F32)

        def bias_mean(number):
            added = bank(number, [P, C_OUT // P], F32)
            nc.tensor.matmul(out=added[:], lhsT=ones[:], rhs=conv_b_sb[:], start=True, stop=True)
            return lambda engine: nc.scalar.activation(
                out=scaled_bias[:],
                in_=added[:],
                func=ACT.Copy,
                scale=-0.5 / C_OUT,
                accum_out=half_bias_mean[:, 0:1],
            )

        def invert_row_sums(group):
            tile_no, half = divmod(group, HALVES)
            heads = slice(HALF_HEADS * half, HALF_HEADS * half + HALF_HEADS)
            inverse = small.tile([P, HALF_HEADS], F32, tag="inverse")
            nc.vector.reciprocal(out=inverse[:], in_=row_sums[tile_no][:, heads])
            inverse_sums[group] = inverse

        def relu_and_divide(engine, group, first, count):
            if first == 0:
                relu_o = work.tile([P, HALF_HEADS, DH], F32, tag="attended")
                attended[group] = relu_o
            if engine == "vector":
                heads = slice(first, first + count)
                inverse = inverse_sums[group][:, heads].unsqueeze(2).to_broadcast([P, count, DH])
                nc.vector.scalar_tensor_tensor(
                    out=attended[group][:, heads, :],
                    in0=o_banks[group][:, heads, :],
                    scalar=0.0,
                    in1=inverse,
                    op0=ALU.max,
                    op1=ALU.mult,
                )
            else:
                for n in range(first, first + count):
                    nc.scalar.activation(
                        out=attended[group][:, n, :],
                        in_=o_banks[group][:, n, :],
                        func=ACT.Relu,
                        scale=inverse_sums[group][:, n : n + 1],
                    )

        def open_rows(tile_no):
            rows = work.tile([P, C_OUT], F32, tag="y", bufs=4)
            y_rows[tile_no] = rows
            sums = small.tile([P, HALVES + tile_no // (TILES - 1)], F32, tag="y_sums")
            y_sums[tile_no] = sums

        def add_streams(group, first, count, other, column):
            tile_no, half = divmod(group, HALVES)
            start = BANK * half + DH * first
            nc.vector.scalar_tensor_tensor(
                out=y_rows[tile_no][:, start : start + DH * count],
                in0=other,
                scalar=0.0,
                in1=attended[group][:, first : first + count, :].rearrange("p h d -> p (h d)"),
                op0=ALU.add,
                op1=ALU.add,
                accum_out=y_sums[tile_no][:, column : column + 1],
            )

        def add_to_early(group, first, count, column):
            tile_no, half = divmod(group, HALVES)
            start = BANK * half + DH * first
            add_streams(group, first, count, y_rows[tile_no][:, start : start + DH * count], column)

        def add_bias(engine, group, source):
            tile_no, half = divmod(group, HALVES)
            cols = half_cols(half)
            engine.tensor_tensor(out=y_rows[tile_no][:, cols], in0=source, in1=conv_b_all[:, cols], op=ALU.add)

        def mean(tile_no, bias):
            scaled_sums = small.tile([P, HALVES + tile_no // (TILES - 1)], F32, tag="scaled_sums")
            negative = small.tile([P, 1], F32, tag="minus_mean")
            nc.scalar.activation(
                out=scaled_sums[:],
                in_=y_sums[tile_no][:],
                func=ACT.Identity,
                bias=bias,
                scale=-1.0 / C_OUT,
                accum_out=negative[:, 0:1],
            )
            minus_mean[tile_no] = negative

        def squares(tile_no):
            squared = work.tile([P, C_OUT], BF16, tag="squared", bufs=2)
            square_sum = small.tile([P, 1], F32, tag="square_sum")
            nc.scalar.activation(
                out=squared[:],
                in_=y_rows[tile_no][:],
                func=ACT.Square,
                bias=minus_mean[tile_no][:, 0:1],
                scale=1.0,
                accum_out=square_sum[:, 0:1],
            )
            square_sums[tile_no] = square_sum

        def deviation(tile_no):
            var_eps = small.tile([P, 1], F32, tag="var_eps")
            nc.gpsimd.tensor_scalar(
                out=var_eps[:],
                in0=square_sums[tile_no][:],
                scalar1=1.0 / C_OUT,
                scalar2=LN_EPS,
                op0=ALU.mult,
                op1=ALU.add,
            )
            inverse_std = small.tile([P, 1], F32, tag="rstd")
            nc.gpsimd.tensor_tensor(out=inverse_std[:], in0=var_eps[:], in1=minus_half[:], op=ALU.pow)
            rstd[tile_no] = inverse_std

        def normalise(tile_no):
            nc.gpsimd.tensor_scalar(
                out=y_rows[tile_no][:],
                in0=y_rows[tile_no][:],
                scalar1=minus_mean[tile_no][:, 0:1],
                scalar2=rstd[tile_no][:, 0:1],
                op0=ALU.add,
                op1=ALU.mult,
            )

        def affine(tile_no, half, vector, op):
            cols = half_cols(half)
            nc.gpsimd.tensor_tensor(
                out=y_rows[tile_no][:, cols], in0=y_rows[tile_no][:, cols], in1=vector[:, cols], op=op
            )

        def store(tile_no, cols):
            nc.sync.dma_start(out=out_rows[tile_no, :, cols], in_=y_rows[tile_no][:, cols])

        def centre(tile_no, half):
            cols = half_cols(half)
            scaled = work.tile([P, BANK], F32, tag="attended")
            centred[tile_no, half] = scaled
            nc.vector.scalar_tensor_tensor(
                out=scaled[:],
                in0=y_rows[tile_no][:, cols],
                scalar=minus_mean[tile_no][:, 0:1],
                in1=ln_w_all[:, cols],
                op0=ALU.add,
                op1=ALU.mult,
            )

        def finish(tile_no, half, part, parts):
            width = BANK // parts
            within = slice(width * part, width * part + width)
            cols = slice(BANK * half + width * part, BANK * half + width * part + width)
            nc.vector.scalar_tensor_tensor(
                out=y_rows[tile_no][:, cols],
                in0=centred[tile_no, half][:, within],
                scalar=rstd[tile_no][:, 0:1],
                in1=ln_b_all[:, cols],
                op0=ALU.mult,
                op1=ALU.add,
            )
            store(tile_no, cols)

        def fill_k(h):
            return lambda number: transpose_k(number, h), None

        def fill_x(half, pair):
            done = (lambda: quantise_channels_last("x", x_codes, x_scales, half)) if pair else None
            return lambda number: group_channels_last(number, "x", x_sb[2 * half + pair][:], half, pair), done

        def fill_cw(half, pair):
            done = (lambda: quantise_channels_last("cw", cw_codes, cw_scales, half)) if pair else None
            rows = slice(2 * pair, 2 * pair + 2)
            return lambda number: group_channels_last(number, "cw", cw_sb[half][:, rows, :], half, pair), done

        def fill_v(h, g):
            done = (lambda: quantise_values(h)) if g else None
            return lambda number: values(number, h, g), done

        def fill_q(tile_no, half):
            return lambda number: transpose_q(number, tile_no, half), None

        def fill_vs(h):
            return [fill_v(h, 0), fill_v(h, 1)]

        halves = [(half, pair) for half in range(2) for pair in range(2)]
        prep = [fill_x(0, 0), fill_x(0, 1), fill_x(1, 0), fill_x(1, 1), fill_k(0), fill_k(1), fill_v(0, 0), fill_v(0, 1), fill_v(1, 0), fill_v(1, 1), fill_v(2, 0), fill_v(2, 1), fill_v(3, 0), fill_v(3, 1), fill_k(2), fill_k(3), fill_k(4), fill_k(5), fill_v(4, 0), fill_v(4, 1), fill_v(5, 0), fill_v(5, 1), fill_v(6, 0), fill_v(6, 1), fill_v(7, 0), fill_v(7, 1), fill_k(6), fill_k(7), fill_cw(0, 0), fill_cw(0, 1), fill_cw(1, 0), fill_cw(1, 1), fill_q(0, 0), fill_q(0, 1)]

        DRAIN = ("scalar", "vector", "scalar")
        DELAY = 2
        filled = []

        def prepare(n):
            if 0 <= n - DELAY - 1 < len(prep) and prep[n - DELAY - 1][1]:
                prep[n - DELAY - 1][1]()
            if 0 <= n < len(prep):
                filled.append(prep[n][0](n % 8))
            if 0 <= n - DELAY < len(prep):
                filled[n - DELAY](DRAIN[(n - DELAY) % len(DRAIN)])

        FLIP = 3
        LAG = FLIP + 2
        for n in range(len(prep) + DELAY + 1):
            prepare(n)
            if n == 4:
                group_wv(0)
            if n == 5:
                quantise_wv(0)
            if n == 7:
                group_wv(1)
            if n == 8:
                quantise_wv(1)
        bias_mean(7)("scalar")
        late_copies = []
        late_adds = []
        scores(0, 0)
        scores(1, 0)
        scores(0, 1)
        def close_group(group):
            relu_and_divide("scalar" if group % HALVES == 0 else "vector", group, 0, HALF_HEADS)
            projection(7, *divmod(group, HALVES))

        def finish_group(group):
            tile_no, half = divmod(group, HALVES)
            if half == 0:
                open_rows(tile_no)
            add_streams(group, 0, HALF_HEADS, proj_banks[tile_no, half][:], half)
            add_bias(nc.gpsimd, group, y_rows[tile_no][:, half_cols(half)])
            if half == 0 and tile_no >= 1:
                deviation(tile_no - 1)
                normalise(tile_no - 1)
                affine(tile_no - 1, 0, ln_w_all, ALU.mult)
            if half == 1 and 1 <= tile_no < TILES - 2 or half == 0 and tile_no == TILES - 2:
                affine(tile_no - 1, 1, ln_w_all, ALU.mult)
                for n in range(HALVES):
                    affine(tile_no - 1, n, ln_b_all, ALU.add)
                    store(tile_no - 1, half_cols(n))

        for i in range(UNITS + LAG):
            group, step = divmod(i - LAG - HALF_HEADS + 1, HALF_HEADS)
            group_runs = 0 <= group < GROUPS - 1
            closing_tile, closing_half = divmod(group, HALVES)
            place = i - LAG - HALF_HEADS * (GROUPS - 1)

            if i < UNITS:
                scale_and_min(i, 0)
            if group_runs and step == 0:
                quantise(group, 0, 2)
            if i + 2 < UNITS:
                scores(i + 2, 0)
            if group_runs and step == 1:
                attend(group, 2, 2)
            if 0 <= i - 1 < UNITS:
                scale_and_min(i - 1, 1)
            if i + 1 < UNITS:
                scores(i + 1, 1)
            if 0 <= i - FLIP < UNITS:
                flip(i - FLIP)
            for early in late_adds:
                add_bias(nc.vector, early, proj_banks[divmod(early, HALVES)][:])
            late_adds.clear()
            if 0 <= i - 2 < UNITS:
                exponentials(i - 2)
            if 0 <= i - FLIP - 1 < UNITS:
                regroup("scalar", i - FLIP - 1)

            for copy in late_copies:
                copy("scalar")
            late_copies.clear()
            q_tile, q_step = divmod(i + 12 - LAG, HEADS)
            if 1 <= q_tile < TILES and q_step in (0, 4):
                late_copies.append(transpose_q(7, q_tile, q_step // 4))

            if group_runs and step == 0:
                quantise(group, 2, 2)
                if group >= 1:
                    finish_group(group - 1)
                attend(group, 0, 2)
            if group_runs and step == 3 and group < GROUPS - 2:
                close_group(group)
            if 1 <= group < GROUPS - 1 and group % HALVES == 0:
                if step == 2:
                    mean(group // HALVES - 1, half_bias_mean[:, 0:1])
                if step == 3:
                    squares(group // HALVES - 1)
            if group_runs and step == 1:
                invert_row_sums(group)
            if place == 2:
                invert_row_sums(GROUPS - 1)

            if group in (GROUPS - 4, GROUPS - 3) and step == 1:
                early = group + 2
                if early % HALVES == 0:
                    open_rows(early // HALVES)
                projection(7, *divmod(early, HALVES))
                late_adds.append(early)
            if place == 1:
                relu_and_divide("vector", GROUPS - 2, 0, HALF_HEADS)
                quantise(GROUPS - 1, 0, 2)
                attend(GROUPS - 1, 0, 2)
            if place == 2:
                add_to_early(GROUPS - 2, 0, HALF_HEADS, 0)
                quantise(GROUPS - 1, place, 1)
                attend(GROUPS - 1, place, 1)
                deviation(TILES - 2)
            if place == 3:
                relu_and_divide("vector", GROUPS - 1, 0, place)
                quantise(GROUPS - 1, place, 1)
                attend(GROUPS - 1, place, 1)
                add_to_early(GROUPS - 1, 0, place, 1)
                for half in range(HALVES):
                    centre(TILES - 2, half)

        relu_and_divide("vector", GROUPS - 1, HALF_HEADS - 1, 1)
        add_to_early(GROUPS - 1, HALF_HEADS - 1, 1, HALVES)
        mean(TILES - 1, 0.0)
        for half in range(HALVES):
            finish(TILES - 2, half, 0, 1)
        squares(TILES - 1)
        for half in range(HALVES):
            centre(TILES - 1, half)
        deviation(TILES - 1)
        for half in range(HALVES):
            for part in range(2):
                finish(TILES - 1, half, part, 2)
